import numpy as np
import ml_dtypes


def mxq(x, axis, fmt="e4m3"):
    dtype, down = {"e4m3": (ml_dtypes.float8_e4m3fn, 7), "e5m2": (ml_dtypes.float8_e5m2, 14)}[fmt]
    v = np.moveaxis(np.asarray(x, np.float32).astype(ml_dtypes.bfloat16).astype(np.float64), axis, -1)
    blocks = v.reshape(v.shape[:-1] + (-1, 32))
    amax = np.abs(blocks).max(-1, keepdims=True)
    byte = np.maximum(np.where(amax > 0, np.frexp(amax)[1] - 1 + 127, 0) - down, 1)
    scale = np.exp2(byte - 127.0)
    codes = (blocks / scale).astype(np.float32).astype(dtype).astype(np.float64)
    return np.moveaxis((codes * scale).reshape(v.shape), -1, axis)


WIDE = False


def mx_kscale(k):
    if not WIDE:
        return np.ones(k)
    levels = np.array([10, -10, 5, -5, 0])
    a = np.random.permutation(np.resize(levels, k // 512 * 4)).reshape(k // 512, 4)
    idx = np.arange(k)
    return np.exp2(a[idx // 512, idx % 128 // 32])


BF16 = ml_dtypes.bfloat16


def bf(x):
    return np.asarray(x, np.float32).astype(BF16)


def f64(x):
    return np.asarray(x).astype(np.float64)


B, F_IN, HID, E, G, H = 1024, 64, 512, 32, 12, 8
BN_EPS = 1e-5
L1_EPS = 1e-6 ** 2
SELU_ALPHA = 1.6732632423543772
SELU_SCALE = 1.0507009873554805


def selu(v):
    return SELU_SCALE * np.where(v > 0.0, v, SELU_ALPHA * (np.exp(np.minimum(v, 0.0)) - 1.0))


def setup_inputs():
    s = mx_kscale(HID)
    t = s / s.min()
    col_std = 0.5 + np.random.random(HID)
    col_mean = 0.5 * np.random.standard_normal(HID)
    return {"h2": bf(np.random.standard_normal((B, HID)) * col_std + col_mean),
            "gamma": bf((1.0 + 0.1 * np.random.standard_normal(HID)) * t),
            "beta": bf(0.1 * np.random.standard_normal(HID) * t),
            "Wh": bf(np.random.standard_normal((H, G, HID, E)) / np.sqrt(HID) / t[:, None]),
            "bh": bf(0.3 * np.random.standard_normal((H, G, E)))}


def reference(h2, gamma, beta, Wh, bh):
    h2 = f64(h2)
    mu = h2.mean(axis=0)
    var = h2.var(axis=0)
    e = selu((h2 - mu) / np.sqrt(var + BN_EPS) * f64(gamma) + f64(beta))
    p = (mxq(e, 1, "e4m3") @ mxq(f64(Wh), 2, "e4m3")).transpose(2, 0, 1, 3)
    d = selu(p + f64(bh))
    a = np.abs(d)
    l1 = np.maximum(a.sum(axis=-1, keepdims=True), L1_EPS)
    return np.sign(d) * (a / l1)

@@ -1,0 +1,351 @@
+import math
+from contextlib import ExitStack
+
+import concourse.mybir as mybir
+from concourse.masks import make_identity
+
+F32 = mybir.dt.float32
+BF16 = mybir.dt.bfloat16
+U32 = mybir.dt.uint32
+U8 = mybir.dt.uint8
+FP8X4 = mybir.dt.float8_e4m3fn_x4
+ALU = mybir.AluOpType
+ACT = mybir.ActivationFunctionType
+
+P = 128
+PACK = 4
+BATCH = 1024
+HID = P * PACK
+HEADS = 96
+E = 32
+COLS = HEADS * E
+BATCH_TILES = BATCH // P
+HALF = 512
+TILES_PER_HALF = HALF // P
+COL_TILES = COLS // P
+HEADS_PER_TILE = P // E
+CHUNK_TILES = 4
+CHUNKS = COL_TILES // CHUNK_TILES
+CHUNK_COLS = CHUNK_TILES * P
+CHUNK_HEADS = CHUNK_COLS // E
+
+BN_EPS = 1e-5
+ALPHA = 1.6732632423543772
+LAMBDA = 1.0507009873554805
+L1_FLOOR = 1e-12 / LAMBDA
+SLOTS = 4
+
+FLOPS = 2 * BATCH * HID * COLS
+
+
+def tile_basicemotionpredictions_pa_kernel(tc, h2, gamma, beta, Wh, bh, out):
+    nc = tc.nc
+    with ExitStack() as ctx:
+        keep = ctx.enter_context(tc.tile_pool(name="keep", bufs=1))
+        w_in = ctx.enter_context(tc.tile_pool(name="w_in", bufs=CHUNKS))
+        w_stage = ctx.enter_context(tc.tile_pool(name="w_stage", bufs=2))
+        e_stage = ctx.enter_context(tc.tile_pool(name="e_stage", bufs=3))
+        work = ctx.enter_context(tc.tile_pool(name="work", bufs=4))
+        small = ctx.enter_context(tc.tile_pool(name="small", bufs=4))
+        out_stage = ctx.enter_context(tc.tile_pool(name="out_stage", bufs=3))
+        psum = ctx.enter_context(tc.psum_pool(name="psum", bufs=8))
+
+        h2_rows = h2.rearrange("(p t) f -> p t f", t=BATCH_TILES)
+        h2_sb = keep.tile([P, BATCH_TILES, HID], BF16)
+        for pair in range(BATCH_TILES // 2):
+            two = slice(2 * pair, 2 * pair + 2)
+            nc.sync.dma_start(out=h2_sb[:, two, :], in_=h2_rows[:, two, :])
+
+        gamma_bf = keep.tile([P, PACK], BF16)
+        nc.scalar.dma_start(out=gamma_bf[:], in_=gamma.rearrange("(p j) -> p j", j=PACK))
+        beta_bf = keep.tile([P, PACK], BF16)
+        nc.scalar.dma_start(out=beta_bf[:], in_=beta.rearrange("(p j) -> p j", j=PACK))
+        bias_rows = keep.tile([P, P], BF16)
+        nc.vector.memset(bias_rows[:], 0.0)
+        nc.scalar.dma_start(
+            out=bias_rows[0:COL_TILES, :],
+            in_=bh.rearrange("h (a b) e -> (h a) (b e)", b=HEADS_PER_TILE),
+        )
+
+        w_rows = Wh.rearrange("h g (p j) e -> p (h g) (j e)", j=PACK)
+        w_raw = []
+        for k in range(CHUNKS):
+            raw = w_in.tile([P, CHUNK_HEADS, PACK * E], BF16, name="w_raw%d" % k, tag="w_raw")
+            nc.sync.dma_start(
+                out=raw[:], in_=w_rows[:, k * CHUNK_HEADS : (k + 1) * CHUNK_HEADS, :]
+            )
+            w_raw.append(raw)
+
+        ident = keep.tile([P, P], F32)
+        make_identity(nc, ident[:])
+        one_col = keep.tile([P, 1], F32)
+        nc.vector.memset(one_col[:], 1.0)
+        neg_half = keep.tile([P, PACK], F32)
+        nc.vector.memset(neg_half[:], -0.5)
+
+        xt = [
+            [
+                psum.tile([P, TILES_PER_HALF, P], F32, name="xt%d%d" % (u, half), tag="bank")
+                for half in range(2)
+            ]
+            for u in range(2)
+        ]
+        for t in range(BATCH_TILES):
+            words = h2_sb[:, t, :].bitcast(F32).rearrange("p (q u) -> p u q", u=2)
+            for u in range(2):
+                nc.tensor.transpose(
+                    xt[u][t // TILES_PER_HALF][:, t % TILES_PER_HALF, :], words[:, u, :], ident[:]
+                )
+
+        stats = keep.tile([P, 2, 4, 6], F32)
+        for half in range(2):
+            for u in range(2):
+                pairs = xt[u][half][:].bitcast(BF16)
+                for s in range(2):
+                    nc.vector.bn_stats(
+                        out=stats[:, u, 2 * half + s, :],
+                        in_=pairs[:, 2 * s : 2 * s + 2, :].rearrange("p t w -> p (t w)"),
+                    )
+        mean_var = keep.tile([P, PACK, 2], F32)
+        for u in range(2):
+            for odd in range(2):
+                nc.vector.bn_aggr(
+                    out=mean_var[:, 2 * u + odd, :], in_=stats[:, u, :, 3 * odd : 3 * odd + 3]
+                )
+
+        gain2 = keep.tile([P, 2, PACK], F32)
+        nc.vector.tensor_scalar_mul(gain2[:, 0, :], gamma_bf[:], -1.0)
+        nc.vector.tensor_scalar_mul(gain2[:, 1, :], gamma_bf[:], LAMBDA)
+        shift2 = keep.tile([P, 2, PACK], F32)
+        nc.vector.tensor_scalar_mul(shift2[:, 0, :], beta_bf[:], -1.0)
+        nc.vector.tensor_scalar_mul(shift2[:, 1, :], beta_bf[:], LAMBDA)
+        log_col = keep.tile([P, 1], F32)
+        nc.vector.tensor_scalar_mul(log_col[:], one_col[:], math.log(LAMBDA * ALPHA))
+
+        var_eps = keep.tile([P, PACK], F32)
+        nc.vector.tensor_scalar_add(var_eps[:], mean_var[:, :, 1], BN_EPS)
+        rstd = keep.tile([P, PACK], F32)
+        nc.gpsimd.tensor_tensor(out=rstd[:], in0=var_eps[:], in1=neg_half[:], op=ALU.pow)
+        scale2 = keep.tile([P, 2, PACK], F32)
+        nc.vector.tensor_tensor(
+            out=scale2[:],
+            in0=gain2[:],
+            in1=rstd[:].unsqueeze(1).to_broadcast([P, 2, PACK]),
+            op=ALU.mult,
+        )
+        mean_scaled = keep.tile([P, 2, PACK], F32)
+        nc.vector.tensor_tensor(
+            out=mean_scaled[:],
+            in0=scale2[:],
+            in1=mean_var[:, :, 0].unsqueeze(1).to_broadcast([P, 2, PACK]),
+            op=ALU.mult,
+        )
+        offset2 = keep.tile([P, 2, PACK], F32)
+        nc.vector.tensor_tensor(out=offset2[:], in0=shift2[:], in1=mean_scaled[:], op=ALU.subtract)
+
+        bias_rows_f = keep.tile([P, P], F32)
+        nc.vector.tensor_copy(out=bias_rows_f[:], in_=bias_rows[:])
+        bias_ps = psum.tile([P, P], F32, tag="bank")
+        nc.tensor.transpose(bias_ps[:], bias_rows_f[:], ident[:])
+        bias_plus = keep.tile([P, COL_TILES], F32)
+        nc.vector.tensor_copy(out=bias_plus[:], in_=bias_ps[:, 0:COL_TILES])
+        bias_minus = keep.tile([P, COL_TILES], F32)
+        nc.vector.tensor_scalar_mul(bias_minus[:], bias_ps[:, 0:COL_TILES], -1.0)
+        bias_less_alpha = keep.tile([P, COL_TILES], F32)
+        nc.vector.tensor_scalar_add(bias_less_alpha[:], bias_ps[:, 0:COL_TILES], -ALPHA)
+
+        w_codes = keep.tile([P, COLS], U32, align_bytes=64)
+        w_scales = keep.tile([P, COLS], U8, align_bytes=64)
+
+        def quantise_w_chunk(k):
+            cols = slice(k * CHUNK_COLS, (k + 1) * CHUNK_COLS)
+            grouped = w_stage.tile([P, CHUNK_HEADS, E, PACK], BF16, align_bytes=64, tag="w_grouped")
+            nc.vector.tensor_copy(
+                out=grouped[:], in_=w_raw[k][:].rearrange("p h (j e) -> p h e j", j=PACK)
+            )
+            nc.vector.quantize_mx(
+                out=w_codes[:, cols].bitcast(FP8X4),
+                scales=w_scales[:, cols],
+                in_=grouped[:].rearrange("p h e j -> p (h e j)"),
+            )
+
+        e_planes = keep.tile([P, PACK, BATCH], BF16)
+        e_grouped = keep.tile([P, BATCH, PACK], BF16, align_bytes=64)
+        e_codes = keep.tile([P, BATCH], U32, align_bytes=64)
+        e_scales = keep.tile([P, BATCH], U8, align_bytes=64)
+
+        def quantise_e_half(half):
+            rows = slice(half * HALF, (half + 1) * HALF)
+            for j in range(PACK):
+                u, odd = divmod(j, 2)
+                x = xt[u][half][:].bitcast(BF16).rearrange("p t (b o) -> p (t b) o", o=2)[:, :, odd]
+                below = e_stage.tile([P, HALF], F32, tag="e_below")
+                nc.scalar.activation(
+                    out=below[:], in_=x, func=ACT.Relu,
+                    scale=scale2[:, 0, j : j + 1], bias=offset2[:, 0, j : j + 1],
+                )
+                linear = e_stage.tile([P, HALF], F32, tag="e_linear")
+                nc.scalar.activation(
+                    out=linear[:], in_=x, func=ACT.Relu,
+                    scale=scale2[:, 1, j : j + 1], bias=offset2[:, 1, j : j + 1],
+                )
+                decay = e_stage.tile([P, HALF], F32, tag="e_decay")
+                nc.scalar.activation(
+                    out=decay[:], in_=below[:], func=ACT.Exp, scale=-1.0, bias=log_col[:]
+                )
+                nc.vector.scalar_tensor_tensor(
+                    out=e_planes[:, j, rows], in0=decay[:], scalar=LAMBDA * ALPHA, in1=linear[:],
+                    op0=ALU.subtract, op1=ALU.add,
+                )
+            nc.vector.tensor_copy(
+                out=e_grouped[:, rows, :], in_=e_planes[:, :, rows].rearrange("p j b -> p b j")
+            )
+            nc.vector.quantize_mx(
+                out=e_codes[:, rows].bitcast(FP8X4),
+                scales=e_scales[:, rows],
+                in_=e_grouped[:, rows, :].rearrange("p b j -> p (b j)"),
+            )
+
+        quantise_w_chunk(0)
+        quantise_e_half(0)
+        quantise_w_chunk(1)
+        quantise_e_half(1)
+        for k in range(2, CHUNKS):
+            quantise_w_chunk(k)
+
+        out_rows = out.rearrange("(p t) h g e -> p t (h g e)", t=BATCH_TILES)
+        rounds = [(half, c) for half in range(2) for c in range(COL_TILES)]
+        groups = TILES_PER_HALF * HEADS_PER_TILE
+        sum_floor = keep.tile([P, SLOTS, groups, 2], F32)
+        nc.vector.memset(sum_floor[:], L1_FLOOR)
+        p_tiles = {}
+        belows = {}
+        decays = {}
+        d_tiles = {}
+        d_banks = {}
+        sizes = {}
+        folds = {}
+        divisors = {}
+        inverses = {}
+        results = {}
+
+        def multiply(n):
+            half, c = rounds[n]
+            rows = slice(half * HALF, (half + 1) * HALF)
+            cols = slice(c * P, (c + 1) * P)
+            p_t = psum.tile([P, HALF], F32, tag="bank")
+            nc.tensor.matmul_mx(
+                out=p_t[:],
+                lhsT=w_codes[:, cols].bitcast(FP8X4), lhsT_scale=w_scales[:, cols],
+                rhs=e_codes[:, rows].bitcast(FP8X4), rhs_scale=e_scales[:, rows],
+                start=True, stop=True,
+            )
+            p_tiles[n] = p_t
+            below = work.tile([P, HALF], F32, tag="below")
+            nc.scalar.activation(
+                out=below[:], in_=p_t[:], func=ACT.Relu, bias=bias_minus[:, c : c + 1], scale=-1.0
+            )
+            belows[n] = below
+
+        def decay(n):
+            decayed = work.tile([P, HALF], F32, tag="decayed")
+            nc.scalar.activation(out=decayed[:], in_=belows[n][:], func=ACT.Exp, scale=-1.0)
+            decays[n] = decayed
+
+        def combine(n):
+            c = rounds[n][1]
+            curved = work.tile([P, HALF], F32, tag="curved")
+            nc.gpsimd.tensor_scalar(
+                out=curved[:], in0=decays[n][:], scalar1=ALPHA,
+                scalar2=bias_less_alpha[:, c : c + 1], op0=ALU.mult, op1=ALU.add,
+            )
+            d_t = work.tile([P, HALF], F32, tag="d_t")
+            nc.vector.scalar_tensor_tensor(
+                out=d_t[:], in0=p_tiles[n][:], scalar=bias_minus[:, c : c + 1], in1=curved[:],
+                op0=ALU.max, op1=ALU.add,
+            )
+            d_tiles[n] = d_t
+
+        def turn(n):
+            d_ps = psum.tile([P, TILES_PER_HALF, P], F32, tag="bank")
+            for t in range(TILES_PER_HALF):
+                nc.tensor.transpose(d_ps[:, t, :], d_tiles[n][:, t * P : (t + 1) * P], ident[:])
+            d_banks[n] = d_ps
+
+        def magnitude(n):
+            size = work.tile([P, groups, E], F32, tag="size")
+            nc.scalar.activation(
+                out=size[:], in_=d_banks[n][:].rearrange("p t (h e) -> p (t h) e", e=E), func=ACT.Abs
+            )
+            sizes[n] = size
+
+        def fold(n):
+            folded = work.tile([P, groups, E // 2], F32, tag="folded")
+            nc.gpsimd.tensor_tensor(
+                out=folded[:], in0=sizes[n][:, :, 0 : E // 2], in1=sizes[n][:, :, E // 2 : E],
+                op=ALU.add,
+            )
+            folds[n] = folded
+
+        def total(n):
+            nc.vector.tensor_reduce(
+                out=sum_floor[:, n % SLOTS, :, 0], in_=folds[n][:],
+                axis=mybir.AxisListType.X, op=ALU.add,
+            )
+
+        def floor(n):
+            divisor = small.tile([P, groups], F32, tag="divisor")
+            nc.vector.tensor_reduce(
+                out=divisor[:], in_=sum_floor[:, n % SLOTS, :, :],
+                axis=mybir.AxisListType.X, op=ALU.max,
+            )
+            divisors[n] = divisor
+
+        def invert(n):
+            inverse = small.tile([P, groups], F32, tag="inverse")
+            nc.vector.reciprocal(out=inverse[:], in_=divisors[n][:])
+            inverses[n] = inverse
+
+        def scale_and_store(n):
+            half, c = rounds[n]
+            k, i = divmod(c, CHUNK_TILES)
+            if i == 0:
+                results[(half, k)] = out_stage.tile(
+                    [P, TILES_PER_HALF, CHUNK_COLS], F32, name="result", tag="result"
+                )
+            result = results[(half, k)]
+            nc.vector.tensor_tensor(
+                out=result[:, :, i * P : (i + 1) * P].rearrange("p t (h e) -> p t h e", e=E),
+                in0=d_banks[n][:].rearrange("p t (h e) -> p t h e", e=E),
+                in1=inverses[n][:]
+                .rearrange("p (t h) -> p t h", h=HEADS_PER_TILE)
+                .unsqueeze(3)
+                .to_broadcast([P, TILES_PER_HALF, HEADS_PER_TILE, E]),
+                op=ALU.mult,
+            )
+            if i == CHUNK_TILES - 1:
+                nc.sync.dma_start(
+                    out=out_rows[
+                        :,
+                        half * TILES_PER_HALF : (half + 1) * TILES_PER_HALF,
+                        k * CHUNK_COLS : (k + 1) * CHUNK_COLS,
+                    ],
+                    in_=result[:],
+                )
+
+        stages = (
+            (multiply, 0),
+            (turn, 2),
+            (magnitude, 3),
+            (decay, 0),
+            (total, 5),
+            (scale_and_store, 6),
+            (floor, 5),
+            (combine, 1),
+            (fold, 4),
+            (invert, 5),
+        )
+        for s in range(len(rounds) + 6):
+            for stage, lag in stages:
+                if 0 <= s - lag < len(rounds):
+                    stage(s - lag)

@@ -50,6 +50,8 @@ def tile_basicemotionpredictions_pa_kernel(tc, h2, gamma, beta, Wh, bh, out):
         out_stage = ctx.enter_context(tc.tile_pool(name="out_stage", bufs=3))
         psum = ctx.enter_context(tc.psum_pool(name="psum", bufs=8))
 
+        ctx.enter_context(tc.manual_schedule())
+
         h2_rows = h2.rearrange("(p t) f -> p t f", t=BATCH_TILES)
         h2_sb = keep.tile([P, BATCH_TILES, HID], BF16)
         for pair in range(BATCH_TILES // 2):
@@ -83,6 +85,25 @@ def tile_basicemotionpredictions_pa_kernel(tc, h2, gamma, beta, Wh, bh, out):
         neg_half = keep.tile([P, PACK], F32)
         nc.vector.memset(neg_half[:], -0.5)
 
+        w_codes = keep.tile([P, COLS], U32, align_bytes=64)
+        w_scales = keep.tile([P, COLS], U8, align_bytes=64)
+        w_grouped = {}
+
+        def regroup_w(k):
+            grouped = w_stage.tile([P, CHUNK_HEADS, E, PACK], BF16, align_bytes=64, tag="w_grouped")
+            nc.vector.tensor_copy(
+                out=grouped[:], in_=w_raw[k][:].rearrange("p h (j e) -> p h e j", j=PACK)
+            )
+            w_grouped[k] = grouped
+
+        def quantise_w(k):
+            cols = slice(k * CHUNK_COLS, (k + 1) * CHUNK_COLS)
+            nc.vector.quantize_mx(
+                out=w_codes[:, cols].bitcast(FP8X4),
+                scales=w_scales[:, cols],
+                in_=w_grouped[k][:].rearrange("p h e j -> p (h e j)"),
+            )
+
         xt = [
             [
                 psum.tile([P, TILES_PER_HALF, P], F32, name="xt%d%d" % (u, half), tag="bank")
@@ -90,15 +111,16 @@ def tile_basicemotionpredictions_pa_kernel(tc, h2, gamma, beta, Wh, bh, out):
             ]
             for u in range(2)
         ]
-        for t in range(BATCH_TILES):
-            words = h2_sb[:, t, :].bitcast(F32).rearrange("p (q u) -> p u q", u=2)
-            for u in range(2):
-                nc.tensor.transpose(
-                    xt[u][t // TILES_PER_HALF][:, t % TILES_PER_HALF, :], words[:, u, :], ident[:]
-                )
-
         stats = keep.tile([P, 2, 4, 6], F32)
+        gain2 = keep.tile([P, 2, PACK], F32)
+        shift2 = keep.tile([P, 2, PACK], F32)
+        log_col = keep.tile([P, 1], F32)
+        bias_rows_f = keep.tile([P, P], F32)
         for half in range(2):
+            for t in range(half * TILES_PER_HALF, (half + 1) * TILES_PER_HALF):
+                words = h2_sb[:, t, :].bitcast(F32).rearrange("p (q u) -> p u q", u=2)
+                for u in range(2):
+                    nc.tensor.transpose(xt[u][half][:, t % TILES_PER_HALF, :], words[:, u, :], ident[:])
             for u in range(2):
                 pairs = xt[u][half][:].bitcast(BF16)
                 for s in range(2):
@@ -106,26 +128,31 @@ def tile_basicemotionpredictions_pa_kernel(tc, h2, gamma, beta, Wh, bh, out):
                         out=stats[:, u, 2 * half + s, :],
                         in_=pairs[:, 2 * s : 2 * s + 2, :].rearrange("p t w -> p (t w)"),
                     )
+            if half == 0:
+                nc.vector.tensor_scalar_mul(gain2[:, 0, :], gamma_bf[:], -1.0)
+                nc.vector.tensor_scalar_mul(gain2[:, 1, :], gamma_bf[:], LAMBDA)
+                nc.vector.tensor_scalar_mul(shift2[:, 0, :], beta_bf[:], -1.0)
+                nc.vector.tensor_scalar_mul(shift2[:, 1, :], beta_bf[:], LAMBDA)
+                nc.vector.tensor_scalar_mul(log_col[:], one_col[:], math.log(LAMBDA * ALPHA))
+                nc.vector.tensor_copy(out=bias_rows_f[:], in_=bias_rows[:])
+        bias_ps = psum.tile([P, P], F32, tag="bank")
+        nc.tensor.transpose(bias_ps[:], bias_rows_f[:], ident[:])
+
         mean_var = keep.tile([P, PACK, 2], F32)
         for u in range(2):
             for odd in range(2):
                 nc.vector.bn_aggr(
                     out=mean_var[:, 2 * u + odd, :], in_=stats[:, u, :, 3 * odd : 3 * odd + 3]
                 )
-
-        gain2 = keep.tile([P, 2, PACK], F32)
-        nc.vector.tensor_scalar_mul(gain2[:, 0, :], gamma_bf[:], -1.0)
-        nc.vector.tensor_scalar_mul(gain2[:, 1, :], gamma_bf[:], LAMBDA)
-        shift2 = keep.tile([P, 2, PACK], F32)
-        nc.vector.tensor_scalar_mul(shift2[:, 0, :], beta_bf[:], -1.0)
-        nc.vector.tensor_scalar_mul(shift2[:, 1, :], beta_bf[:], LAMBDA)
-        log_col = keep.tile([P, 1], F32)
-        nc.vector.tensor_scalar_mul(log_col[:], one_col[:], math.log(LAMBDA * ALPHA))
-
         var_eps = keep.tile([P, PACK], F32)
         nc.vector.tensor_scalar_add(var_eps[:], mean_var[:, :, 1], BN_EPS)
         rstd = keep.tile([P, PACK], F32)
         nc.gpsimd.tensor_tensor(out=rstd[:], in0=var_eps[:], in1=neg_half[:], op=ALU.pow)
+        bias_minus = keep.tile([P, COL_TILES], F32)
+        nc.vector.tensor_scalar_mul(bias_minus[:], bias_ps[:, 0:COL_TILES], -1.0)
+        bias_less_alpha = keep.tile([P, COL_TILES], F32)
+        nc.vector.tensor_scalar_add(bias_less_alpha[:], bias_ps[:, 0:COL_TILES], -ALPHA)
+        regroup_w(0)
         scale2 = keep.tile([P, 2, PACK], F32)
         nc.vector.tensor_tensor(
             out=scale2[:],
@@ -143,75 +170,63 @@ def tile_basicemotionpredictions_pa_kernel(tc, h2, gamma, beta, Wh, bh, out):
         offset2 = keep.tile([P, 2, PACK], F32)
         nc.vector.tensor_tensor(out=offset2[:], in0=shift2[:], in1=mean_scaled[:], op=ALU.subtract)
 
-        bias_rows_f = keep.tile([P, P], F32)
-        nc.vector.tensor_copy(out=bias_rows_f[:], in_=bias_rows[:])
-        bias_ps = psum.tile([P, P], F32, tag="bank")
-        nc.tensor.transpose(bias_ps[:], bias_rows_f[:], ident[:])
-        bias_plus = keep.tile([P, COL_TILES], F32)
-        nc.vector.tensor_copy(out=bias_plus[:], in_=bias_ps[:, 0:COL_TILES])
-        bias_minus = keep.tile([P, COL_TILES], F32)
-        nc.vector.tensor_scalar_mul(bias_minus[:], bias_ps[:, 0:COL_TILES], -1.0)
-        bias_less_alpha = keep.tile([P, COL_TILES], F32)
-        nc.vector.tensor_scalar_add(bias_less_alpha[:], bias_ps[:, 0:COL_TILES], -ALPHA)
-
-        w_codes = keep.tile([P, COLS], U32, align_bytes=64)
-        w_scales = keep.tile([P, COLS], U8, align_bytes=64)
-
-        def quantise_w_chunk(k):
-            cols = slice(k * CHUNK_COLS, (k + 1) * CHUNK_COLS)
-            grouped = w_stage.tile([P, CHUNK_HEADS, E, PACK], BF16, align_bytes=64, tag="w_grouped")
-            nc.vector.tensor_copy(
-                out=grouped[:], in_=w_raw[k][:].rearrange("p h (j e) -> p h e j", j=PACK)
-            )
-            nc.vector.quantize_mx(
-                out=w_codes[:, cols].bitcast(FP8X4),
-                scales=w_scales[:, cols],
-                in_=grouped[:].rearrange("p h e j -> p (h e j)"),
-            )
-
         e_planes = keep.tile([P, PACK, BATCH], BF16)
         e_grouped = keep.tile([P, BATCH, PACK], BF16, align_bytes=64)
         e_codes = keep.tile([P, BATCH], U32, align_bytes=64)
         e_scales = keep.tile([P, BATCH], U8, align_bytes=64)
 
-        def quantise_e_half(half):
+        def selu_plane(half, j):
             rows = slice(half * HALF, (half + 1) * HALF)
-            for j in range(PACK):
-                u, odd = divmod(j, 2)
-                x = xt[u][half][:].bitcast(BF16).rearrange("p t (b o) -> p (t b) o", o=2)[:, :, odd]
-                below = e_stage.tile([P, HALF], F32, tag="e_below")
-                nc.scalar.activation(
-                    out=below[:], in_=x, func=ACT.Relu,
-                    scale=scale2[:, 0, j : j + 1], bias=offset2[:, 0, j : j + 1],
-                )
-                linear = e_stage.tile([P, HALF], F32, tag="e_linear")
-                nc.scalar.activation(
-                    out=linear[:], in_=x, func=ACT.Relu,
-                    scale=scale2[:, 1, j : j + 1], bias=offset2[:, 1, j : j + 1],
-                )
-                decay = e_stage.tile([P, HALF], F32, tag="e_decay")
-                nc.scalar.activation(
-                    out=decay[:], in_=below[:], func=ACT.Exp, scale=-1.0, bias=log_col[:]
-                )
-                nc.vector.scalar_tensor_tensor(
-                    out=e_planes[:, j, rows], in0=decay[:], scalar=LAMBDA * ALPHA, in1=linear[:],
-                    op0=ALU.subtract, op1=ALU.add,
-                )
+            u, odd = divmod(j, 2)
+            x = xt[u][half][:].bitcast(BF16).rearrange("p t (b o) -> p (t b) o", o=2)[:, :, odd]
+            below = e_stage.tile([P, HALF], F32, tag="e_below")
+            nc.scalar.activation(
+                out=below[:], in_=x, func=ACT.Relu,
+                scale=scale2[:, 0, j : j + 1], bias=offset2[:, 0, j : j + 1],
+            )
+            linear = e_stage.tile([P, HALF], F32, tag="e_linear")
+            nc.scalar.activation(
+                out=linear[:], in_=x, func=ACT.Relu,
+                scale=scale2[:, 1, j : j + 1], bias=offset2[:, 1, j : j + 1],
+            )
+            decayed = e_stage.tile([P, HALF], F32, tag="e_decayed")
+            nc.scalar.activation(
+                out=decayed[:], in_=below[:], func=ACT.Exp, scale=-1.0, bias=log_col[:]
+            )
+            nc.vector.scalar_tensor_tensor(
+                out=e_planes[:, j, rows], in0=decayed[:], scalar=LAMBDA * ALPHA, in1=linear[:],
+                op0=ALU.subtract, op1=ALU.add,
+            )
+
+        def regroup_e(half):
+            rows = slice(half * HALF, (half + 1) * HALF)
             nc.vector.tensor_copy(
                 out=e_grouped[:, rows, :], in_=e_planes[:, :, rows].rearrange("p j b -> p b j")
             )
+
+        def quantise_e(half):
+            rows = slice(half * HALF, (half + 1) * HALF)
             nc.vector.quantize_mx(
                 out=e_codes[:, rows].bitcast(FP8X4),
                 scales=e_scales[:, rows],
                 in_=e_grouped[:, rows, :].rearrange("p b j -> p (b j)"),
             )
 
-        quantise_w_chunk(0)
-        quantise_e_half(0)
-        quantise_w_chunk(1)
-        quantise_e_half(1)
-        for k in range(2, CHUNKS):
-            quantise_w_chunk(k)
+        for half in range(2):
+            first = 3 * half
+            quantise_w(first)
+            selu_plane(half, 0)
+            regroup_w(first + 1)
+            selu_plane(half, 1)
+            quantise_w(first + 1)
+            selu_plane(half, 2)
+            regroup_w(first + 2)
+            selu_plane(half, 3)
+            regroup_e(half)
+            quantise_w(first + 2)
+            quantise_e(half)
+            if half == 0:
+                regroup_w(first + 3)
 
         out_rows = out.rearrange("(p t) h g e -> p t (h g e)", t=BATCH_TILES)
         rounds = [(half, c) for half in range(2) for c in range(COL_TILES)]
@@ -333,19 +348,18 @@ def tile_basicemotionpredictions_pa_kernel(tc, h2, gamma, beta, Wh, bh, out):
                     in_=result[:],
                 )
 
-        stages = (
-            (multiply, 0),
-            (turn, 2),
-            (magnitude, 3),
-            (decay, 0),
-            (total, 5),
-            (scale_and_store, 6),
-            (floor, 5),
-            (combine, 1),
-            (fold, 4),
-            (invert, 5),
-        )
+        def at(stage, n):
+            if 0 <= n < len(rounds):
+                stage(n)
+
         for s in range(len(rounds) + 6):
-            for stage, lag in stages:
-                if 0 <= s - lag < len(rounds):
-                    stage(s - lag)
+            at(multiply, s)
+            at(turn, s - 2)
+            at(magnitude, s - 3)
+            at(decay, s)
+            at(total, s - 5)
+            at(scale_and_store, s - 6)
+            at(floor, s - 5)
+            at(combine, s - 1)
+            at(fold, s - 4)
+            at(invert, s - 5)

@@ -256,9 +256,13 @@ def tile_basicemotionpredictions_pa_kernel(tc, h2, gamma, beta, Wh, bh, out):
                 start=True, stop=True,
             )
             p_tiles[n] = p_t
+
+        def clamp(n):
+            c = rounds[n][1]
             below = work.tile([P, HALF], F32, tag="below")
             nc.scalar.activation(
-                out=below[:], in_=p_t[:], func=ACT.Relu, bias=bias_minus[:, c : c + 1], scale=-1.0
+                out=below[:], in_=p_tiles[n][:], func=ACT.Relu, bias=bias_minus[:, c : c + 1],
+                scale=-1.0,
             )
             belows[n] = below
 
@@ -352,9 +356,10 @@ def tile_basicemotionpredictions_pa_kernel(tc, h2, gamma, beta, Wh, bh, out):
             if 0 <= n < len(rounds):
                 stage(n)
 
-        for s in range(len(rounds) + 6):
-            at(multiply, s)
+        for s in range(-1, len(rounds) + 6):
+            at(multiply, s + 1)
             at(turn, s - 2)
+            at(clamp, s)
             at(magnitude, s - 3)
             at(decay, s)
             at(total, s - 5)

@@ -34,6 +34,7 @@ ALPHA = 1.6732632423543772
 LAMBDA = 1.0507009873554805
 L1_FLOOR = 1e-12 / LAMBDA
 SLOTS = 4
+RUN = 4
 
 FLOPS = 2 * BATCH * HID * COLS
 
@@ -47,7 +48,7 @@ def tile_basicemotionpredictions_pa_kernel(tc, h2, gamma, beta, Wh, bh, out):
         e_stage = ctx.enter_context(tc.tile_pool(name="e_stage", bufs=3))
         work = ctx.enter_context(tc.tile_pool(name="work", bufs=4))
         small = ctx.enter_context(tc.tile_pool(name="small", bufs=4))
-        out_stage = ctx.enter_context(tc.tile_pool(name="out_stage", bufs=3))
+        out_stage = ctx.enter_context(tc.tile_pool(name="out_stage", bufs=6))
         psum = ctx.enter_context(tc.psum_pool(name="psum", bufs=8))
 
         ctx.enter_context(tc.manual_schedule())
@@ -92,7 +93,8 @@ def tile_basicemotionpredictions_pa_kernel(tc, h2, gamma, beta, Wh, bh, out):
         def regroup_w(k):
             grouped = w_stage.tile([P, CHUNK_HEADS, E, PACK], BF16, align_bytes=64, tag="w_grouped")
             nc.vector.tensor_copy(
-                out=grouped[:], in_=w_raw[k][:].rearrange("p h (j e) -> p h e j", j=PACK)
+                out=grouped[:].rearrange("p h (c i) j -> p h c j i", i=RUN),
+                in_=w_raw[k][:].rearrange("p h (j c i) -> p h c j i", j=PACK, i=RUN),
             )
             w_grouped[k] = grouped
 
@@ -201,7 +203,8 @@ def tile_basicemotionpredictions_pa_kernel(tc, h2, gamma, beta, Wh, bh, out):
         def regroup_e(half):
             rows = slice(half * HALF, (half + 1) * HALF)
             nc.vector.tensor_copy(
-                out=e_grouped[:, rows, :], in_=e_planes[:, :, rows].rearrange("p j b -> p b j")
+                out=e_grouped[:, rows, :].rearrange("p (c i) j -> p c j i", i=RUN),
+                in_=e_planes[:, :, rows].rearrange("p j (c i) -> p c j i", i=RUN),
             )
 
         def quantise_e(half):
@@ -242,7 +245,6 @@ def tile_basicemotionpredictions_pa_kernel(tc, h2, gamma, beta, Wh, bh, out):
         folds = {}
         divisors = {}
         inverses = {}
-        results = {}
 
         def multiply(n):
             half, c = rounds[n]
@@ -327,14 +329,9 @@ def tile_basicemotionpredictions_pa_kernel(tc, h2, gamma, beta, Wh, bh, out):
 
         def scale_and_store(n):
             half, c = rounds[n]
-            k, i = divmod(c, CHUNK_TILES)
-            if i == 0:
-                results[(half, k)] = out_stage.tile(
-                    [P, TILES_PER_HALF, CHUNK_COLS], F32, name="result", tag="result"
-                )
-            result = results[(half, k)]
+            result = out_stage.tile([P, TILES_PER_HALF, P], F32, tag="result")
             nc.vector.tensor_tensor(
-                out=result[:, :, i * P : (i + 1) * P].rearrange("p t (h e) -> p t h e", e=E),
+                out=result[:].rearrange("p t (h e) -> p t h e", e=E),
                 in0=d_banks[n][:].rearrange("p t (h e) -> p t h e", e=E),
                 in1=inverses[n][:]
                 .rearrange("p (t h) -> p t h", h=HEADS_PER_TILE)
@@ -342,15 +339,12 @@ def tile_basicemotionpredictions_pa_kernel(tc, h2, gamma, beta, Wh, bh, out):
                 .to_broadcast([P, TILES_PER_HALF, HEADS_PER_TILE, E]),
                 op=ALU.mult,
             )
-            if i == CHUNK_TILES - 1:
-                nc.sync.dma_start(
-                    out=out_rows[
-                        :,
-                        half * TILES_PER_HALF : (half + 1) * TILES_PER_HALF,
-                        k * CHUNK_COLS : (k + 1) * CHUNK_COLS,
-                    ],
-                    in_=result[:],
-                )
+            nc.sync.dma_start(
+                out=out_rows[
+                    :, half * TILES_PER_HALF : (half + 1) * TILES_PER_HALF, c * P : (c + 1) * P
+                ],
+                in_=result[:],
+            )
 
         def at(stage, n):
             if 0 <= n < len(rounds):

@@ -23,17 +23,20 @@ BATCH_TILES = BATCH // P
 HALF = 512
 TILES_PER_HALF = HALF // P
 COL_TILES = COLS // P
-HEADS_PER_TILE = P // E
+SPLIT = 8
+SUB = E // SPLIT
+GROUP_HEADS = P // SUB
+HEAD_GROUPS = HEADS // GROUP_HEADS
+GROUP_COLS = GROUP_HEADS * E
 CHUNK_TILES = 4
 CHUNKS = COL_TILES // CHUNK_TILES
 CHUNK_COLS = CHUNK_TILES * P
-CHUNK_HEADS = CHUNK_COLS // E
+CHUNKS_PER_GROUP = SPLIT // CHUNK_TILES
 
 BN_EPS = 1e-5
 ALPHA = 1.6732632423543772
 LAMBDA = 1.0507009873554805
 L1_FLOOR = 1e-12 / LAMBDA
-SLOTS = 4
 RUN = 4
 
 FLOPS = 2 * BATCH * HID * COLS
@@ -43,13 +46,15 @@ def tile_basicemotionpredictions_pa_kernel(tc, h2, gamma, beta, Wh, bh, out):
     nc = tc.nc
     with ExitStack() as ctx:
         keep = ctx.enter_context(tc.tile_pool(name="keep", bufs=1))
-        w_in = ctx.enter_context(tc.tile_pool(name="w_in", bufs=CHUNKS))
+        w_in = ctx.enter_context(tc.tile_pool(name="w_in", bufs=HEAD_GROUPS))
         w_stage = ctx.enter_context(tc.tile_pool(name="w_stage", bufs=2))
         e_stage = ctx.enter_context(tc.tile_pool(name="e_stage", bufs=3))
-        work = ctx.enter_context(tc.tile_pool(name="work", bufs=4))
-        small = ctx.enter_context(tc.tile_pool(name="small", bufs=4))
-        out_stage = ctx.enter_context(tc.tile_pool(name="out_stage", bufs=6))
-        psum = ctx.enter_context(tc.psum_pool(name="psum", bufs=8))
+        work = ctx.enter_context(tc.tile_pool(name="work", bufs=3))
+        held = ctx.enter_context(tc.tile_pool(name="held", bufs=20))
+        small = ctx.enter_context(tc.tile_pool(name="small", bufs=2))
+        out_stage = ctx.enter_context(tc.tile_pool(name="out_stage", bufs=4))
+        psum = ctx.enter_context(tc.psum_pool(name="psum", bufs=3))
+        psum_acc = ctx.enter_context(tc.psum_pool(name="psum_acc", bufs=2))
 
         ctx.enter_context(tc.manual_schedule())
 
@@ -65,18 +70,25 @@ def tile_basicemotionpredictions_pa_kernel(tc, h2, gamma, beta, Wh, bh, out):
         nc.scalar.dma_start(out=beta_bf[:], in_=beta.rearrange("(p j) -> p j", j=PACK))
         bias_rows = keep.tile([P, P], BF16)
         nc.vector.memset(bias_rows[:], 0.0)
-        nc.scalar.dma_start(
-            out=bias_rows[0:COL_TILES, :],
-            in_=bh.rearrange("h (a b) e -> (h a) (b e)", b=HEADS_PER_TILE),
+        bh_tiles = bh.rearrange("h g e -> (h g) e").rearrange(
+            "(a n) (s i) -> a s n i", a=HEAD_GROUPS, i=SUB
         )
+        for g in range(HEAD_GROUPS):
+            nc.scalar.dma_start(
+                out=bias_rows[g * SPLIT : (g + 1) * SPLIT, :].rearrange("s (n i) -> s n i", i=SUB),
+                in_=bh_tiles[g],
+            )
 
         w_rows = Wh.rearrange("h g (p j) e -> p (h g) (j e)", j=PACK)
         w_raw = []
-        for k in range(CHUNKS):
-            raw = w_in.tile([P, CHUNK_HEADS, PACK * E], BF16, name="w_raw%d" % k, tag="w_raw")
-            nc.sync.dma_start(
-                out=raw[:], in_=w_rows[:, k * CHUNK_HEADS : (k + 1) * CHUNK_HEADS, :]
-            )
+        for g in range(HEAD_GROUPS):
+            raw = w_in.tile([P, GROUP_HEADS, PACK * E], BF16, name="w_raw%d" % g, tag="w_raw")
+            for part in range(2):
+                some = slice(part * GROUP_HEADS // 2, (part + 1) * GROUP_HEADS // 2)
+                nc.sync.dma_start(
+                    out=raw[:, some, :],
+                    in_=w_rows[:, g * GROUP_HEADS + some.start : g * GROUP_HEADS + some.stop, :],
+                )
             w_raw.append(raw)
 
         ident = keep.tile([P, P], F32)
@@ -91,10 +103,15 @@ def tile_basicemotionpredictions_pa_kernel(tc, h2, gamma, beta, Wh, bh, out):
         w_grouped = {}
 
         def regroup_w(k):
-            grouped = w_stage.tile([P, CHUNK_HEADS, E, PACK], BF16, align_bytes=64, tag="w_grouped")
+            g, a = divmod(k, CHUNKS_PER_GROUP)
+            grouped = w_stage.tile(
+                [P, CHUNK_TILES, GROUP_HEADS, SUB, PACK], BF16, align_bytes=64, tag="w_grouped"
+            )
             nc.vector.tensor_copy(
-                out=grouped[:].rearrange("p h (c i) j -> p h c j i", i=RUN),
-                in_=w_raw[k][:].rearrange("p h (j c i) -> p h c j i", j=PACK, i=RUN),
+                out=grouped[:].rearrange("p s n i j -> p s n j i"),
+                in_=w_raw[g][:].rearrange(
+                    "p n (j a s i) -> p a s n j i", j=PACK, a=CHUNKS_PER_GROUP, s=CHUNK_TILES
+                )[:, a],
             )
             w_grouped[k] = grouped
 
@@ -103,12 +120,15 @@ def tile_basicemotionpredictions_pa_kernel(tc, h2, gamma, beta, Wh, bh, out):
             nc.vector.quantize_mx(
                 out=w_codes[:, cols].bitcast(FP8X4),
                 scales=w_scales[:, cols],
-                in_=w_grouped[k][:].rearrange("p h e j -> p (h e j)"),
+                in_=w_grouped[k][:].rearrange("p s n i j -> p (s n i j)"),
             )
 
         xt = [
             [
-                psum.tile([P, TILES_PER_HALF, P], F32, name="xt%d%d" % (u, half), tag="bank")
+                psum.tile(
+                    [P, TILES_PER_HALF, P], F32, name="xt%d%d" % (u, half),
+                    tag=("product", "turned")[half],
+                )
                 for half in range(2)
             ]
             for u in range(2)
@@ -137,7 +157,7 @@ def tile_basicemotionpredictions_pa_kernel(tc, h2, gamma, beta, Wh, bh, out):
                 nc.vector.tensor_scalar_mul(shift2[:, 1, :], beta_bf[:], LAMBDA)
                 nc.vector.tensor_scalar_mul(log_col[:], one_col[:], math.log(LAMBDA * ALPHA))
                 nc.vector.tensor_copy(out=bias_rows_f[:], in_=bias_rows[:])
-        bias_ps = psum.tile([P, P], F32, tag="bank")
+        bias_ps = psum.tile([P, P], F32, tag="product")
         nc.tensor.transpose(bias_ps[:], bias_rows_f[:], ident[:])
 
         mean_var = keep.tile([P, PACK, 2], F32)
@@ -152,8 +172,15 @@ def tile_basicemotionpredictions_pa_kernel(tc, h2, gamma, beta, Wh, bh, out):
         nc.gpsimd.tensor_tensor(out=rstd[:], in0=var_eps[:], in1=neg_half[:], op=ALU.pow)
         bias_minus = keep.tile([P, COL_TILES], F32)
         nc.vector.tensor_scalar_mul(bias_minus[:], bias_ps[:, 0:COL_TILES], -1.0)
-        bias_less_alpha = keep.tile([P, COL_TILES], F32)
-        nc.vector.tensor_scalar_add(bias_less_alpha[:], bias_ps[:, 0:COL_TILES], -ALPHA)
+        bias_plus = keep.tile([P, COL_TILES], F32)
+        nc.vector.tensor_copy(out=bias_plus[:], in_=bias_ps[:, 0:COL_TILES])
+        bias_drop = keep.tile([P, COL_TILES], F32)
+        nc.vector.tensor_scalar(
+            out=bias_drop[:], in0=bias_ps[:, 0:COL_TILES], scalar1=-1.0, scalar2=-ALPHA,
+            op0=ALU.mult, op1=ALU.add,
+        )
+        bias_log = keep.tile([P, COL_TILES], F32)
+        nc.vector.tensor_scalar_add(bias_log[:], bias_ps[:, 0:COL_TILES], math.log(ALPHA))
         regroup_w(0)
         scale2 = keep.tile([P, 2, PACK], F32)
         nc.vector.tensor_tensor(
@@ -233,24 +260,22 @@ def tile_basicemotionpredictions_pa_kernel(tc, h2, gamma, beta, Wh, bh, out):
 
         out_rows = out.rearrange("(p t) h g e -> p t (h g e)", t=BATCH_TILES)
         rounds = [(half, c) for half in range(2) for c in range(COL_TILES)]
-        groups = TILES_PER_HALF * HEADS_PER_TILE
-        sum_floor = keep.tile([P, SLOTS, groups, 2], F32)
-        nc.vector.memset(sum_floor[:], L1_FLOOR)
         p_tiles = {}
-        belows = {}
-        decays = {}
+        growths = {}
+        curves = {}
+        lows = {}
         d_tiles = {}
-        d_banks = {}
         sizes = {}
-        folds = {}
-        divisors = {}
+        sums = {}
         inverses = {}
+        d_banks = {}
+        results = {}
 
         def multiply(n):
             half, c = rounds[n]
             rows = slice(half * HALF, (half + 1) * HALF)
             cols = slice(c * P, (c + 1) * P)
-            p_t = psum.tile([P, HALF], F32, tag="bank")
+            p_t = psum.tile([P, HALF], F32, tag="product")
             nc.tensor.matmul_mx(
                 out=p_t[:],
                 lhsT=w_codes[:, cols].bitcast(FP8X4), lhsT_scale=w_scales[:, cols],
@@ -259,106 +284,120 @@ def tile_basicemotionpredictions_pa_kernel(tc, h2, gamma, beta, Wh, bh, out):
             )
             p_tiles[n] = p_t
 
-        def clamp(n):
+        def grow(n):
             c = rounds[n][1]
-            below = work.tile([P, HALF], F32, tag="below")
+            grown = work.tile([P, HALF], F32, tag="grown")
             nc.scalar.activation(
-                out=below[:], in_=p_tiles[n][:], func=ACT.Relu, bias=bias_minus[:, c : c + 1],
-                scale=-1.0,
+                out=grown[:], in_=p_tiles[n][:], func=ACT.Exp, bias=bias_log[:, c : c + 1], scale=1.0
             )
-            belows[n] = below
+            growths[n] = grown
 
-        def decay(n):
-            decayed = work.tile([P, HALF], F32, tag="decayed")
-            nc.scalar.activation(out=decayed[:], in_=belows[n][:], func=ACT.Exp, scale=-1.0)
-            decays[n] = decayed
-
-        def combine(n):
+        def curve(n):
             c = rounds[n][1]
             curved = work.tile([P, HALF], F32, tag="curved")
             nc.gpsimd.tensor_scalar(
-                out=curved[:], in0=decays[n][:], scalar1=ALPHA,
-                scalar2=bias_less_alpha[:, c : c + 1], op0=ALU.mult, op1=ALU.add,
+                out=curved[:], in0=growths[n][:], scalar1=1.0,
+                scalar2=bias_drop[:, c : c + 1], op0=ALU.mult, op1=ALU.add,
             )
-            d_t = work.tile([P, HALF], F32, tag="d_t")
-            nc.vector.scalar_tensor_tensor(
-                out=d_t[:], in0=p_tiles[n][:], scalar=bias_minus[:, c : c + 1], in1=curved[:],
-                op0=ALU.max, op1=ALU.add,
-            )
-            d_tiles[n] = d_t
+            curves[n] = curved
 
-        def turn(n):
-            d_ps = psum.tile([P, TILES_PER_HALF, P], F32, tag="bank")
-            for t in range(TILES_PER_HALF):
-                nc.tensor.transpose(d_ps[:, t, :], d_tiles[n][:, t * P : (t + 1) * P], ident[:])
-            d_banks[n] = d_ps
+        def combine(n):
+            c = rounds[n][1]
+            low = work.tile([P, HALF], F32, tag="low")
+            nc.vector.scalar_tensor_tensor(
+                out=low[:], in0=p_tiles[n][:], scalar=bias_minus[:, c : c + 1], in1=curves[n][:],
+                op0=ALU.max, op1=ALU.min,
+            )
+            lows[n] = low
 
         def magnitude(n):
-            size = work.tile([P, groups, E], F32, tag="size")
+            c = rounds[n][1]
+            size = work.tile([P, HALF], F32, tag="size")
             nc.scalar.activation(
-                out=size[:], in_=d_banks[n][:].rearrange("p t (h e) -> p (t h) e", e=E), func=ACT.Abs
+                out=size[:], in_=lows[n][:], func=ACT.Abs, bias=bias_plus[:, c : c + 1], scale=1.0
             )
             sizes[n] = size
 
-        def fold(n):
-            folded = work.tile([P, groups, E // 2], F32, tag="folded")
-            nc.gpsimd.tensor_tensor(
-                out=folded[:], in0=sizes[n][:, :, 0 : E // 2], in1=sizes[n][:, :, E // 2 : E],
-                op=ALU.add,
+        def lift(n):
+            c = rounds[n][1]
+            d_t = held.tile([P, HALF], F32, tag="d_t")
+            nc.gpsimd.tensor_scalar(
+                out=d_t[:], in0=lows[n][:], scalar1=1.0,
+                scalar2=bias_plus[:, c : c + 1], op0=ALU.mult, op1=ALU.add,
             )
-            folds[n] = folded
+            d_tiles[n] = d_t
 
-        def total(n):
+        def fold(n):
+            q, s = divmod(n, SPLIT)
+            if s == 0:
+                sums[q] = psum_acc.tile([P, TILES_PER_HALF, P], F32, name="sums%d" % q, tag="sums")
+            for t in range(TILES_PER_HALF):
+                nc.tensor.matmul(
+                    out=sums[q][:, t, :], lhsT=sizes[n][:, t * P : (t + 1) * P], rhs=ident[:],
+                    is_transpose=True,
+                    start=(s == 0 and t == 0), stop=(s == SPLIT - 1 and t == TILES_PER_HALF - 1),
+                )
+
+        def norm(q):
+            total = small.tile([P, TILES_PER_HALF * GROUP_HEADS], F32, tag="total")
             nc.vector.tensor_reduce(
-                out=sum_floor[:, n % SLOTS, :, 0], in_=folds[n][:],
+                out=total[:], in_=sums[q][:].rearrange("p t (n i) -> p (t n) i", i=SUB),
                 axis=mybir.AxisListType.X, op=ALU.add,
             )
+            divisor = small.tile([P, TILES_PER_HALF * GROUP_HEADS], F32, tag="divisor")
+            nc.vector.tensor_scalar_max(divisor[:], total[:], L1_FLOOR)
+            inverse = small.tile([P, TILES_PER_HALF, GROUP_HEADS], F32, tag="inverse")
+            nc.vector.reciprocal(out=inverse[:].rearrange("p t n -> p (t n)"), in_=divisor[:])
+            inverses[q] = inverse
 
-        def floor(n):
-            divisor = small.tile([P, groups], F32, tag="divisor")
-            nc.vector.tensor_reduce(
-                out=divisor[:], in_=sum_floor[:, n % SLOTS, :, :],
-                axis=mybir.AxisListType.X, op=ALU.max,
-            )
-            divisors[n] = divisor
+        def turn(x):
+            q, u = divmod(x, SPLIT)
+            t, a = divmod(u, CHUNKS_PER_GROUP)
+            d_ps = psum.tile([P, CHUNK_TILES, P], F32, tag="turned")
+            for i in range(CHUNK_TILES):
+                n = q * SPLIT + a * CHUNK_TILES + i
+                nc.tensor.transpose(d_ps[:, i, :], d_tiles[n][:, t * P : (t + 1) * P], ident[:])
+            d_banks[x] = d_ps
 
-        def invert(n):
-            inverse = small.tile([P, groups], F32, tag="inverse")
-            nc.vector.reciprocal(out=inverse[:], in_=divisors[n][:])
-            inverses[n] = inverse
-
-        def scale_and_store(n):
-            half, c = rounds[n]
-            result = out_stage.tile([P, TILES_PER_HALF, P], F32, tag="result")
+        def scale_and_store(x):
+            q, u = divmod(x, SPLIT)
+            t, a = divmod(u, CHUNKS_PER_GROUP)
+            half, g = divmod(q, HEAD_GROUPS)
+            if a == 0:
+                results[q, t] = out_stage.tile([P, GROUP_COLS], F32, name="result", tag="result")
+            result = results[q, t]
             nc.vector.tensor_tensor(
-                out=result[:].rearrange("p t (h e) -> p t h e", e=E),
-                in0=d_banks[n][:].rearrange("p t (h e) -> p t h e", e=E),
-                in1=inverses[n][:]
-                .rearrange("p (t h) -> p t h", h=HEADS_PER_TILE)
+                out=result[:].rearrange("p (n s i) -> p s n i", s=SPLIT, i=SUB)[
+                    :, a * CHUNK_TILES : (a + 1) * CHUNK_TILES
+                ],
+                in0=d_banks[x][:].rearrange("p s (n i) -> p s n i", i=SUB),
+                in1=inverses[q][:, t, :]
+                .unsqueeze(1)
                 .unsqueeze(3)
-                .to_broadcast([P, TILES_PER_HALF, HEADS_PER_TILE, E]),
+                .to_broadcast([P, CHUNK_TILES, GROUP_HEADS, SUB]),
                 op=ALU.mult,
             )
-            nc.sync.dma_start(
-                out=out_rows[
-                    :, half * TILES_PER_HALF : (half + 1) * TILES_PER_HALF, c * P : (c + 1) * P
-                ],
-                in_=result[:],
-            )
+            if a == CHUNKS_PER_GROUP - 1:
+                nc.sync.dma_start(
+                    out=out_rows[
+                        :, half * TILES_PER_HALF + t, g * GROUP_COLS : (g + 1) * GROUP_COLS
+                    ],
+                    in_=result[:],
+                )
 
         def at(stage, n):
             if 0 <= n < len(rounds):
                 stage(n)
 
-        for s in range(-1, len(rounds) + 6):
-            at(multiply, s + 1)
-            at(turn, s - 2)
-            at(clamp, s)
-            at(magnitude, s - 3)
-            at(decay, s)
-            at(total, s - 5)
-            at(scale_and_store, s - 6)
-            at(floor, s - 5)
-            at(combine, s - 1)
-            at(fold, s - 4)
-            at(invert, s - 5)
+        for j in range(-1, len(rounds) + 13):
+            at(multiply, j + 1)
+            at(fold, j - 3)
+            at(turn, j - 11)
+            at(grow, j)
+            at(magnitude, j - 2)
+            at(lift, j - 2)
+            at(curve, j)
+            at(scale_and_store, j - 12)
+            if j >= 11 and (j - 11) % SPLIT == 0 and (j - 11) // SPLIT < len(rounds) // SPLIT:
+                norm((j - 11) // SPLIT)
+            at(combine, j - 1)

@@ -37,6 +37,9 @@ BN_EPS = 1e-5
 ALPHA = 1.6732632423543772
 LAMBDA = 1.0507009873554805
 L1_FLOOR = 1e-12 / LAMBDA
+RAMP_PERIOD = 5
+VECTOR_RAMPS = (1, 3)
+Z_FACTORS = (1.0, LAMBDA, -1.0)
 RUN = 4
 
 FLOPS = 2 * BATCH * HID * COLS
@@ -48,8 +51,8 @@ def tile_basicemotionpredictions_pa_kernel(tc, h2, gamma, beta, Wh, bh, out):
         keep = ctx.enter_context(tc.tile_pool(name="keep", bufs=1))
         w_in = ctx.enter_context(tc.tile_pool(name="w_in", bufs=HEAD_GROUPS))
         w_stage = ctx.enter_context(tc.tile_pool(name="w_stage", bufs=2))
-        e_stage = ctx.enter_context(tc.tile_pool(name="e_stage", bufs=3))
-        work = ctx.enter_context(tc.tile_pool(name="work", bufs=3))
+        e_stage = ctx.enter_context(tc.tile_pool(name="e_stage", bufs=4))
+        work = ctx.enter_context(tc.tile_pool(name="work", bufs=4))
         held = ctx.enter_context(tc.tile_pool(name="held", bufs=20))
         small = ctx.enter_context(tc.tile_pool(name="small", bufs=2))
         out_stage = ctx.enter_context(tc.tile_pool(name="out_stage", bufs=4))
@@ -134,8 +137,8 @@ def tile_basicemotionpredictions_pa_kernel(tc, h2, gamma, beta, Wh, bh, out):
             for u in range(2)
         ]
         stats = keep.tile([P, 2, 4, 6], F32)
-        gain2 = keep.tile([P, 2, PACK], F32)
-        shift2 = keep.tile([P, 2, PACK], F32)
+        gain2 = keep.tile([P, len(Z_FACTORS), PACK], F32)
+        shift2 = keep.tile([P, len(Z_FACTORS), PACK], F32)
         log_col = keep.tile([P, 1], F32)
         bias_rows_f = keep.tile([P, P], F32)
         for half in range(2):
@@ -151,10 +154,9 @@ def tile_basicemotionpredictions_pa_kernel(tc, h2, gamma, beta, Wh, bh, out):
                         in_=pairs[:, 2 * s : 2 * s + 2, :].rearrange("p t w -> p (t w)"),
                     )
             if half == 0:
-                nc.vector.tensor_scalar_mul(gain2[:, 0, :], gamma_bf[:], -1.0)
-                nc.vector.tensor_scalar_mul(gain2[:, 1, :], gamma_bf[:], LAMBDA)
-                nc.vector.tensor_scalar_mul(shift2[:, 0, :], beta_bf[:], -1.0)
-                nc.vector.tensor_scalar_mul(shift2[:, 1, :], beta_bf[:], LAMBDA)
+                for row, factor in enumerate(Z_FACTORS):
+                    nc.vector.tensor_scalar_mul(gain2[:, row, :], gamma_bf[:], factor)
+                    nc.vector.tensor_scalar_mul(shift2[:, row, :], beta_bf[:], factor)
                 nc.vector.tensor_scalar_mul(log_col[:], one_col[:], math.log(LAMBDA * ALPHA))
                 nc.vector.tensor_copy(out=bias_rows_f[:], in_=bias_rows[:])
         bias_ps = psum.tile([P, P], F32, tag="product")
@@ -170,58 +172,73 @@ def tile_basicemotionpredictions_pa_kernel(tc, h2, gamma, beta, Wh, bh, out):
         nc.vector.tensor_scalar_add(var_eps[:], mean_var[:, :, 1], BN_EPS)
         rstd = keep.tile([P, PACK], F32)
         nc.gpsimd.tensor_tensor(out=rstd[:], in0=var_eps[:], in1=neg_half[:], op=ALU.pow)
-        bias_minus = keep.tile([P, COL_TILES], F32)
-        nc.vector.tensor_scalar_mul(bias_minus[:], bias_ps[:, 0:COL_TILES], -1.0)
         bias_plus = keep.tile([P, COL_TILES], F32)
         nc.vector.tensor_copy(out=bias_plus[:], in_=bias_ps[:, 0:COL_TILES])
-        bias_drop = keep.tile([P, COL_TILES], F32)
-        nc.vector.tensor_scalar(
-            out=bias_drop[:], in0=bias_ps[:, 0:COL_TILES], scalar1=-1.0, scalar2=-ALPHA,
-            op0=ALU.mult, op1=ALU.add,
-        )
         bias_log = keep.tile([P, COL_TILES], F32)
         nc.vector.tensor_scalar_add(bias_log[:], bias_ps[:, 0:COL_TILES], math.log(ALPHA))
         regroup_w(0)
-        scale2 = keep.tile([P, 2, PACK], F32)
+        scale2 = keep.tile([P, len(Z_FACTORS), PACK], F32)
         nc.vector.tensor_tensor(
             out=scale2[:],
             in0=gain2[:],
-            in1=rstd[:].unsqueeze(1).to_broadcast([P, 2, PACK]),
+            in1=rstd[:].unsqueeze(1).to_broadcast([P, len(Z_FACTORS), PACK]),
             op=ALU.mult,
         )
-        mean_scaled = keep.tile([P, 2, PACK], F32)
+        mean_scaled = keep.tile([P, len(Z_FACTORS), PACK], F32)
         nc.vector.tensor_tensor(
             out=mean_scaled[:],
             in0=scale2[:],
-            in1=mean_var[:, :, 0].unsqueeze(1).to_broadcast([P, 2, PACK]),
+            in1=mean_var[:, :, 0].unsqueeze(1).to_broadcast([P, len(Z_FACTORS), PACK]),
             op=ALU.mult,
         )
-        offset2 = keep.tile([P, 2, PACK], F32)
+        offset2 = keep.tile([P, len(Z_FACTORS), PACK], F32)
         nc.vector.tensor_tensor(out=offset2[:], in0=shift2[:], in1=mean_scaled[:], op=ALU.subtract)
+        offset_log = keep.tile([P, PACK], F32)
+        nc.vector.tensor_scalar_add(offset_log[:], offset2[:, 0, :], math.log(LAMBDA * ALPHA))
 
         e_planes = keep.tile([P, PACK, BATCH], BF16)
         e_grouped = keep.tile([P, BATCH, PACK], BF16, align_bytes=64)
         e_codes = keep.tile([P, BATCH], U32, align_bytes=64)
         e_scales = keep.tile([P, BATCH], U8, align_bytes=64)
 
-        def selu_plane(half, j):
-            rows = slice(half * HALF, (half + 1) * HALF)
+        e_parts = {}
+
+        e_clamped = {}
+
+        def feature(half, j):
             u, odd = divmod(j, 2)
-            x = xt[u][half][:].bitcast(BF16).rearrange("p t (b o) -> p (t b) o", o=2)[:, :, odd]
-            below = e_stage.tile([P, HALF], F32, tag="e_below")
-            nc.scalar.activation(
-                out=below[:], in_=x, func=ACT.Relu,
-                scale=scale2[:, 0, j : j + 1], bias=offset2[:, 0, j : j + 1],
+            return xt[u][half][:].bitcast(BF16).rearrange("p t (b o) -> p (t b) o", o=2)[:, :, odd]
+
+        def clamp_by_vector(half, j):
+            clamped = e_stage.tile([P, HALF], F32, tag="e_clamped")
+            nc.vector.tensor_scalar(
+                out=clamped[:], in0=feature(half, j), scalar1=scale2[:, 0, j : j + 1],
+                scalar2=offset2[:, 2, j : j + 1], op0=ALU.mult, op1=ALU.min,
             )
+            e_clamped[half, j] = (clamped, 1.0, offset_log[:, j : j + 1])
+
+        def clamp_by_scalar(half, j):
+            clamped = e_stage.tile([P, HALF], F32, tag="e_clamped")
+            nc.scalar.activation(
+                out=clamped[:], in_=feature(half, j), func=ACT.Relu,
+                scale=scale2[:, 2, j : j + 1], bias=offset2[:, 2, j : j + 1],
+            )
+            e_clamped[half, j] = (clamped, -1.0, log_col[:])
+
+        def selu_parts(half, j):
+            clamped, sign, bias = e_clamped[half, j]
+            decayed = e_stage.tile([P, HALF], F32, tag="e_decayed")
+            nc.scalar.activation(out=decayed[:], in_=clamped[:], func=ACT.Exp, scale=sign, bias=bias)
             linear = e_stage.tile([P, HALF], F32, tag="e_linear")
             nc.scalar.activation(
-                out=linear[:], in_=x, func=ACT.Relu,
+                out=linear[:], in_=feature(half, j), func=ACT.Relu,
                 scale=scale2[:, 1, j : j + 1], bias=offset2[:, 1, j : j + 1],
             )
-            decayed = e_stage.tile([P, HALF], F32, tag="e_decayed")
-            nc.scalar.activation(
-                out=decayed[:], in_=below[:], func=ACT.Exp, scale=-1.0, bias=log_col[:]
-            )
+            e_parts[half, j] = (decayed, linear)
+
+        def selu_plane(half, j):
+            rows = slice(half * HALF, (half + 1) * HALF)
+            decayed, linear = e_parts[half, j]
             nc.vector.scalar_tensor_tensor(
                 out=e_planes[:, j, rows], in0=decayed[:], scalar=LAMBDA * ALPHA, in1=linear[:],
                 op0=ALU.subtract, op1=ALU.add,
@@ -242,28 +259,32 @@ def tile_basicemotionpredictions_pa_kernel(tc, h2, gamma, beta, Wh, bh, out):
                 in_=e_grouped[:, rows, :].rearrange("p b j -> p (b j)"),
             )
 
-        for half in range(2):
-            first = 3 * half
-            quantise_w(first)
-            selu_plane(half, 0)
-            regroup_w(first + 1)
-            selu_plane(half, 1)
-            quantise_w(first + 1)
-            selu_plane(half, 2)
-            regroup_w(first + 2)
-            selu_plane(half, 3)
-            regroup_e(half)
-            quantise_w(first + 2)
-            quantise_e(half)
-            if half == 0:
-                regroup_w(first + 3)
+        clamp_by_vector(0, 0)
+        clamp_by_vector(0, 1)
+        selu_parts(0, 0)
+        quantise_w(0)
+        clamp_by_vector(0, 2)
+        selu_parts(0, 1)
+        selu_plane(0, 0)
+        clamp_by_vector(0, 3)
+        selu_parts(0, 2)
+        selu_plane(0, 1)
+        regroup_w(1)
+        selu_parts(0, 3)
+        selu_plane(0, 2)
+        clamp_by_scalar(1, 0)
+        selu_plane(0, 3)
+        selu_parts(1, 0)
+        regroup_e(0)
+        clamp_by_scalar(1, 1)
+        quantise_w(1)
+        quantise_e(0)
 
         out_rows = out.rearrange("(p t) h g e -> p t (h g e)", t=BATCH_TILES)
         rounds = [(half, c) for half in range(2) for c in range(COL_TILES)]
         p_tiles = {}
         growths = {}
-        curves = {}
-        lows = {}
+        ramps = {}
         d_tiles = {}
         sizes = {}
         sums = {}
@@ -292,40 +313,33 @@ def tile_basicemotionpredictions_pa_kernel(tc, h2, gamma, beta, Wh, bh, out):
             )
             growths[n] = grown
 
-        def curve(n):
+        def ramp(n):
             c = rounds[n][1]
-            curved = work.tile([P, HALF], F32, tag="curved")
-            nc.gpsimd.tensor_scalar(
-                out=curved[:], in0=growths[n][:], scalar1=1.0,
-                scalar2=bias_drop[:, c : c + 1], op0=ALU.mult, op1=ALU.add,
-            )
-            curves[n] = curved
+            ramped = work.tile([P, HALF], F32, tag="ramped")
+            if n % RAMP_PERIOD in VECTOR_RAMPS:
+                nc.vector.tensor_scalar(
+                    out=ramped[:], in0=p_tiles[n][:], scalar1=bias_plus[:, c : c + 1], scalar2=0.0,
+                    op0=ALU.add, op1=ALU.max,
+                )
+            else:
+                nc.scalar.activation(
+                    out=ramped[:], in_=p_tiles[n][:], func=ACT.Relu, bias=bias_plus[:, c : c + 1],
+                    scale=1.0,
+                )
+            ramps[n] = ramped
 
         def combine(n):
-            c = rounds[n][1]
-            low = work.tile([P, HALF], F32, tag="low")
-            nc.vector.scalar_tensor_tensor(
-                out=low[:], in0=p_tiles[n][:], scalar=bias_minus[:, c : c + 1], in1=curves[n][:],
-                op0=ALU.max, op1=ALU.min,
-            )
-            lows[n] = low
-
-        def magnitude(n):
-            c = rounds[n][1]
-            size = work.tile([P, HALF], F32, tag="size")
-            nc.scalar.activation(
-                out=size[:], in_=lows[n][:], func=ACT.Abs, bias=bias_plus[:, c : c + 1], scale=1.0
-            )
-            sizes[n] = size
-
-        def lift(n):
-            c = rounds[n][1]
             d_t = held.tile([P, HALF], F32, tag="d_t")
-            nc.gpsimd.tensor_scalar(
-                out=d_t[:], in0=lows[n][:], scalar1=1.0,
-                scalar2=bias_plus[:, c : c + 1], op0=ALU.mult, op1=ALU.add,
+            nc.vector.scalar_tensor_tensor(
+                out=d_t[:], in0=growths[n][:], scalar=ALPHA, in1=ramps[n][:],
+                op0=ALU.subtract, op1=ALU.min,
             )
             d_tiles[n] = d_t
+
+        def magnitude(n):
+            size = work.tile([P, HALF], F32, tag="size")
+            nc.scalar.activation(out=size[:], in_=d_tiles[n][:], func=ACT.Abs)
+            sizes[n] = size
 
         def fold(n):
             q, s = divmod(n, SPLIT)
@@ -389,15 +403,43 @@ def tile_basicemotionpredictions_pa_kernel(tc, h2, gamma, beta, Wh, bh, out):
             if 0 <= n < len(rounds):
                 stage(n)
 
-        for j in range(-1, len(rounds) + 13):
+        def ramp_if(n, by_vector):
+            if 0 <= n < len(rounds) and (n % RAMP_PERIOD in VECTOR_RAMPS) == by_vector:
+                ramp(n)
+
+        def later(stage, *what):
+            return lambda: stage(*what)
+
+        woven = {
+            0: ([later(selu_parts, 1, 1)], [later(selu_plane, 1, 0)]),
+            1: ([later(clamp_by_scalar, 1, 2)], [later(selu_plane, 1, 1)]),
+            2: ([later(selu_parts, 1, 2)], [later(regroup_w, 2)]),
+            3: ([later(clamp_by_scalar, 1, 3)], [later(selu_plane, 1, 2)]),
+            4: ([later(selu_parts, 1, 3)], [later(quantise_w, 2)]),
+            5: ([], [later(selu_plane, 1, 3)]),
+            8: ([], [later(regroup_e, 1)]),
+            11: ([], [later(quantise_e, 1)]),
+            6: ([], [later(regroup_w, 3)]),
+            7: ([], [later(quantise_w, 3)]),
+            9: ([], [later(regroup_w, 4)]),
+            10: ([], [later(quantise_w, 4)]),
+            12: ([], [later(regroup_w, 5)]),
+            13: ([], [later(quantise_w, 5)]),
+        }
+
+        for j in range(-1, len(rounds) + 14):
             at(multiply, j + 1)
-            at(fold, j - 3)
-            at(turn, j - 11)
+            at(fold, j - 4)
+            at(turn, j - 12)
+            at(magnitude, j - 3)
             at(grow, j)
-            at(magnitude, j - 2)
-            at(lift, j - 2)
-            at(curve, j)
-            at(scale_and_store, j - 12)
-            if j >= 11 and (j - 11) % SPLIT == 0 and (j - 11) // SPLIT < len(rounds) // SPLIT:
-                norm((j - 11) // SPLIT)
-            at(combine, j - 1)
+            ramp_if(j, False)
+            for task in woven.get(j, ([], []))[0]:
+                task()
+            at(scale_and_store, j - 13)
+            ramp_if(j - 1, True)
+            if j >= 12 and (j - 12) % SPLIT == 0 and (j - 12) // SPLIT < len(rounds) // SPLIT:
+                norm((j - 12) // SPLIT)
+            at(combine, j - 2)
+            for task in woven.get(j, ([], []))[1]:
+                task()

@@ -37,8 +37,8 @@ BN_EPS = 1e-5
 ALPHA = 1.6732632423543772
 LAMBDA = 1.0507009873554805
 L1_FLOOR = 1e-12 / LAMBDA
-RAMP_PERIOD = 5
-VECTOR_RAMPS = (1, 3)
+LIFT_PERIOD = 5
+SCALAR_LIFTS = (1, 3)
 Z_FACTORS = (1.0, LAMBDA, -1.0)
 RUN = 4
 
@@ -56,7 +56,8 @@ def tile_basicemotionpredictions_pa_kernel(tc, h2, gamma, beta, Wh, bh, out):
         held = ctx.enter_context(tc.tile_pool(name="held", bufs=20))
         small = ctx.enter_context(tc.tile_pool(name="small", bufs=2))
         out_stage = ctx.enter_context(tc.tile_pool(name="out_stage", bufs=4))
-        psum = ctx.enter_context(tc.psum_pool(name="psum", bufs=3))
+        psum = ctx.enter_context(tc.psum_pool(name="psum", bufs=4))
+        psum_turn = ctx.enter_context(tc.psum_pool(name="psum_turn", bufs=2))
         psum_acc = ctx.enter_context(tc.psum_pool(name="psum_acc", bufs=2))
 
         ctx.enter_context(tc.manual_schedule())
@@ -105,17 +106,21 @@ def tile_basicemotionpredictions_pa_kernel(tc, h2, gamma, beta, Wh, bh, out):
         w_scales = keep.tile([P, COLS], U8, align_bytes=64)
         w_grouped = {}
 
-        def regroup_w(k):
+        def regroup_w(k, by_scalar=False):
             g, a = divmod(k, CHUNKS_PER_GROUP)
             grouped = w_stage.tile(
                 [P, CHUNK_TILES, GROUP_HEADS, SUB, PACK], BF16, align_bytes=64, tag="w_grouped"
             )
-            nc.vector.tensor_copy(
-                out=grouped[:].rearrange("p s n i j -> p s n j i"),
-                in_=w_raw[g][:].rearrange(
-                    "p n (j a s i) -> p a s n j i", j=PACK, a=CHUNKS_PER_GROUP, s=CHUNK_TILES
-                )[:, a],
-            )
+            spread = w_raw[g][:].rearrange(
+                "p n (j a s i) -> p a s n j i", j=PACK, a=CHUNKS_PER_GROUP, s=CHUNK_TILES
+            )[:, a]
+            if by_scalar:
+                for s in range(CHUNK_TILES):
+                    nc.scalar.copy(
+                        out=grouped[:, s].rearrange("p n i j -> p n j i"), in_=spread[:, s]
+                    )
+            else:
+                nc.vector.tensor_copy(out=grouped[:].rearrange("p s n i j -> p s n j i"), in_=spread)
             w_grouped[k] = grouped
 
         def quantise_w(k):
@@ -128,7 +133,7 @@ def tile_basicemotionpredictions_pa_kernel(tc, h2, gamma, beta, Wh, bh, out):
 
         xt = [
             [
-                psum.tile(
+                (psum, psum_turn)[half].tile(
                     [P, TILES_PER_HALF, P], F32, name="xt%d%d" % (u, half),
                     tag=("product", "turned")[half],
                 )
@@ -162,6 +167,8 @@ def tile_basicemotionpredictions_pa_kernel(tc, h2, gamma, beta, Wh, bh, out):
         bias_ps = psum.tile([P, P], F32, tag="product")
         nc.tensor.transpose(bias_ps[:], bias_rows_f[:], ident[:])
 
+        regroup_w(0, by_scalar=True)
+
         mean_var = keep.tile([P, PACK, 2], F32)
         for u in range(2):
             for odd in range(2):
@@ -174,9 +181,15 @@ def tile_basicemotionpredictions_pa_kernel(tc, h2, gamma, beta, Wh, bh, out):
         nc.gpsimd.tensor_tensor(out=rstd[:], in0=var_eps[:], in1=neg_half[:], op=ALU.pow)
         bias_plus = keep.tile([P, COL_TILES], F32)
         nc.vector.tensor_copy(out=bias_plus[:], in_=bias_ps[:, 0:COL_TILES])
+        bias_minus = keep.tile([P, COL_TILES], F32)
+        nc.vector.tensor_scalar_mul(bias_minus[:], bias_ps[:, 0:COL_TILES], -1.0)
+        bias_drop = keep.tile([P, COL_TILES], F32)
+        nc.vector.tensor_scalar(
+            out=bias_drop[:], in0=bias_ps[:, 0:COL_TILES], scalar1=-1.0, scalar2=-ALPHA,
+            op0=ALU.mult, op1=ALU.add,
+        )
         bias_log = keep.tile([P, COL_TILES], F32)
         nc.vector.tensor_scalar_add(bias_log[:], bias_ps[:, 0:COL_TILES], math.log(ALPHA))
-        regroup_w(0)
         scale2 = keep.tile([P, len(Z_FACTORS), PACK], F32)
         nc.vector.tensor_tensor(
             out=scale2[:],
@@ -225,34 +238,37 @@ def tile_basicemotionpredictions_pa_kernel(tc, h2, gamma, beta, Wh, bh, out):
             )
             e_clamped[half, j] = (clamped, -1.0, log_col[:])
 
-        def selu_parts(half, j):
+        def selu_parts(half, j, first=0, count=HALF):
             clamped, sign, bias = e_clamped[half, j]
-            decayed = e_stage.tile([P, HALF], F32, tag="e_decayed")
-            nc.scalar.activation(out=decayed[:], in_=clamped[:], func=ACT.Exp, scale=sign, bias=bias)
-            linear = e_stage.tile([P, HALF], F32, tag="e_linear")
+            decayed = e_stage.tile([P, count], F32, tag="e_decayed")
             nc.scalar.activation(
-                out=linear[:], in_=feature(half, j), func=ACT.Relu,
+                out=decayed[:], in_=clamped[:, first : first + count], func=ACT.Exp, scale=sign,
+                bias=bias,
+            )
+            linear = e_stage.tile([P, count], F32, tag="e_linear")
+            nc.scalar.activation(
+                out=linear[:], in_=feature(half, j)[:, first : first + count], func=ACT.Relu,
                 scale=scale2[:, 1, j : j + 1], bias=offset2[:, 1, j : j + 1],
             )
-            e_parts[half, j] = (decayed, linear)
+            e_parts[half, j, first] = (decayed, linear)
 
-        def selu_plane(half, j):
-            rows = slice(half * HALF, (half + 1) * HALF)
-            decayed, linear = e_parts[half, j]
+        def selu_plane(half, j, first=0, count=HALF):
+            rows = slice(half * HALF + first, half * HALF + first + count)
+            decayed, linear = e_parts[half, j, first]
             nc.vector.scalar_tensor_tensor(
                 out=e_planes[:, j, rows], in0=decayed[:], scalar=LAMBDA * ALPHA, in1=linear[:],
                 op0=ALU.subtract, op1=ALU.add,
             )
 
-        def regroup_e(half):
-            rows = slice(half * HALF, (half + 1) * HALF)
+        def regroup_e(half, first=0, count=HALF):
+            rows = slice(half * HALF + first, half * HALF + first + count)
             nc.vector.tensor_copy(
                 out=e_grouped[:, rows, :].rearrange("p (c i) j -> p c j i", i=RUN),
                 in_=e_planes[:, :, rows].rearrange("p j (c i) -> p c j i", i=RUN),
             )
 
-        def quantise_e(half):
-            rows = slice(half * HALF, (half + 1) * HALF)
+        def quantise_e(half, first=0, count=HALF):
+            rows = slice(half * HALF + first, half * HALF + first + count)
             nc.vector.quantize_mx(
                 out=e_codes[:, rows].bitcast(FP8X4),
                 scales=e_scales[:, rows],
@@ -269,22 +285,27 @@ def tile_basicemotionpredictions_pa_kernel(tc, h2, gamma, beta, Wh, bh, out):
         clamp_by_vector(0, 3)
         selu_parts(0, 2)
         selu_plane(0, 1)
-        regroup_w(1)
-        selu_parts(0, 3)
+        selu_parts(0, 3, 0, HALF // 2)
         selu_plane(0, 2)
+        selu_parts(0, 3, HALF // 2, HALF // 2)
+        selu_plane(0, 3, 0, HALF // 2)
+        regroup_e(0, 0, HALF // 2)
         clamp_by_scalar(1, 0)
-        selu_plane(0, 3)
+        selu_plane(0, 3, HALF // 2, HALF // 2)
+        quantise_e(0, 0, HALF // 2)
+        regroup_e(0, HALF // 2, HALF // 2)
         selu_parts(1, 0)
-        regroup_e(0)
         clamp_by_scalar(1, 1)
-        quantise_w(1)
-        quantise_e(0)
+        selu_plane(1, 0)
+        quantise_e(0, HALF // 2, HALF // 2)
+        regroup_w(1)
 
         out_rows = out.rearrange("(p t) h g e -> p t (h g e)", t=BATCH_TILES)
         rounds = [(half, c) for half in range(2) for c in range(COL_TILES)]
         p_tiles = {}
         growths = {}
-        ramps = {}
+        curves = {}
+        lows = {}
         d_tiles = {}
         sizes = {}
         sums = {}
@@ -313,33 +334,46 @@ def tile_basicemotionpredictions_pa_kernel(tc, h2, gamma, beta, Wh, bh, out):
             )
             growths[n] = grown
 
-        def ramp(n):
+        def curve(n):
             c = rounds[n][1]
-            ramped = work.tile([P, HALF], F32, tag="ramped")
-            if n % RAMP_PERIOD in VECTOR_RAMPS:
-                nc.vector.tensor_scalar(
-                    out=ramped[:], in0=p_tiles[n][:], scalar1=bias_plus[:, c : c + 1], scalar2=0.0,
-                    op0=ALU.add, op1=ALU.max,
-                )
-            else:
-                nc.scalar.activation(
-                    out=ramped[:], in_=p_tiles[n][:], func=ACT.Relu, bias=bias_plus[:, c : c + 1],
-                    scale=1.0,
-                )
-            ramps[n] = ramped
+            curved = work.tile([P, HALF], F32, tag="curved")
+            nc.gpsimd.tensor_scalar(
+                out=curved[:], in0=growths[n][:], scalar1=1.0,
+                scalar2=bias_drop[:, c : c + 1], op0=ALU.mult, op1=ALU.add,
+            )
+            curves[n] = curved
 
         def combine(n):
-            d_t = held.tile([P, HALF], F32, tag="d_t")
+            c = rounds[n][1]
+            low = work.tile([P, HALF], F32, tag="low")
             nc.vector.scalar_tensor_tensor(
-                out=d_t[:], in0=growths[n][:], scalar=ALPHA, in1=ramps[n][:],
-                op0=ALU.subtract, op1=ALU.min,
+                out=low[:], in0=p_tiles[n][:], scalar=bias_minus[:, c : c + 1], in1=curves[n][:],
+                op0=ALU.max, op1=ALU.min,
             )
-            d_tiles[n] = d_t
+            lows[n] = low
 
         def magnitude(n):
+            c = rounds[n][1]
             size = work.tile([P, HALF], F32, tag="size")
-            nc.scalar.activation(out=size[:], in_=d_tiles[n][:], func=ACT.Abs)
+            nc.scalar.activation(
+                out=size[:], in_=lows[n][:], func=ACT.Abs, bias=bias_plus[:, c : c + 1], scale=1.0
+            )
             sizes[n] = size
+
+        def lift(n):
+            c = rounds[n][1]
+            d_t = held.tile([P, HALF], F32, tag="d_t")
+            if n % LIFT_PERIOD in SCALAR_LIFTS:
+                nc.scalar.activation(
+                    out=d_t[:], in_=lows[n][:], func=ACT.Identity, bias=bias_plus[:, c : c + 1],
+                    scale=1.0,
+                )
+            else:
+                nc.gpsimd.tensor_scalar(
+                    out=d_t[:], in0=lows[n][:], scalar1=1.0,
+                    scalar2=bias_plus[:, c : c + 1], op0=ALU.mult, op1=ALU.add,
+                )
+            d_tiles[n] = d_t
 
         def fold(n):
             q, s = divmod(n, SPLIT)
@@ -367,7 +401,10 @@ def tile_basicemotionpredictions_pa_kernel(tc, h2, gamma, beta, Wh, bh, out):
         def turn(x):
             q, u = divmod(x, SPLIT)
             t, a = divmod(u, CHUNKS_PER_GROUP)
-            d_ps = psum.tile([P, CHUNK_TILES, P], F32, tag="turned")
+            if x >= len(rounds) - SPLIT and x % 2 == 1:
+                d_ps = psum.tile([P, CHUNK_TILES, P], F32, tag="product")
+            else:
+                d_ps = psum_turn.tile([P, CHUNK_TILES, P], F32, tag="turned")
             for i in range(CHUNK_TILES):
                 n = q * SPLIT + a * CHUNK_TILES + i
                 nc.tensor.transpose(d_ps[:, i, :], d_tiles[n][:, t * P : (t + 1) * P], ident[:])
@@ -403,43 +440,39 @@ def tile_basicemotionpredictions_pa_kernel(tc, h2, gamma, beta, Wh, bh, out):
             if 0 <= n < len(rounds):
                 stage(n)
 
-        def ramp_if(n, by_vector):
-            if 0 <= n < len(rounds) and (n % RAMP_PERIOD in VECTOR_RAMPS) == by_vector:
-                ramp(n)
-
         def later(stage, *what):
             return lambda: stage(*what)
 
-        woven = {
-            0: ([later(selu_parts, 1, 1)], [later(selu_plane, 1, 0)]),
-            1: ([later(clamp_by_scalar, 1, 2)], [later(selu_plane, 1, 1)]),
-            2: ([later(selu_parts, 1, 2)], [later(regroup_w, 2)]),
-            3: ([later(clamp_by_scalar, 1, 3)], [later(selu_plane, 1, 2)]),
-            4: ([later(selu_parts, 1, 3)], [later(quantise_w, 2)]),
-            5: ([], [later(selu_plane, 1, 3)]),
-            8: ([], [later(regroup_e, 1)]),
-            11: ([], [later(quantise_e, 1)]),
-            6: ([], [later(regroup_w, 3)]),
-            7: ([], [later(quantise_w, 3)]),
-            9: ([], [later(regroup_w, 4)]),
-            10: ([], [later(quantise_w, 4)]),
-            12: ([], [later(regroup_w, 5)]),
-            13: ([], [later(quantise_w, 5)]),
-        }
+        woven = {}
+
+        def weave(step, engine, stage, *what):
+            woven.setdefault(step, ([], []))[engine].append(later(stage, *what))
+
+        for plane in range(1, PACK):
+            if plane > 1:
+                weave(2 * plane - 3, 0, clamp_by_scalar, 1, plane)
+            weave(2 * plane - 2, 0, selu_parts, 1, plane)
+            weave(2 * plane - 1, 1, selu_plane, 1, plane)
+        weave(7, 1, regroup_e, 1)
+        weave(9, 1, quantise_e, 1)
+        weave(1, 1, quantise_w, 1)
+        for k in range(2, CHUNKS):
+            weave(CHUNK_TILES * k - 7, 1, regroup_w, k)
+            weave(CHUNK_TILES * k - 5, 1, quantise_w, k)
 
         for j in range(-1, len(rounds) + 14):
             at(multiply, j + 1)
-            at(fold, j - 4)
             at(turn, j - 12)
-            at(magnitude, j - 3)
+            at(fold, j - 4)
             at(grow, j)
-            ramp_if(j, False)
+            at(lift, j - 3)
+            at(curve, j)
+            at(magnitude, j - 3)
             for task in woven.get(j, ([], []))[0]:
                 task()
             at(scale_and_store, j - 13)
-            ramp_if(j - 1, True)
             if j >= 12 and (j - 12) % SPLIT == 0 and (j - 12) // SPLIT < len(rounds) // SPLIT:
                 norm((j - 12) // SPLIT)
-            at(combine, j - 2)
+            at(combine, j - 1)
             for task in woven.get(j, ([], []))[1]:
                 task()

@@ -40,6 +40,8 @@ L1_FLOOR = 1e-12 / LAMBDA
 LIFT_PERIOD = 5
 SCALAR_LIFTS = (1, 3)
 Z_FACTORS = (1.0, LAMBDA, -1.0)
+REST_STEP = 5
+GROUP_LEAD = 7
 RUN = 4
 
 FLOPS = 2 * BATCH * HID * COLS
@@ -105,6 +107,7 @@ def tile_basicemotionpredictions_pa_kernel(tc, h2, gamma, beta, Wh, bh, out):
         w_codes = keep.tile([P, COLS], U32, align_bytes=64)
         w_scales = keep.tile([P, COLS], U8, align_bytes=64)
         w_grouped = {}
+        w_grouped_all = {}
 
         def regroup_w(k, by_scalar=False):
             g, a = divmod(k, CHUNKS_PER_GROUP)
@@ -122,6 +125,24 @@ def tile_basicemotionpredictions_pa_kernel(tc, h2, gamma, beta, Wh, bh, out):
             else:
                 nc.vector.tensor_copy(out=grouped[:].rearrange("p s n i j -> p s n j i"), in_=spread)
             w_grouped[k] = grouped
+
+        def regroup_group(g):
+            grouped = w_stage.tile(
+                [P, SPLIT, GROUP_HEADS, SUB, PACK], BF16, align_bytes=64, tag="w_grouped_all"
+            )
+            nc.vector.tensor_copy(
+                out=grouped[:].rearrange("p s n i j -> p s n j i"),
+                in_=w_raw[g][:].rearrange("p n (j s i) -> p s n j i", j=PACK, s=SPLIT),
+            )
+            w_grouped_all[g] = grouped
+
+        def quantise_group(g):
+            cols = slice(g * GROUP_COLS, (g + 1) * GROUP_COLS)
+            nc.vector.quantize_mx(
+                out=w_codes[:, cols].bitcast(FP8X4),
+                scales=w_scales[:, cols],
+                in_=w_grouped_all[g][:].rearrange("p s n i j -> p (s n i j)"),
+            )
 
         def quantise_w(k):
             cols = slice(k * CHUNK_COLS, (k + 1) * CHUNK_COLS)
@@ -215,6 +236,8 @@ def tile_basicemotionpredictions_pa_kernel(tc, h2, gamma, beta, Wh, bh, out):
         e_scales = keep.tile([P, BATCH], U8, align_bytes=64)
 
         e_parts = {}
+        decayed_rest = keep.tile([P, PACK - 1, HALF], F32)
+        linear_rest = keep.tile([P, PACK - 1, HALF], F32)
 
         e_clamped = {}
 
@@ -238,16 +261,22 @@ def tile_basicemotionpredictions_pa_kernel(tc, h2, gamma, beta, Wh, bh, out):
             )
             e_clamped[half, j] = (clamped, -1.0, log_col[:])
 
-        def selu_parts(half, j, first=0, count=HALF):
+        def selu_parts(half, j, first=0, count=HALF, joint=False):
             clamped, sign, bias = e_clamped[half, j]
-            decayed = e_stage.tile([P, count], F32, tag="e_decayed")
+            if joint:
+                decayed = decayed_rest[:, j - 1, :]
+                linear = linear_rest[:, j - 1, :]
+            else:
+                decayed_tile = e_stage.tile([P, count], F32, tag="e_decayed")
+                linear_tile = e_stage.tile([P, count], F32, tag="e_linear")
+                decayed = decayed_tile[:]
+                linear = linear_tile[:]
             nc.scalar.activation(
-                out=decayed[:], in_=clamped[:, first : first + count], func=ACT.Exp, scale=sign,
+                out=decayed, in_=clamped[:, first : first + count], func=ACT.Exp, scale=sign,
                 bias=bias,
             )
-            linear = e_stage.tile([P, count], F32, tag="e_linear")
             nc.scalar.activation(
-                out=linear[:], in_=feature(half, j)[:, first : first + count], func=ACT.Relu,
+                out=linear, in_=feature(half, j)[:, first : first + count], func=ACT.Relu,
                 scale=scale2[:, 1, j : j + 1], bias=offset2[:, 1, j : j + 1],
             )
             e_parts[half, j, first] = (decayed, linear)
@@ -256,8 +285,14 @@ def tile_basicemotionpredictions_pa_kernel(tc, h2, gamma, beta, Wh, bh, out):
             rows = slice(half * HALF + first, half * HALF + first + count)
             decayed, linear = e_parts[half, j, first]
             nc.vector.scalar_tensor_tensor(
-                out=e_planes[:, j, rows], in0=decayed[:], scalar=LAMBDA * ALPHA, in1=linear[:],
+                out=e_planes[:, j, rows], in0=decayed, scalar=LAMBDA * ALPHA, in1=linear,
                 op0=ALU.subtract, op1=ALU.add,
+            )
+
+        def selu_rest():
+            nc.vector.scalar_tensor_tensor(
+                out=e_planes[:, 1:PACK, HALF : 2 * HALF], in0=decayed_rest[:], scalar=LAMBDA * ALPHA,
+                in1=linear_rest[:], op0=ALU.subtract, op1=ALU.add,
             )
 
         def regroup_e(half, first=0, count=HALF):
@@ -393,7 +428,11 @@ def tile_basicemotionpredictions_pa_kernel(tc, h2, gamma, beta, Wh, bh, out):
                 axis=mybir.AxisListType.X, op=ALU.add,
             )
             divisor = small.tile([P, TILES_PER_HALF * GROUP_HEADS], F32, tag="divisor")
-            nc.vector.tensor_scalar_max(divisor[:], total[:], L1_FLOOR)
+            unused = small.tile([P, 1], F32, tag="unused")
+            nc.vector.tensor_scalar(
+                out=divisor[:], in0=total[:], scalar1=L1_FLOOR, scalar2=None, op0=ALU.max, op1=ALU.add,
+                accum_out=unused[:],
+            )
             inverse = small.tile([P, TILES_PER_HALF, GROUP_HEADS], F32, tag="inverse")
             nc.vector.reciprocal(out=inverse[:].rearrange("p t n -> p (t n)"), in_=divisor[:])
             inverses[q] = inverse
@@ -451,14 +490,14 @@ def tile_basicemotionpredictions_pa_kernel(tc, h2, gamma, beta, Wh, bh, out):
         for plane in range(1, PACK):
             if plane > 1:
                 weave(2 * plane - 3, 0, clamp_by_scalar, 1, plane)
-            weave(2 * plane - 2, 0, selu_parts, 1, plane)
-            weave(2 * plane - 1, 1, selu_plane, 1, plane)
+            weave(2 * plane - 2, 0, selu_parts, 1, plane, 0, HALF, True)
+        weave(REST_STEP, 1, selu_rest)
         weave(7, 1, regroup_e, 1)
         weave(9, 1, quantise_e, 1)
         weave(1, 1, quantise_w, 1)
-        for k in range(2, CHUNKS):
-            weave(CHUNK_TILES * k - 7, 1, regroup_w, k)
-            weave(CHUNK_TILES * k - 5, 1, quantise_w, k)
+        for g in range(1, HEAD_GROUPS):
+            weave(SPLIT * g - GROUP_LEAD, 1, regroup_group, g)
+            weave(SPLIT * g - GROUP_LEAD + 2, 1, quantise_group, g)
 
         for j in range(-1, len(rounds) + 14):
             at(multiply, j + 1)

@@ -71,19 +71,14 @@ def tile_basicemotionpredictions_pa_kernel(tc, h2, gamma, beta, Wh, bh, out):
             nc.sync.dma_start(out=h2_sb[:, two, :], in_=h2_rows[:, two, :])
 
         gamma_bf = keep.tile([P, PACK], BF16)
-        nc.scalar.dma_start(out=gamma_bf[:], in_=gamma.rearrange("(p j) -> p j", j=PACK))
+        nc.sync.dma_start(out=gamma_bf[:], in_=gamma.rearrange("(p j) -> p j", j=PACK))
         beta_bf = keep.tile([P, PACK], BF16)
-        nc.scalar.dma_start(out=beta_bf[:], in_=beta.rearrange("(p j) -> p j", j=PACK))
+        nc.sync.dma_start(out=beta_bf[:], in_=beta.rearrange("(p j) -> p j", j=PACK))
         bias_rows = keep.tile([P, P], BF16)
         nc.vector.memset(bias_rows[:], 0.0)
         bh_tiles = bh.rearrange("h g e -> (h g) e").rearrange(
             "(a n) (s i) -> a s n i", a=HEAD_GROUPS, i=SUB
         )
-        for g in range(HEAD_GROUPS):
-            nc.scalar.dma_start(
-                out=bias_rows[g * SPLIT : (g + 1) * SPLIT, :].rearrange("s (n i) -> s n i", i=SUB),
-                in_=bh_tiles[g],
-            )
 
         w_rows = Wh.rearrange("h g (p j) e -> p (h g) (j e)", j=PACK)
         w_raw = []
@@ -96,6 +91,14 @@ def tile_basicemotionpredictions_pa_kernel(tc, h2, gamma, beta, Wh, bh, out):
                     in_=w_rows[:, g * GROUP_HEADS + some.start : g * GROUP_HEADS + some.stop, :],
                 )
             w_raw.append(raw)
+            if g == 0:
+                for group in range(HEAD_GROUPS):
+                    nc.sync.dma_start(
+                        out=bias_rows[group * SPLIT : (group + 1) * SPLIT, :].rearrange(
+                            "s (n i) -> s n i", i=SUB
+                        ),
+                        in_=bh_tiles[group],
+                    )
 
         ident = keep.tile([P, P], F32)
         make_identity(nc, ident[:])
@@ -166,6 +169,8 @@ def tile_basicemotionpredictions_pa_kernel(tc, h2, gamma, beta, Wh, bh, out):
         gain2 = keep.tile([P, len(Z_FACTORS), PACK], F32)
         shift2 = keep.tile([P, len(Z_FACTORS), PACK], F32)
         log_col = keep.tile([P, 1], F32)
+        log_alpha = keep.tile([P, 1], F32)
+        minus_alpha = keep.tile([P, 1], F32)
         bias_rows_f = keep.tile([P, P], F32)
         for half in range(2):
             for t in range(half * TILES_PER_HALF, (half + 1) * TILES_PER_HALF):
@@ -184,9 +189,8 @@ def tile_basicemotionpredictions_pa_kernel(tc, h2, gamma, beta, Wh, bh, out):
                     nc.vector.tensor_scalar_mul(gain2[:, row, :], gamma_bf[:], factor)
                     nc.vector.tensor_scalar_mul(shift2[:, row, :], beta_bf[:], factor)
                 nc.vector.tensor_scalar_mul(log_col[:], one_col[:], math.log(LAMBDA * ALPHA))
-                nc.vector.tensor_copy(out=bias_rows_f[:], in_=bias_rows[:])
-        bias_ps = psum.tile([P, P], F32, tag="product")
-        nc.tensor.transpose(bias_ps[:], bias_rows_f[:], ident[:])
+                nc.vector.tensor_scalar_mul(log_alpha[:], one_col[:], math.log(ALPHA))
+                nc.vector.tensor_scalar_mul(minus_alpha[:], one_col[:], -ALPHA)
 
         regroup_w(0, by_scalar=True)
 
@@ -200,17 +204,9 @@ def tile_basicemotionpredictions_pa_kernel(tc, h2, gamma, beta, Wh, bh, out):
         nc.vector.tensor_scalar_add(var_eps[:], mean_var[:, :, 1], BN_EPS)
         rstd = keep.tile([P, PACK], F32)
         nc.gpsimd.tensor_tensor(out=rstd[:], in0=var_eps[:], in1=neg_half[:], op=ALU.pow)
-        bias_plus = keep.tile([P, COL_TILES], F32)
-        nc.vector.tensor_copy(out=bias_plus[:], in_=bias_ps[:, 0:COL_TILES])
-        bias_minus = keep.tile([P, COL_TILES], F32)
-        nc.vector.tensor_scalar_mul(bias_minus[:], bias_ps[:, 0:COL_TILES], -1.0)
-        bias_drop = keep.tile([P, COL_TILES], F32)
-        nc.vector.tensor_scalar(
-            out=bias_drop[:], in0=bias_ps[:, 0:COL_TILES], scalar1=-1.0, scalar2=-ALPHA,
-            op0=ALU.mult, op1=ALU.add,
-        )
-        bias_log = keep.tile([P, COL_TILES], F32)
-        nc.vector.tensor_scalar_add(bias_log[:], bias_ps[:, 0:COL_TILES], math.log(ALPHA))
+        nc.gpsimd.tensor_copy(out=bias_rows_f[:], in_=bias_rows[:])
+        bias_ps = psum.tile([P, P], F32, tag="product")
+        nc.tensor.transpose(bias_ps[:], bias_rows_f[:], ident[:])
         scale2 = keep.tile([P, len(Z_FACTORS), PACK], F32)
         nc.vector.tensor_tensor(
             out=scale2[:],
@@ -334,6 +330,18 @@ def tile_basicemotionpredictions_pa_kernel(tc, h2, gamma, beta, Wh, bh, out):
         selu_plane(1, 0)
         quantise_e(0, HALF // 2, HALF // 2)
         regroup_w(1)
+        bias_plus = keep.tile([P, COL_TILES], F32)
+        nc.scalar.copy(out=bias_plus[:], in_=bias_ps[:, 0:COL_TILES])
+        bias_log = keep.tile([P, COL_TILES], F32)
+        nc.scalar.activation(
+            out=bias_log[:], in_=bias_ps[:, 0:COL_TILES], func=ACT.Identity, bias=log_alpha[:], scale=1.0
+        )
+        bias_drop = keep.tile([P, COL_TILES], F32)
+        nc.scalar.activation(
+            out=bias_drop[:], in_=bias_ps[:, 0:COL_TILES], func=ACT.Identity, bias=minus_alpha[:], scale=-1.0
+        )
+        bias_minus = keep.tile([P, COL_TILES], F32)
+        nc.scalar.mul(bias_minus[:], bias_ps[:, 0:COL_TILES], -1.0)
 
         out_rows = out.rearrange("(p t) h g e -> p t (h g e)", t=BATCH_TILES)
         rounds = [(half, c) for half in range(2) for c in range(COL_TILES)]

@@ -172,6 +172,9 @@ def tile_basicemotionpredictions_pa_kernel(tc, h2, gamma, beta, Wh, bh, out):
         log_alpha = keep.tile([P, 1], F32)
         minus_alpha = keep.tile([P, 1], F32)
         bias_rows_f = keep.tile([P, P], F32)
+        nc.vector.tensor_scalar_mul(log_col[:], one_col[:], math.log(LAMBDA * ALPHA))
+        nc.vector.tensor_scalar_mul(log_alpha[:], one_col[:], math.log(ALPHA))
+        nc.vector.tensor_scalar_mul(minus_alpha[:], one_col[:], -ALPHA)
         for half in range(2):
             for t in range(half * TILES_PER_HALF, (half + 1) * TILES_PER_HALF):
                 words = h2_sb[:, t, :].bitcast(F32).rearrange("p (q u) -> p u q", u=2)
@@ -188,9 +191,6 @@ def tile_basicemotionpredictions_pa_kernel(tc, h2, gamma, beta, Wh, bh, out):
                 for row, factor in enumerate(Z_FACTORS):
                     nc.vector.tensor_scalar_mul(gain2[:, row, :], gamma_bf[:], factor)
                     nc.vector.tensor_scalar_mul(shift2[:, row, :], beta_bf[:], factor)
-                nc.vector.tensor_scalar_mul(log_col[:], one_col[:], math.log(LAMBDA * ALPHA))
-                nc.vector.tensor_scalar_mul(log_alpha[:], one_col[:], math.log(ALPHA))
-                nc.vector.tensor_scalar_mul(minus_alpha[:], one_col[:], -ALPHA)
 
         regroup_w(0, by_scalar=True)
 
@@ -327,8 +327,8 @@ def tile_basicemotionpredictions_pa_kernel(tc, h2, gamma, beta, Wh, bh, out):
         regroup_e(0, HALF // 2, HALF // 2)
         selu_parts(1, 0)
         clamp_by_scalar(1, 1)
-        selu_plane(1, 0)
         quantise_e(0, HALF // 2, HALF // 2)
+        selu_plane(1, 0)
         regroup_w(1)
         bias_plus = keep.tile([P, COL_TILES], F32)
         nc.scalar.copy(out=bias_plus[:], in_=bias_ps[:, 0:COL_TILES])
@@ -512,7 +512,7 @@ def tile_basicemotionpredictions_pa_kernel(tc, h2, gamma, beta, Wh, bh, out):
             at(turn, j - 12)
             at(fold, j - 4)
             at(grow, j)
-            at(lift, j - 3)
+            at(lift, j - 4)
             at(curve, j)
             at(magnitude, j - 3)
             for task in woven.get(j, ([], []))[0]:

@@ -106,6 +106,8 @@ def tile_basicemotionpredictions_pa_kernel(tc, h2, gamma, beta, Wh, bh, out):
         nc.vector.memset(one_col[:], 1.0)
         neg_half = keep.tile([P, PACK], F32)
         nc.vector.memset(neg_half[:], -0.5)
+        warm = keep.tile([P, 1], F32)
+        nc.scalar.activation(out=warm[:], in_=one_col[:], func=ACT.Exp)
 
         w_codes = keep.tile([P, COLS], U32, align_bytes=64)
         w_scales = keep.tile([P, COLS], U8, align_bytes=64)
@@ -189,8 +191,11 @@ def tile_basicemotionpredictions_pa_kernel(tc, h2, gamma, beta, Wh, bh, out):
                     )
             if half == 0:
                 for row, factor in enumerate(Z_FACTORS):
-                    nc.vector.tensor_scalar_mul(gain2[:, row, :], gamma_bf[:], factor)
-                    nc.vector.tensor_scalar_mul(shift2[:, row, :], beta_bf[:], factor)
+                    for multiple, small_input in ((gain2, gamma_bf), (shift2, beta_bf)):
+                        nc.gpsimd.tensor_scalar(
+                            out=multiple[:, row, :], in0=small_input[:], scalar1=factor, scalar2=0.0,
+                            op0=ALU.mult, op1=ALU.add,
+                        )
 
         regroup_w(0, by_scalar=True)
 
@@ -207,18 +212,25 @@ def tile_basicemotionpredictions_pa_kernel(tc, h2, gamma, beta, Wh, bh, out):
         nc.gpsimd.tensor_copy(out=bias_rows_f[:], in_=bias_rows[:])
         bias_ps = psum.tile([P, P], F32, tag="product")
         nc.tensor.transpose(bias_ps[:], bias_rows_f[:], ident[:])
-        scale2 = keep.tile([P, len(Z_FACTORS), PACK], F32)
+        mean_gain = keep.tile([P, len(Z_FACTORS), PACK], F32)
         nc.vector.tensor_tensor(
-            out=scale2[:],
+            out=mean_gain[:],
             in0=gain2[:],
-            in1=rstd[:].unsqueeze(1).to_broadcast([P, len(Z_FACTORS), PACK]),
+            in1=mean_var[:, :, 0].unsqueeze(1).to_broadcast([P, len(Z_FACTORS), PACK]),
             op=ALU.mult,
         )
         mean_scaled = keep.tile([P, len(Z_FACTORS), PACK], F32)
         nc.vector.tensor_tensor(
             out=mean_scaled[:],
-            in0=scale2[:],
-            in1=mean_var[:, :, 0].unsqueeze(1).to_broadcast([P, len(Z_FACTORS), PACK]),
+            in0=mean_gain[:],
+            in1=rstd[:].unsqueeze(1).to_broadcast([P, len(Z_FACTORS), PACK]),
+            op=ALU.mult,
+        )
+        scale2 = keep.tile([P, len(Z_FACTORS), PACK], F32)
+        nc.vector.tensor_tensor(
+            out=scale2[:],
+            in0=gain2[:],
+            in1=rstd[:].unsqueeze(1).to_broadcast([P, len(Z_FACTORS), PACK]),
             op=ALU.mult,
         )
         offset2 = keep.tile([P, len(Z_FACTORS), PACK], F32)

@@ -37,11 +37,37 @@ BN_EPS = 1e-5
 ALPHA = 1.6732632423543772
 LAMBDA = 1.0507009873554805
 L1_FLOOR = 1e-12 / LAMBDA
-LIFT_PERIOD = 5
-SCALAR_LIFTS = (1, 3)
+LIFT_PERIOD = 3
+SCALAR_LIFTS = (1,)
 Z_FACTORS = (1.0, LAMBDA, -1.0)
-REST_STEP = 5
+GROUPED_STEP = 5
+QE_STEP = 6
+PAIR = 1
+PRE1 = 6
+RATE1 = 1
+G1_PRE = True
+Q1_STEP = 1
+QG1_STEP = 3
+ARS = False
+HEAD = 2
+QW = 3
+EARLY1 = False
+CL1_V = False
+E1_FIRST = 0
+E1_EVERY = 1
+LIFT_FROM = 8
+W1_BY = "g"
+G1_BY = "v"
+G2_BY = "v"
+G1_STEP = 1
+G2_STEP = 8
+CLIP_LIFT = 0
 GROUP_LEAD = 7
+TURN = 12
+FOLD = 4
+LIFT = 4
+ABS = 3
+COMB = 1
 RUN = 4
 
 FLOPS = 2 * BATCH * HID * COLS
@@ -55,6 +81,11 @@ def tile_basicemotionpredictions_pa_kernel(tc, h2, gamma, beta, Wh, bh, out):
         w_stage = ctx.enter_context(tc.tile_pool(name="w_stage", bufs=2))
         e_stage = ctx.enter_context(tc.tile_pool(name="e_stage", bufs=4))
         work = ctx.enter_context(tc.tile_pool(name="work", bufs=4))
+        joint_pool = {
+            HALF // HEAD: ctx.enter_context(tc.tile_pool(name="joint_pieces", bufs=2)),
+            HALF: ctx.enter_context(tc.tile_pool(name="joint_half", bufs=1)),
+        }
+        grow_pool = ctx.enter_context(tc.tile_pool(name="grow_pool", bufs=3))
         held = ctx.enter_context(tc.tile_pool(name="held", bufs=20))
         small = ctx.enter_context(tc.tile_pool(name="small", bufs=2))
         out_stage = ctx.enter_context(tc.tile_pool(name="out_stage", bufs=4))
@@ -107,14 +138,14 @@ def tile_basicemotionpredictions_pa_kernel(tc, h2, gamma, beta, Wh, bh, out):
         neg_half = keep.tile([P, PACK], F32)
         nc.vector.memset(neg_half[:], -0.5)
         warm = keep.tile([P, 1], F32)
-        nc.scalar.activation(out=warm[:], in_=one_col[:], func=ACT.Exp)
+        nc.scalar.activation(out=warm[:], in_=one_col[:], func=ACT.Abs_reciprocal_sqrt if ARS else ACT.Exp)
 
         w_codes = keep.tile([P, COLS], U32, align_bytes=64)
         w_scales = keep.tile([P, COLS], U8, align_bytes=64)
         w_grouped = {}
         w_grouped_all = {}
 
-        def regroup_w(k, by_scalar=False):
+        def regroup_w(k, by_scalar=False, by_g=False):
             g, a = divmod(k, CHUNKS_PER_GROUP)
             grouped = w_stage.tile(
                 [P, CHUNK_TILES, GROUP_HEADS, SUB, PACK], BF16, align_bytes=64, tag="w_grouped"
@@ -122,7 +153,13 @@ def tile_basicemotionpredictions_pa_kernel(tc, h2, gamma, beta, Wh, bh, out):
             spread = w_raw[g][:].rearrange(
                 "p n (j a s i) -> p a s n j i", j=PACK, a=CHUNKS_PER_GROUP, s=CHUNK_TILES
             )[:, a]
-            if by_scalar:
+            if by_g:
+                for s in range(CHUNK_TILES):
+                    nc.gpsimd.tensor_scalar(
+                        out=grouped[:, s], in0=spread[:, s].rearrange("p n j i -> p n i j"),
+                        scalar1=1.0, scalar2=0.0, op0=ALU.mult, op1=ALU.add,
+                    )
+            elif by_scalar:
                 for s in range(CHUNK_TILES):
                     nc.scalar.copy(
                         out=grouped[:, s].rearrange("p n i j -> p n j i"), in_=spread[:, s]
@@ -131,15 +168,25 @@ def tile_basicemotionpredictions_pa_kernel(tc, h2, gamma, beta, Wh, bh, out):
                 nc.vector.tensor_copy(out=grouped[:].rearrange("p s n i j -> p s n j i"), in_=spread)
             w_grouped[k] = grouped
 
-        def regroup_group(g):
-            grouped = w_stage.tile(
-                [P, SPLIT, GROUP_HEADS, SUB, PACK], BF16, align_bytes=64, tag="w_grouped_all"
-            )
-            nc.vector.tensor_copy(
-                out=grouped[:].rearrange("p s n i j -> p s n j i"),
-                in_=w_raw[g][:].rearrange("p n (j s i) -> p s n j i", j=PACK, s=SPLIT),
-            )
-            w_grouped_all[g] = grouped
+        def regroup_group(g, engine, first=0, count=SPLIT):
+            if first == 0:
+                w_grouped_all[g] = w_stage.tile(
+                    [P, SPLIT, GROUP_HEADS, SUB, PACK], BF16, name="grouped_all%d" % g, align_bytes=64, tag="w_grouped_all"
+                )
+            spread = w_raw[g][:].rearrange("p n (j s i) -> p s n j i", j=PACK, s=SPLIT)
+            for s in range(first, first + count):
+                if engine == "g":
+                    nc.gpsimd.tensor_scalar(
+                        out=w_grouped_all[g][:, s], in0=spread[:, s].rearrange("p n j i -> p n i j"),
+                        scalar1=1.0, scalar2=0.0, op0=ALU.mult, op1=ALU.add,
+                    )
+                elif engine == "s":
+                    nc.scalar.copy(out=w_grouped_all[g][:, s].rearrange("p n i j -> p n j i"), in_=spread[:, s])
+            if engine == "v":
+                nc.vector.tensor_copy(
+                    out=w_grouped_all[g][:, first : first + count].rearrange("p s n i j -> p s n j i"),
+                    in_=spread[:, first : first + count],
+                )
 
         def quantise_group(g):
             cols = slice(g * GROUP_COLS, (g + 1) * GROUP_COLS)
@@ -208,8 +255,18 @@ def tile_basicemotionpredictions_pa_kernel(tc, h2, gamma, beta, Wh, bh, out):
         var_eps = keep.tile([P, PACK], F32)
         nc.vector.tensor_scalar_add(var_eps[:], mean_var[:, :, 1], BN_EPS)
         rstd = keep.tile([P, PACK], F32)
-        nc.gpsimd.tensor_tensor(out=rstd[:], in0=var_eps[:], in1=neg_half[:], op=ALU.pow)
+        if ARS:
+            nc.scalar.activation(out=rstd[:], in_=var_eps[:], func=ACT.Abs_reciprocal_sqrt)
+            nc.scalar.activation(out=warm[:], in_=one_col[:], func=ACT.Exp)
+        else:
+            nc.gpsimd.tensor_tensor(out=rstd[:], in0=var_eps[:], in1=neg_half[:], op=ALU.pow)
+        if W1_BY == "g":
+            regroup_w(1, by_g=True)
         nc.gpsimd.tensor_copy(out=bias_rows_f[:], in_=bias_rows[:])
+        if G1_BY == "g":
+            regroup_group(1, "g")
+        if G1_BY == "gv":
+            regroup_group(1, "g", 0, 4)
         bias_ps = psum.tile([P, P], F32, tag="product")
         nc.tensor.transpose(bias_ps[:], bias_rows_f[:], ident[:])
         mean_gain = keep.tile([P, len(Z_FACTORS), PACK], F32)
@@ -244,8 +301,7 @@ def tile_basicemotionpredictions_pa_kernel(tc, h2, gamma, beta, Wh, bh, out):
         e_scales = keep.tile([P, BATCH], U8, align_bytes=64)
 
         e_parts = {}
-        decayed_rest = keep.tile([P, PACK - 1, HALF], F32)
-        linear_rest = keep.tile([P, PACK - 1, HALF], F32)
+        joint_parts = {}
 
         e_clamped = {}
 
@@ -269,24 +325,33 @@ def tile_basicemotionpredictions_pa_kernel(tc, h2, gamma, beta, Wh, bh, out):
             )
             e_clamped[half, j] = (clamped, -1.0, log_col[:])
 
-        def selu_parts(half, j, first=0, count=HALF, joint=False):
+        CL1 = clamp_by_vector if CL1_V else clamp_by_scalar
+
+        def selu_parts(half, j, first=0, count=HALF, joint=False, what="both"):
             clamped, sign, bias = e_clamped[half, j]
             if joint:
-                decayed = decayed_rest[:, j - 1, :]
-                linear = linear_rest[:, j - 1, :]
+                if (half, first) not in joint_parts:
+                    joint_parts[half, first] = (
+                        joint_pool[count].tile([P, PACK, count], F32, name="decayed_all", tag="decayed"),
+                        joint_pool[count].tile([P, PACK, count], F32, name="linear_all", tag="linear"),
+                    )
+                decayed = joint_parts[half, first][0][:, j, :]
+                linear = joint_parts[half, first][1][:, j, :]
             else:
                 decayed_tile = e_stage.tile([P, count], F32, tag="e_decayed")
                 linear_tile = e_stage.tile([P, count], F32, tag="e_linear")
                 decayed = decayed_tile[:]
                 linear = linear_tile[:]
-            nc.scalar.activation(
-                out=decayed, in_=clamped[:, first : first + count], func=ACT.Exp, scale=sign,
-                bias=bias,
-            )
-            nc.scalar.activation(
-                out=linear, in_=feature(half, j)[:, first : first + count], func=ACT.Relu,
-                scale=scale2[:, 1, j : j + 1], bias=offset2[:, 1, j : j + 1],
-            )
+            if what != "relu":
+                nc.scalar.activation(
+                    out=decayed, in_=clamped[:, first : first + count], func=ACT.Exp, scale=sign,
+                    bias=bias,
+                )
+            if what != "exp":
+                nc.scalar.activation(
+                    out=linear, in_=feature(half, j)[:, first : first + count], func=ACT.Relu,
+                    scale=scale2[:, 1, j : j + 1], bias=offset2[:, 1, j : j + 1],
+                )
             e_parts[half, j, first] = (decayed, linear)
 
         def selu_plane(half, j, first=0, count=HALF):
@@ -297,10 +362,12 @@ def tile_basicemotionpredictions_pa_kernel(tc, h2, gamma, beta, Wh, bh, out):
                 op0=ALU.subtract, op1=ALU.add,
             )
 
-        def selu_rest():
+        def selu_grouped(half=1, first=0, count=HALF):
+            rows = slice(half * HALF + first, half * HALF + first + count)
             nc.vector.scalar_tensor_tensor(
-                out=e_planes[:, 1:PACK, HALF : 2 * HALF], in0=decayed_rest[:], scalar=LAMBDA * ALPHA,
-                in1=linear_rest[:], op0=ALU.subtract, op1=ALU.add,
+                out=e_grouped[:, rows, :], in0=joint_parts[half, first][0][:].rearrange("p j b -> p b j"),
+                scalar=LAMBDA * ALPHA, in1=joint_parts[half, first][1][:].rearrange("p j b -> p b j"),
+                op0=ALU.subtract, op1=ALU.add,
             )
 
         def regroup_e(half, first=0, count=HALF):
@@ -318,39 +385,62 @@ def tile_basicemotionpredictions_pa_kernel(tc, h2, gamma, beta, Wh, bh, out):
                 in_=e_grouped[:, rows, :].rearrange("p b j -> p (b j)"),
             )
 
-        clamp_by_vector(0, 0)
-        clamp_by_vector(0, 1)
-        selu_parts(0, 0)
-        quantise_w(0)
-        clamp_by_vector(0, 2)
-        selu_parts(0, 1)
-        selu_plane(0, 0)
-        clamp_by_vector(0, 3)
-        selu_parts(0, 2)
-        selu_plane(0, 1)
-        selu_parts(0, 3, 0, HALF // 2)
-        selu_plane(0, 2)
-        selu_parts(0, 3, HALF // 2, HALF // 2)
-        selu_plane(0, 3, 0, HALF // 2)
-        regroup_e(0, 0, HALF // 2)
-        clamp_by_scalar(1, 0)
-        selu_plane(0, 3, HALF // 2, HALF // 2)
-        quantise_e(0, 0, HALF // 2)
-        regroup_e(0, HALF // 2, HALF // 2)
-        selu_parts(1, 0)
-        clamp_by_scalar(1, 1)
-        quantise_e(0, HALF // 2, HALF // 2)
-        selu_plane(1, 0)
-        regroup_w(1)
-        bias_plus = keep.tile([P, COL_TILES], F32)
-        nc.scalar.copy(out=bias_plus[:], in_=bias_ps[:, 0:COL_TILES])
+        half1 = []
+        for j in range(PACK):
+            if not CL1_V:
+                half1.append(lambda j=j: clamp_by_scalar(1, j))
+            else:
+                half1.append(lambda j=j: clamp_by_vector(1, j))
+            half1.append(lambda j=j: selu_parts(1, j, 0, HALF, True, "exp"))
+            half1.append(lambda j=j: selu_parts(1, j, 0, HALF, True, "relu"))
+        if HEAD == 0:
+            clamp_by_vector(0, 0)
+            clamp_by_vector(0, 1)
+            selu_parts(0, 0)
+            quantise_w(0)
+            clamp_by_vector(0, 2)
+            selu_parts(0, 1)
+            selu_plane(0, 0)
+            clamp_by_vector(0, 3)
+            selu_parts(0, 2)
+            selu_plane(0, 1)
+            selu_parts(0, 3, 0, HALF // 2)
+            selu_plane(0, 2)
+            selu_parts(0, 3, HALF // 2, HALF // 2)
+            selu_plane(0, 3, 0, HALF // 2)
+            regroup_e(0, 0, HALF // 2)
+            CL1(1, 0)
+            selu_plane(0, 3, HALF // 2, HALF // 2)
+            quantise_e(0, 0, HALF // 2)
+            regroup_e(0, HALF // 2, HALF // 2)
+            selu_parts(1, 0, 0, HALF, True)
+            CL1(1, 1)
+            quantise_e(0, HALF // 2, HALF // 2)
+        else:
+            nq = HEAD
+            w = HALF // nq
+            for j in range(PACK):
+                clamp_by_vector(0, j)
+                if j == QW:
+                    quantise_w(0)
+            for r in range(nq):
+                for j in range(PACK):
+                    selu_parts(0, j, r * w, w, True)
+                selu_grouped(0, r * w, w)
+                quantise_e(0, r * w, w)
+            for task in half1[:PRE1]:
+                task()
+            if G1_PRE:
+                regroup_group(1, "v")
+        if W1_BY == "v":
+            regroup_w(1)
+        bias_less = keep.tile([P, COL_TILES], F32)
+        nc.scalar.activation(
+            out=bias_less[:], in_=bias_ps[:, 0:COL_TILES], func=ACT.Identity, bias=minus_alpha[:], scale=1.0
+        )
         bias_log = keep.tile([P, COL_TILES], F32)
         nc.scalar.activation(
             out=bias_log[:], in_=bias_ps[:, 0:COL_TILES], func=ACT.Identity, bias=log_alpha[:], scale=1.0
-        )
-        bias_drop = keep.tile([P, COL_TILES], F32)
-        nc.scalar.activation(
-            out=bias_drop[:], in_=bias_ps[:, 0:COL_TILES], func=ACT.Identity, bias=minus_alpha[:], scale=-1.0
         )
         bias_minus = keep.tile([P, COL_TILES], F32)
         nc.scalar.mul(bias_minus[:], bias_ps[:, 0:COL_TILES], -1.0)
@@ -383,27 +473,27 @@ def tile_basicemotionpredictions_pa_kernel(tc, h2, gamma, beta, Wh, bh, out):
 
         def grow(n):
             c = rounds[n][1]
-            grown = work.tile([P, HALF], F32, tag="grown")
+            if n % PAIR == 0:
+                growths[n // PAIR] = grow_pool.tile([P, PAIR, HALF], F32, name="grown", tag="grown")
             nc.scalar.activation(
-                out=grown[:], in_=p_tiles[n][:], func=ACT.Exp, bias=bias_log[:, c : c + 1], scale=1.0
+                out=growths[n // PAIR][:, n % PAIR, :], in_=p_tiles[n][:], func=ACT.Exp, bias=bias_log[:, c : c + 1], scale=1.0
             )
-            growths[n] = grown
 
-        def curve(n):
-            c = rounds[n][1]
-            curved = work.tile([P, HALF], F32, tag="curved")
+        def clip(m):
+            clipped = grow_pool.tile([P, PAIR, HALF], F32, tag="clipped")
             nc.gpsimd.tensor_scalar(
-                out=curved[:], in0=growths[n][:], scalar1=1.0,
-                scalar2=bias_drop[:, c : c + 1], op0=ALU.mult, op1=ALU.add,
+                out=clipped[:].rearrange("p r b -> p (r b)"),
+                in0=growths[m][:].rearrange("p r b -> p (r b)"), scalar1=ALPHA, scalar2=0.0,
+                op0=ALU.min, op1=ALU.max,
             )
-            curves[n] = curved
+            curves[m] = clipped
 
         def combine(n):
             c = rounds[n][1]
             low = work.tile([P, HALF], F32, tag="low")
             nc.vector.scalar_tensor_tensor(
-                out=low[:], in0=p_tiles[n][:], scalar=bias_minus[:, c : c + 1], in1=curves[n][:],
-                op0=ALU.max, op1=ALU.min,
+                out=low[:], in0=p_tiles[n][:], scalar=bias_minus[:, c : c + 1], in1=curves[n // PAIR][:, n % PAIR, :],
+                op0=ALU.max, op1=ALU.add,
             )
             lows[n] = low
 
@@ -411,22 +501,22 @@ def tile_basicemotionpredictions_pa_kernel(tc, h2, gamma, beta, Wh, bh, out):
             c = rounds[n][1]
             size = work.tile([P, HALF], F32, tag="size")
             nc.scalar.activation(
-                out=size[:], in_=lows[n][:], func=ACT.Abs, bias=bias_plus[:, c : c + 1], scale=1.0
+                out=size[:], in_=lows[n][:], func=ACT.Abs, bias=bias_less[:, c : c + 1], scale=1.0
             )
             sizes[n] = size
 
         def lift(n):
             c = rounds[n][1]
             d_t = held.tile([P, HALF], F32, tag="d_t")
-            if n % LIFT_PERIOD in SCALAR_LIFTS:
+            if n >= LIFT_FROM and n % LIFT_PERIOD in SCALAR_LIFTS:
                 nc.scalar.activation(
-                    out=d_t[:], in_=lows[n][:], func=ACT.Identity, bias=bias_plus[:, c : c + 1],
+                    out=d_t[:], in_=lows[n][:], func=ACT.Identity, bias=bias_less[:, c : c + 1],
                     scale=1.0,
                 )
             else:
                 nc.gpsimd.tensor_scalar(
                     out=d_t[:], in0=lows[n][:], scalar1=1.0,
-                    scalar2=bias_plus[:, c : c + 1], op0=ALU.mult, op1=ALU.add,
+                    scalar2=bias_less[:, c : c + 1], op0=ALU.mult, op1=ALU.add,
                 )
             d_tiles[n] = d_t
 
@@ -507,31 +597,37 @@ def tile_basicemotionpredictions_pa_kernel(tc, h2, gamma, beta, Wh, bh, out):
         def weave(step, engine, stage, *what):
             woven.setdefault(step, ([], []))[engine].append(later(stage, *what))
 
-        for plane in range(1, PACK):
-            if plane > 1:
-                weave(2 * plane - 3, 0, clamp_by_scalar, 1, plane)
-            weave(2 * plane - 2, 0, selu_parts, 1, plane, 0, HALF, True)
-        weave(REST_STEP, 1, selu_rest)
-        weave(7, 1, regroup_e, 1)
-        weave(9, 1, quantise_e, 1)
-        weave(1, 1, quantise_w, 1)
-        for g in range(1, HEAD_GROUPS):
-            weave(SPLIT * g - GROUP_LEAD, 1, regroup_group, g)
-            weave(SPLIT * g - GROUP_LEAD + 2, 1, quantise_group, g)
+        for i, task in enumerate(half1[PRE1:]):
+            woven.setdefault(E1_FIRST + i // RATE1, ([], []))[0 if i % 3 or not CL1_V else 1].append(task)
+        weave(GROUPED_STEP, 1, selu_grouped)
+        weave(QE_STEP, 1, quantise_e, 1)
+        weave(Q1_STEP, 1, quantise_w, 1)
+        if G1_BY == "v" and not G1_PRE:
+            weave(G1_STEP, 1, regroup_group, 1, "v")
+        if G1_BY == "gv":
+            weave(G1_STEP, 1, regroup_group, 1, "v", 4, 4)
+        weave(QG1_STEP, 1, quantise_group, 1)
+        if G2_BY == "v":
+            weave(G2_STEP, 1, regroup_group, 2, "v")
+        else:
+            for s in range(SPLIT):
+                weave(G2_STEP + s // 2 - 4, 0, regroup_group, 2, "s", s, 1)
+        weave(G2_STEP + 2, 1, quantise_group, 2)
 
-        for j in range(-1, len(rounds) + 14):
+        for j in range(-1, len(rounds) + TURN + 2):
             at(multiply, j + 1)
-            at(turn, j - 12)
-            at(fold, j - 4)
+            at(turn, j - TURN)
+            at(fold, j - FOLD)
             at(grow, j)
-            at(lift, j - 4)
-            at(curve, j)
-            at(magnitude, j - 3)
+            at(lift, j - LIFT)
+            if j % PAIR == PAIR - 1 and 0 <= j < len(rounds):
+                clip(j // PAIR)
+            at(magnitude, j - ABS)
             for task in woven.get(j, ([], []))[0]:
                 task()
-            at(scale_and_store, j - 13)
-            if j >= 12 and (j - 12) % SPLIT == 0 and (j - 12) // SPLIT < len(rounds) // SPLIT:
-                norm((j - 12) // SPLIT)
-            at(combine, j - 1)
+            at(scale_and_store, j - TURN - 1)
+            if j >= TURN and (j - TURN) % SPLIT == 0 and (j - TURN) // SPLIT < len(rounds) // SPLIT:
+                norm((j - TURN) // SPLIT)
+            at(combine, j - COMB)
             for task in woven.get(j, ([], []))[1]:
                 task()

@@ -43,6 +43,7 @@ Z_FACTORS = (1.0, LAMBDA, -1.0)
 GROUPED_STEP = 5
 QE_STEP = 6
 PAIR = 1
+CURVE = True
 PRE1 = 6
 RATE1 = 1
 G1_PRE = True
@@ -435,9 +436,16 @@ def tile_basicemotionpredictions_pa_kernel(tc, h2, gamma, beta, Wh, bh, out):
         if W1_BY == "v":
             regroup_w(1)
         bias_less = keep.tile([P, COL_TILES], F32)
-        nc.scalar.activation(
-            out=bias_less[:], in_=bias_ps[:, 0:COL_TILES], func=ACT.Identity, bias=minus_alpha[:], scale=1.0
-        )
+        if CURVE:
+            nc.scalar.copy(out=bias_less[:], in_=bias_ps[:, 0:COL_TILES])
+            bias_drop = keep.tile([P, COL_TILES], F32)
+            nc.scalar.activation(
+                out=bias_drop[:], in_=bias_ps[:, 0:COL_TILES], func=ACT.Identity, bias=minus_alpha[:], scale=-1.0
+            )
+        else:
+            nc.scalar.activation(
+                out=bias_less[:], in_=bias_ps[:, 0:COL_TILES], func=ACT.Identity, bias=minus_alpha[:], scale=1.0
+            )
         bias_log = keep.tile([P, COL_TILES], F32)
         nc.scalar.activation(
             out=bias_log[:], in_=bias_ps[:, 0:COL_TILES], func=ACT.Identity, bias=log_alpha[:], scale=1.0
@@ -481,11 +489,19 @@ def tile_basicemotionpredictions_pa_kernel(tc, h2, gamma, beta, Wh, bh, out):
 
         def clip(m):
             clipped = grow_pool.tile([P, PAIR, HALF], F32, tag="clipped")
-            nc.gpsimd.tensor_scalar(
-                out=clipped[:].rearrange("p r b -> p (r b)"),
-                in0=growths[m][:].rearrange("p r b -> p (r b)"), scalar1=ALPHA, scalar2=0.0,
-                op0=ALU.min, op1=ALU.max,
-            )
+            if CURVE:
+                c = rounds[m][1]
+                nc.gpsimd.tensor_scalar(
+                    out=clipped[:].rearrange("p r b -> p (r b)"),
+                    in0=growths[m][:].rearrange("p r b -> p (r b)"), scalar1=1.0, scalar2=bias_drop[:, c : c + 1],
+                    op0=ALU.mult, op1=ALU.add,
+                )
+            else:
+                nc.gpsimd.tensor_scalar(
+                    out=clipped[:].rearrange("p r b -> p (r b)"),
+                    in0=growths[m][:].rearrange("p r b -> p (r b)"), scalar1=ALPHA, scalar2=0.0,
+                    op0=ALU.min, op1=ALU.max,
+                )
             curves[m] = clipped
 
         def combine(n):
@@ -493,7 +509,7 @@ def tile_basicemotionpredictions_pa_kernel(tc, h2, gamma, beta, Wh, bh, out):
             low = work.tile([P, HALF], F32, tag="low")
             nc.vector.scalar_tensor_tensor(
                 out=low[:], in0=p_tiles[n][:], scalar=bias_minus[:, c : c + 1], in1=curves[n // PAIR][:, n % PAIR, :],
-                op0=ALU.max, op1=ALU.add,
+                op0=ALU.max, op1=ALU.min if CURVE else ALU.add,
             )
             lows[n] = low
 

@@ -37,38 +37,50 @@ BN_EPS = 1e-5
 ALPHA = 1.6732632423543772
 LAMBDA = 1.0507009873554805
 L1_FLOOR = 1e-12 / LAMBDA
-LIFT_PERIOD = 3
-SCALAR_LIFTS = (1,)
+LIFT_PERIOD = 5
+SCALAR_LIFTS = (1, 3)
 Z_FACTORS = (1.0, LAMBDA, -1.0)
-GROUPED_STEP = 5
-QE_STEP = 6
+GROUPED_STEP = 3
+QE_STEP = 9
 PAIR = 1
+PB = 5
+FSTEP = 1
+FLAG = 2
+FBY = "v"
+E_BY = "pe"
+ELAG = 1
+W1_LATE = False
+NORM = 0
+ORDER = 1
+FULLRELU = False
+RELU2 = False
+W0_BY = "s"
 CURVE = True
 PRE1 = 6
-RATE1 = 1
+RATE1 = 2
 G1_PRE = True
 Q1_STEP = 1
 QG1_STEP = 3
 ARS = False
-HEAD = 2
+HEAD = 3
 QW = 3
 EARLY1 = False
 CL1_V = False
 E1_FIRST = 0
 E1_EVERY = 1
-LIFT_FROM = 8
+LIFT_FROM = 0
 W1_BY = "g"
 G1_BY = "v"
-G2_BY = "v"
+G2_BY = "pe"
 G1_STEP = 1
-G2_STEP = 8
+G2_STEP = 10
 CLIP_LIFT = 0
 GROUP_LEAD = 7
-TURN = 12
-FOLD = 4
-LIFT = 4
-ABS = 3
-COMB = 1
+TURN = 13
+FOLD = 5
+LIFT = 5
+ABS = 4
+COMB = 2
 RUN = 4
 
 FLOPS = 2 * BATCH * HID * COLS
@@ -83,16 +95,15 @@ def tile_basicemotionpredictions_pa_kernel(tc, h2, gamma, beta, Wh, bh, out):
         e_stage = ctx.enter_context(tc.tile_pool(name="e_stage", bufs=4))
         work = ctx.enter_context(tc.tile_pool(name="work", bufs=4))
         joint_pool = {
-            HALF // HEAD: ctx.enter_context(tc.tile_pool(name="joint_pieces", bufs=2)),
-            HALF: ctx.enter_context(tc.tile_pool(name="joint_half", bufs=1)),
+            HALF: ctx.enter_context(tc.tile_pool(name="joint_half", bufs=2)),
         }
         grow_pool = ctx.enter_context(tc.tile_pool(name="grow_pool", bufs=3))
         held = ctx.enter_context(tc.tile_pool(name="held", bufs=20))
         small = ctx.enter_context(tc.tile_pool(name="small", bufs=2))
         out_stage = ctx.enter_context(tc.tile_pool(name="out_stage", bufs=4))
-        psum = ctx.enter_context(tc.psum_pool(name="psum", bufs=4))
+        psum = ctx.enter_context(tc.psum_pool(name="psum", bufs=PB))
         psum_turn = ctx.enter_context(tc.psum_pool(name="psum_turn", bufs=2))
-        psum_acc = ctx.enter_context(tc.psum_pool(name="psum_acc", bufs=2))
+        psum_acc = ctx.enter_context(tc.psum_pool(name="psum_acc", bufs=6 - PB))
 
         ctx.enter_context(tc.manual_schedule())
 
@@ -134,6 +145,8 @@ def tile_basicemotionpredictions_pa_kernel(tc, h2, gamma, beta, Wh, bh, out):
 
         ident = keep.tile([P, P], F32)
         make_identity(nc, ident[:])
+        ident_bf = keep.tile([P, P], BF16)
+        nc.vector.tensor_copy(out=ident_bf[:], in_=ident[:])
         one_col = keep.tile([P, 1], F32)
         nc.vector.memset(one_col[:], 1.0)
         neg_half = keep.tile([P, PACK], F32)
@@ -188,6 +201,27 @@ def tile_basicemotionpredictions_pa_kernel(tc, h2, gamma, beta, Wh, bh, out):
                     out=w_grouped_all[g][:, first : first + count].rearrange("p s n i j -> p s n j i"),
                     in_=spread[:, first : first + count],
                 )
+
+        def fill(g, i):
+            if i == 0:
+                w_grouped_all[g] = w_stage.tile(
+                    [P, SPLIT, GROUP_HEADS, SUB, PACK], BF16, name="grouped_all%d" % g, align_bytes=64, tag="w_grouped_all"
+                )
+            passed = psum_turn.tile([P, 2, HALF], BF16, name="passed", tag="turned")
+            spread = w_raw[g][:].rearrange("p n (j s i) -> p s n i j", j=PACK, s=SPLIT)
+            for s in range(2):
+                nc.tensor.matmul(
+                    out=passed[:, s, :], lhsT=ident_bf[:], rhs=spread[:, 2 * i + s], start=True, stop=True,
+                )
+            fills[g, i] = passed
+
+        def drain_fill(g, i, engine):
+            out = w_grouped_all[g][:, 2 * i : 2 * i + 2].rearrange("p s n i j -> p (s n i j)")
+            in_ = fills[g, i][:].rearrange("p s c -> p (s c)")
+            if engine == "v":
+                nc.vector.tensor_copy(out=out, in_=in_)
+            else:
+                nc.scalar.copy(out=out, in_=in_)
 
         def quantise_group(g):
             cols = slice(g * GROUP_COLS, (g + 1) * GROUP_COLS)
@@ -245,7 +279,8 @@ def tile_basicemotionpredictions_pa_kernel(tc, h2, gamma, beta, Wh, bh, out):
                             op0=ALU.mult, op1=ALU.add,
                         )
 
-        regroup_w(0, by_scalar=True)
+        if W0_BY == "s":
+            regroup_w(0, by_scalar=True)
 
         mean_var = keep.tile([P, PACK, 2], F32)
         for u in range(2):
@@ -261,6 +296,8 @@ def tile_basicemotionpredictions_pa_kernel(tc, h2, gamma, beta, Wh, bh, out):
             nc.scalar.activation(out=warm[:], in_=one_col[:], func=ACT.Exp)
         else:
             nc.gpsimd.tensor_tensor(out=rstd[:], in0=var_eps[:], in1=neg_half[:], op=ALU.pow)
+        if W0_BY == "g":
+            regroup_w(0, by_g=True)
         if W1_BY == "g":
             regroup_w(1, by_g=True)
         nc.gpsimd.tensor_copy(out=bias_rows_f[:], in_=bias_rows[:])
@@ -277,6 +314,10 @@ def tile_basicemotionpredictions_pa_kernel(tc, h2, gamma, beta, Wh, bh, out):
             in1=mean_var[:, :, 0].unsqueeze(1).to_broadcast([P, len(Z_FACTORS), PACK]),
             op=ALU.mult,
         )
+        if W0_BY == "v":
+            regroup_w(0)
+            if QW == -1:
+                quantise_w(0)
         mean_scaled = keep.tile([P, len(Z_FACTORS), PACK], F32)
         nc.vector.tensor_tensor(
             out=mean_scaled[:],
@@ -305,6 +346,7 @@ def tile_basicemotionpredictions_pa_kernel(tc, h2, gamma, beta, Wh, bh, out):
         joint_parts = {}
 
         e_clamped = {}
+        fills = {}
 
         def feature(half, j):
             u, odd = divmod(j, 2)
@@ -329,7 +371,8 @@ def tile_basicemotionpredictions_pa_kernel(tc, h2, gamma, beta, Wh, bh, out):
         CL1 = clamp_by_vector if CL1_V else clamp_by_scalar
 
         def selu_parts(half, j, first=0, count=HALF, joint=False, what="both"):
-            clamped, sign, bias = e_clamped[half, j]
+            if what != "relu":
+                clamped, sign, bias = e_clamped[half, j]
             if joint:
                 if (half, first) not in joint_parts:
                     joint_parts[half, first] = (
@@ -363,13 +406,33 @@ def tile_basicemotionpredictions_pa_kernel(tc, h2, gamma, beta, Wh, bh, out):
                 op0=ALU.subtract, op1=ALU.add,
             )
 
-        def selu_grouped(half=1, first=0, count=HALF):
+        def selu_planes(half=1, first=0, count=HALF):
             rows = slice(half * HALF + first, half * HALF + first + count)
             nc.vector.scalar_tensor_tensor(
-                out=e_grouped[:, rows, :], in0=joint_parts[half, first][0][:].rearrange("p j b -> p b j"),
-                scalar=LAMBDA * ALPHA, in1=joint_parts[half, first][1][:].rearrange("p j b -> p b j"),
+                out=e_planes[:, :, rows],
+                in0=joint_parts[half, first][0][:],
+                scalar=LAMBDA * ALPHA,
+                in1=joint_parts[half, first][1][:],
                 op0=ALU.subtract, op1=ALU.add,
             )
+
+        def fill_e(i):
+            passed = psum_turn.tile([P, 2, HALF], BF16, name="passed_e", tag="turned")
+            for s in range(2):
+                first = HALF + i * 256 + s * P
+                nc.tensor.matmul(
+                    out=passed[:, s, :], lhsT=ident_bf[:],
+                    rhs=e_planes[:, :, first : first + P].rearrange("p j b -> p b j"), start=True, stop=True,
+                )
+            fills["e", i] = passed
+
+        def drain_e(i, engine):
+            out = e_grouped[:, HALF + i * 256 : HALF + (i + 1) * 256, :].rearrange("p b j -> p (b j)")
+            in_ = fills["e", i][:].rearrange("p s c -> p (s c)")
+            if engine == "v":
+                nc.vector.tensor_copy(out=out, in_=in_)
+            else:
+                nc.scalar.copy(out=out, in_=in_)
 
         def regroup_e(half, first=0, count=HALF):
             rows = slice(half * HALF + first, half * HALF + first + count)
@@ -417,23 +480,116 @@ def tile_basicemotionpredictions_pa_kernel(tc, h2, gamma, beta, Wh, bh, out):
             selu_parts(1, 0, 0, HALF, True)
             CL1(1, 1)
             quantise_e(0, HALF // 2, HALF // 2)
+        elif HEAD == 3:
+            def part(j, what, first=0, count=HALF):
+                if (0, 0) not in joint_parts:
+                    joint_parts[0, 0] = (
+                        joint_pool[HALF].tile([P, PACK, HALF], F32, name="decayed_all", tag="decayed"),
+                        joint_pool[HALF].tile([P, PACK, HALF], F32, name="linear_all", tag="linear"),
+                    )
+                if what == "exp":
+                    clamped, sign, bias = e_clamped[0, j]
+                    nc.scalar.activation(
+                        out=joint_parts[0, 0][0][:, j, first : first + count], in_=clamped[:, first : first + count],
+                        func=ACT.Exp, scale=sign, bias=bias,
+                    )
+                else:
+                    nc.scalar.activation(
+                        out=joint_parts[0, 0][1][:, j, first : first + count], in_=feature(0, j)[:, first : first + count],
+                        func=ACT.Relu, scale=scale2[:, 1, j : j + 1], bias=offset2[:, 1, j : j + 1],
+                    )
+
+            def planes(j, many, first=0, count=HALF):
+                nc.vector.scalar_tensor_tensor(
+                    out=e_planes[:, j : j + many, first : first + count],
+                    in0=joint_parts[0, 0][0][:, j : j + many, first : first + count],
+                    scalar=LAMBDA * ALPHA, in1=joint_parts[0, 0][1][:, j : j + many, first : first + count],
+                    op0=ALU.subtract, op1=ALU.add,
+                )
+
+            R = HALF // 2
+            part(2, "relu")
+            clamp_by_vector(0, 0)
+            part(3, "relu")
+            clamp_by_vector(0, 1)
+            part(0, "exp")
+            part(1, "exp")
+            clamp_by_vector(0, 2)
+            clamp_by_vector(0, 3)
+            quantise_w(0)
+            part(0, "relu")
+            planes(0, 1)
+            part(1, "relu")
+            planes(1, 1)
+            part(2, "exp")
+            part(3, "exp", 0, R)
+            planes(2, 1)
+            planes(3, 1, 0, R)
+            part(3, "exp", R, R)
+            regroup_e(0, 0, R)
+            planes(3, 1, R, R)
+            quantise_e(0, 0, R)
+            regroup_e(0, R, R)
+            if W1_LATE:
+                regroup_w(1)
+            quantise_e(0, R, R)
+            for task in half1[:PRE1]:
+                task()
+            if G1_PRE:
+                regroup_group(1, "v")
         else:
             nq = HEAD
             w = HALF // nq
-            for j in range(PACK):
+            if ORDER == 1:
+                for r in range(nq):
+                    joint_parts[0, r * w] = (
+                        joint_pool[w].tile([P, PACK, w], F32, name="decayed_all", tag="decayed"),
+                        joint_pool[w].tile([P, PACK, w], F32, name="linear_all", tag="linear"),
+                    )
+                if FULLRELU:
+                    assert False
+                for (sj, vj) in ((2, 0), (3, 1)):
+                    for r in range(nq if RELU2 else 1):
+                        selu_parts(0, sj, r * w, w, True, "relu")
+                    clamp_by_vector(0, vj)
+                if QW == 1:
+                    quantise_w(0)
+                for j in (0, 1):
+                    selu_parts(0, j, 0, w, True, "exp")
+                clamp_by_vector(0, 2)
+                clamp_by_vector(0, 3)
+                for j in (0, 1):
+                    selu_parts(0, j, 0, w, True, "relu")
+                for j in (2, 3):
+                    selu_parts(0, j, 0, w, True, "exp")
+                if QW == 3:
+                    quantise_w(0)
+                selu_planes(0, 0, w)
+                regroup_e(0, 0, w)
+                quantise_e(0, 0, w)
+                for r in range(1, nq):
+                    for j in range(PACK):
+                        if not (RELU2 and j >= 2):
+                            selu_parts(0, j, r * w, w, True, "relu")
+                        selu_parts(0, j, r * w, w, True, "exp")
+                    selu_planes(0, r * w, w)
+                    regroup_e(0, r * w, w)
+                    quantise_e(0, r * w, w)
+            for j in range(PACK if ORDER == 0 else 0):
                 clamp_by_vector(0, j)
                 if j == QW:
                     quantise_w(0)
-            for r in range(nq):
+            for r in range(nq if ORDER == 0 else 0):
                 for j in range(PACK):
                     selu_parts(0, j, r * w, w, True)
-                selu_grouped(0, r * w, w)
+                selu_planes(0, r * w, w)
+                regroup_e(0, r * w, w)
                 quantise_e(0, r * w, w)
             for task in half1[:PRE1]:
                 task()
             if G1_PRE:
                 regroup_group(1, "v")
-        if W1_BY == "v":
+        if W1_BY == "v" and not W1_LATE:
             regroup_w(1)
         bias_less = keep.tile([P, COL_TILES], F32)
         if CURVE:
@@ -463,6 +619,8 @@ def tile_basicemotionpredictions_pa_kernel(tc, h2, gamma, beta, Wh, bh, out):
         sizes = {}
         sums = {}
         inverses = {}
+        totals = {}
+        divisors = {}
         d_banks = {}
         results = {}
 
@@ -553,12 +711,20 @@ def tile_basicemotionpredictions_pa_kernel(tc, h2, gamma, beta, Wh, bh, out):
                 out=total[:], in_=sums[q][:].rearrange("p t (n i) -> p (t n) i", i=SUB),
                 axis=mybir.AxisListType.X, op=ALU.add,
             )
+            totals[q] = total
+
+        def floor_sums(q):
+            total = totals[q]
             divisor = small.tile([P, TILES_PER_HALF * GROUP_HEADS], F32, tag="divisor")
             unused = small.tile([P, 1], F32, tag="unused")
             nc.vector.tensor_scalar(
                 out=divisor[:], in0=total[:], scalar1=L1_FLOOR, scalar2=None, op0=ALU.max, op1=ALU.add,
                 accum_out=unused[:],
             )
+            divisors[q] = divisor
+
+        def invert(q):
+            divisor = divisors[q]
             inverse = small.tile([P, TILES_PER_HALF, GROUP_HEADS], F32, tag="inverse")
             nc.vector.reciprocal(out=inverse[:].rearrange("p t n -> p (t n)"), in_=divisor[:])
             inverses[q] = inverse
@@ -608,6 +774,7 @@ def tile_basicemotionpredictions_pa_kernel(tc, h2, gamma, beta, Wh, bh, out):
         def later(stage, *what):
             return lambda: stage(*what)
 
+        early = {}
         woven = {}
 
         def weave(step, engine, stage, *what):
@@ -615,7 +782,13 @@ def tile_basicemotionpredictions_pa_kernel(tc, h2, gamma, beta, Wh, bh, out):
 
         for i, task in enumerate(half1[PRE1:]):
             woven.setdefault(E1_FIRST + i // RATE1, ([], []))[0 if i % 3 or not CL1_V else 1].append(task)
-        weave(GROUPED_STEP, 1, selu_grouped)
+        weave(GROUPED_STEP, 1, selu_planes)
+        if E_BY == "v":
+            weave(GROUPED_STEP + 1, 1, regroup_e, 1)
+        else:
+            for i in range(2):
+                early.setdefault(GROUPED_STEP + 2 + i, []).append(later(fill_e, i))
+                weave(GROUPED_STEP + 2 + i + ELAG, 0 if FBY == "s" else 1, drain_e, i, FBY)
         weave(QE_STEP, 1, quantise_e, 1)
         weave(Q1_STEP, 1, quantise_w, 1)
         if G1_BY == "v" and not G1_PRE:
@@ -623,15 +796,22 @@ def tile_basicemotionpredictions_pa_kernel(tc, h2, gamma, beta, Wh, bh, out):
         if G1_BY == "gv":
             weave(G1_STEP, 1, regroup_group, 1, "v", 4, 4)
         weave(QG1_STEP, 1, quantise_group, 1)
+        tensor_woven = early
         if G2_BY == "v":
             weave(G2_STEP, 1, regroup_group, 2, "v")
+        elif G2_BY == "pe":
+            for i in range(4):
+                tensor_woven.setdefault(G2_STEP - 5 + FSTEP * i, []).append(later(fill, 2, i))
+                weave(G2_STEP - 5 + FSTEP * i + FLAG, 0 if FBY == "s" else 1, drain_fill, 2, i, FBY)
         else:
             for s in range(SPLIT):
                 weave(G2_STEP + s // 2 - 4, 0, regroup_group, 2, "s", s, 1)
-        weave(G2_STEP + 2, 1, quantise_group, 2)
+        weave(G2_STEP + 2 if G2_BY != "pe" else G2_STEP - 4 + 3 * FSTEP + FLAG, 1, quantise_group, 2)
 
         for j in range(-1, len(rounds) + TURN + 2):
             at(multiply, j + 1)
+            for task in tensor_woven.get(j, []):
+                task()
             at(turn, j - TURN)
             at(fold, j - FOLD)
             at(grow, j)
@@ -641,9 +821,32 @@ def tile_basicemotionpredictions_pa_kernel(tc, h2, gamma, beta, Wh, bh, out):
             at(magnitude, j - ABS)
             for task in woven.get(j, ([], []))[0]:
                 task()
-            at(scale_and_store, j - TURN - 1)
-            if j >= TURN and (j - TURN) % SPLIT == 0 and (j - TURN) // SPLIT < len(rounds) // SPLIT:
-                norm((j - TURN) // SPLIT)
-            at(combine, j - COMB)
+            q, place = divmod(j - TURN, SPLIT)
+            sets = len(rounds) // SPLIT
+            if NORM == 0:
+                at(scale_and_store, j - TURN - 1)
+                if place == 0 and 0 <= q < sets:
+                    norm(q)
+                    floor_sums(q)
+                    invert(q)
+                at(combine, j - COMB)
+            elif place == 0 and 0 <= q < sets:
+                at(scale_and_store, j - TURN - 1)
+                norm(q)
+                at(combine, j - COMB)
+                floor_sums(q)
+                if NORM == 2:
+                    invert(q)
+            elif place == 1 and 0 <= q < sets:
+                if NORM == 1:
+                    at(combine, j - COMB)
+                    invert(q)
+                    at(scale_and_store, j - TURN - 1)
+                else:
+                    at(combine, j - COMB)
+                    at(scale_and_store, j - TURN - 1)
+            else:
+                at(scale_and_store, j - TURN - 1)
+                at(combine, j - COMB)
             for task in woven.get(j, ([], []))[1]:
                 task()

@@ -37,48 +37,56 @@ BN_EPS = 1e-5
 ALPHA = 1.6732632423543772
 LAMBDA = 1.0507009873554805
 L1_FLOOR = 1e-12 / LAMBDA
-LIFT_PERIOD = 5
-SCALAR_LIFTS = (1, 3)
+LIFT_PERIOD = 3
+SCALAR_LIFTS = (1,)
 Z_FACTORS = (1.0, LAMBDA, -1.0)
-GROUPED_STEP = 3
-QE_STEP = 9
+GROUPED_STEP = 4
+QE_STEP = 6
 PAIR = 1
 PB = 5
 FSTEP = 1
 FLAG = 2
 FBY = "v"
-E_BY = "pe"
+E_BY = "v"
 ELAG = 1
 W1_LATE = False
+GRATE = 1
+G1_G = 8
+G_UNITS = ()
+TAILX = 35
+TAILX2 = 100
+FOLDFIRST = 100
+QG2_STEP = 11
+FLOOR = "v"
 NORM = 0
 ORDER = 1
 FULLRELU = False
 RELU2 = False
-W0_BY = "s"
+W0_BY = "v"
 CURVE = True
-PRE1 = 6
-RATE1 = 2
+PRE1 = 7
+RATE1 = 3
 G1_PRE = True
 Q1_STEP = 1
-QG1_STEP = 3
+QG1_STEP = 0
 ARS = False
 HEAD = 3
 QW = 3
 EARLY1 = False
 CL1_V = False
-E1_FIRST = 0
+E1_FIRST = 1
 E1_EVERY = 1
 LIFT_FROM = 0
 W1_BY = "g"
 G1_BY = "v"
-G2_BY = "pe"
+G2_BY = "v"
 G1_STEP = 1
-G2_STEP = 10
+G2_STEP = 8
 CLIP_LIFT = 0
 GROUP_LEAD = 7
 TURN = 13
 FOLD = 5
-LIFT = 5
+LIFT = 4
 ABS = 4
 COMB = 2
 RUN = 4
@@ -188,7 +196,7 @@ def tile_basicemotionpredictions_pa_kernel(tc, h2, gamma, beta, Wh, bh, out):
                     [P, SPLIT, GROUP_HEADS, SUB, PACK], BF16, name="grouped_all%d" % g, align_bytes=64, tag="w_grouped_all"
                 )
             spread = w_raw[g][:].rearrange("p n (j s i) -> p s n j i", j=PACK, s=SPLIT)
-            for s in range(first, first + count):
+            for s in range(first, first + count if engine != "v" else first):
                 if engine == "g":
                     nc.gpsimd.tensor_scalar(
                         out=w_grouped_all[g][:, s], in0=spread[:, s].rearrange("p n j i -> p n i j"),
@@ -305,6 +313,8 @@ def tile_basicemotionpredictions_pa_kernel(tc, h2, gamma, beta, Wh, bh, out):
             regroup_group(1, "g")
         if G1_BY == "gv":
             regroup_group(1, "g", 0, 4)
+        if G1_BY == "gh":
+            regroup_group(1, "g", 0, G1_G)
         bias_ps = psum.tile([P, P], F32, tag="product")
         nc.tensor.transpose(bias_ps[:], bias_rows_f[:], ident[:])
         mean_gain = keep.tile([P, len(Z_FACTORS), PACK], F32)
@@ -414,6 +424,13 @@ def tile_basicemotionpredictions_pa_kernel(tc, h2, gamma, beta, Wh, bh, out):
                 scalar=LAMBDA * ALPHA,
                 in1=joint_parts[half, first][1][:],
                 op0=ALU.subtract, op1=ALU.add,
+            )
+
+        def regroup_e_by_gpsimd(i):
+            rows = slice(HALF + i * P, HALF + (i + 1) * P)
+            nc.gpsimd.tensor_scalar(
+                out=e_grouped[:, rows, :], in0=e_planes[:, :, rows].rearrange("p j b -> p b j"),
+                scalar1=1.0, scalar2=0.0, op0=ALU.mult, op1=ALU.add,
             )
 
         def fill_e(i):
@@ -535,8 +552,10 @@ def tile_basicemotionpredictions_pa_kernel(tc, h2, gamma, beta, Wh, bh, out):
             quantise_e(0, R, R)
             for task in half1[:PRE1]:
                 task()
-            if G1_PRE:
+            if G1_PRE and G1_BY == "v":
                 regroup_group(1, "v")
+            if G1_BY == "gh" and G1_G < SPLIT:
+                regroup_group(1, "v", G1_G, SPLIT - G1_G)
         else:
             nq = HEAD
             w = HALF // nq
@@ -587,8 +606,10 @@ def tile_basicemotionpredictions_pa_kernel(tc, h2, gamma, beta, Wh, bh, out):
                 quantise_e(0, r * w, w)
             for task in half1[:PRE1]:
                 task()
-            if G1_PRE:
+            if G1_PRE and G1_BY == "v":
                 regroup_group(1, "v")
+            if G1_BY == "gh" and G1_G < SPLIT:
+                regroup_group(1, "v", G1_G, SPLIT - G1_G)
         if W1_BY == "v" and not W1_LATE:
             regroup_w(1)
         bias_less = keep.tile([P, COL_TILES], F32)
@@ -716,6 +737,12 @@ def tile_basicemotionpredictions_pa_kernel(tc, h2, gamma, beta, Wh, bh, out):
         def floor_sums(q):
             total = totals[q]
             divisor = small.tile([P, TILES_PER_HALF * GROUP_HEADS], F32, tag="divisor")
+            if FLOOR == "g":
+                nc.gpsimd.tensor_scalar(
+                    out=divisor[:], in0=total[:], scalar1=3.0e38, scalar2=L1_FLOOR, op0=ALU.min, op1=ALU.max
+                )
+                divisors[q] = divisor
+                return
             unused = small.tile([P, 1], F32, tag="unused")
             nc.vector.tensor_scalar(
                 out=divisor[:], in0=total[:], scalar1=L1_FLOOR, scalar2=None, op0=ALU.max, op1=ALU.add,
@@ -732,7 +759,7 @@ def tile_basicemotionpredictions_pa_kernel(tc, h2, gamma, beta, Wh, bh, out):
         def turn(x):
             q, u = divmod(x, SPLIT)
             t, a = divmod(u, CHUNKS_PER_GROUP)
-            if x >= len(rounds) - SPLIT and x % 2 == 1:
+            if x >= TAILX and (x % 2 == 1 or x >= TAILX2):
                 d_ps = psum.tile([P, CHUNK_TILES, P], F32, tag="product")
             else:
                 d_ps = psum_turn.tile([P, CHUNK_TILES, P], F32, tag="turned")
@@ -748,11 +775,17 @@ def tile_basicemotionpredictions_pa_kernel(tc, h2, gamma, beta, Wh, bh, out):
             if a == 0:
                 results[q, t] = out_stage.tile([P, GROUP_COLS], F32, name="result", tag="result")
             result = results[q, t]
-            nc.vector.tensor_tensor(
+            turned = d_banks[x]
+            engine = nc.vector
+            if x in G_UNITS:
+                turned = out_stage.tile([P, CHUNK_TILES, P], F32, name="lifted", tag="lifted")
+                nc.scalar.copy(out=turned[:], in_=d_banks[x][:])
+                engine = nc.gpsimd
+            engine.tensor_tensor(
                 out=result[:].rearrange("p (n s i) -> p s n i", s=SPLIT, i=SUB)[
                     :, a * CHUNK_TILES : (a + 1) * CHUNK_TILES
                 ],
-                in0=d_banks[x][:].rearrange("p s (n i) -> p s n i", i=SUB),
+                in0=turned[:].rearrange("p s (n i) -> p s n i", i=SUB),
                 in1=inverses[q][:, t, :]
                 .unsqueeze(1)
                 .unsqueeze(3)
@@ -785,7 +818,7 @@ def tile_basicemotionpredictions_pa_kernel(tc, h2, gamma, beta, Wh, bh, out):
         weave(GROUPED_STEP, 1, selu_planes)
         if E_BY == "v":
             weave(GROUPED_STEP + 1, 1, regroup_e, 1)
-        else:
+        elif E_BY == "pe":
             for i in range(2):
                 early.setdefault(GROUPED_STEP + 2 + i, []).append(later(fill_e, i))
                 weave(GROUPED_STEP + 2 + i + ELAG, 0 if FBY == "s" else 1, drain_e, i, FBY)
@@ -797,6 +830,22 @@ def tile_basicemotionpredictions_pa_kernel(tc, h2, gamma, beta, Wh, bh, out):
             weave(G1_STEP, 1, regroup_group, 1, "v", 4, 4)
         weave(QG1_STEP, 1, quantise_group, 1)
         tensor_woven = early
+        g_woven = {}
+        if G1_BY == "gl":
+            for s in range(SPLIT):
+                g_woven.setdefault(G1_STEP + s // GRATE, []).append(later(regroup_group, 1, "g", s, 1))
+        if G2_BY == "gl":
+            for s in range(SPLIT):
+                g_woven.setdefault(G2_STEP + s // GRATE, []).append(later(regroup_group, 2, "g", s, 1))
+        if G2_BY == "sl":
+            for s in range(SPLIT):
+                weave(G2_STEP + s // GRATE, 0, regroup_group, 2, "s", s, 1)
+        if G1_BY == "sl":
+            for s in range(SPLIT):
+                weave(G1_STEP + s // GRATE, 0, regroup_group, 1, "s", s, 1)
+        if E_BY == "g":
+            for i in range(4):
+                g_woven.setdefault(GROUPED_STEP + 1 + i // 2, []).append(later(regroup_e_by_gpsimd, i))
         if G2_BY == "v":
             weave(G2_STEP, 1, regroup_group, 2, "v")
         elif G2_BY == "pe":
@@ -806,18 +855,24 @@ def tile_basicemotionpredictions_pa_kernel(tc, h2, gamma, beta, Wh, bh, out):
         else:
             for s in range(SPLIT):
                 weave(G2_STEP + s // 2 - 4, 0, regroup_group, 2, "s", s, 1)
-        weave(G2_STEP + 2 if G2_BY != "pe" else G2_STEP - 4 + 3 * FSTEP + FLAG, 1, quantise_group, 2)
+        weave(QG2_STEP if G2_BY != "pe" else G2_STEP - 4 + 3 * FSTEP + FLAG, 1, quantise_group, 2)
 
         for j in range(-1, len(rounds) + TURN + 2):
             at(multiply, j + 1)
             for task in tensor_woven.get(j, []):
                 task()
-            at(turn, j - TURN)
-            at(fold, j - FOLD)
+            if j >= FOLDFIRST:
+                at(fold, j - FOLD)
+                at(turn, j - TURN)
+            else:
+                at(turn, j - TURN)
+                at(fold, j - FOLD)
             at(grow, j)
             at(lift, j - LIFT)
             if j % PAIR == PAIR - 1 and 0 <= j < len(rounds):
                 clip(j // PAIR)
+            for task in g_woven.get(j, []):
+                task()
             at(magnitude, j - ABS)
             for task in woven.get(j, ([], []))[0]:
                 task()

@@ -51,6 +51,9 @@ E_BY = "v"
 ELAG = 1
 W1_LATE = False
 GRATE = 1
+WB = 5
+GB = 5
+HB = 19
 G1_G = 8
 G_UNITS = ()
 TAILX = 35
@@ -101,12 +104,12 @@ def tile_basicemotionpredictions_pa_kernel(tc, h2, gamma, beta, Wh, bh, out):
         w_in = ctx.enter_context(tc.tile_pool(name="w_in", bufs=HEAD_GROUPS))
         w_stage = ctx.enter_context(tc.tile_pool(name="w_stage", bufs=2))
         e_stage = ctx.enter_context(tc.tile_pool(name="e_stage", bufs=4))
-        work = ctx.enter_context(tc.tile_pool(name="work", bufs=4))
+        work = ctx.enter_context(tc.tile_pool(name="work", bufs=WB))
         joint_pool = {
             HALF: ctx.enter_context(tc.tile_pool(name="joint_half", bufs=2)),
         }
-        grow_pool = ctx.enter_context(tc.tile_pool(name="grow_pool", bufs=3))
-        held = ctx.enter_context(tc.tile_pool(name="held", bufs=20))
+        grow_pool = ctx.enter_context(tc.tile_pool(name="grow_pool", bufs=GB))
+        held = ctx.enter_context(tc.tile_pool(name="held", bufs=HB))
         small = ctx.enter_context(tc.tile_pool(name="small", bufs=2))
         out_stage = ctx.enter_context(tc.tile_pool(name="out_stage", bufs=4))
         psum = ctx.enter_context(tc.psum_pool(name="psum", bufs=PB))

@@ -128,11 +128,8 @@ def tile_basicemotionpredictions_pa_kernel(tc, h2, gamma, beta, Wh, bh, out):
         nc.sync.dma_start(out=gamma_bf[:], in_=gamma.rearrange("(p j) -> p j", j=PACK))
         beta_bf = keep.tile([P, PACK], BF16)
         nc.sync.dma_start(out=beta_bf[:], in_=beta.rearrange("(p j) -> p j", j=PACK))
-        bias_rows = keep.tile([P, P], BF16)
-        nc.vector.memset(bias_rows[:], 0.0)
-        bh_tiles = bh.rearrange("h g e -> (h g) e").rearrange(
-            "(a n) (s i) -> a s n i", a=HEAD_GROUPS, i=SUB
-        )
+        bias_heads = keep.tile([P, E], BF16)
+        nc.vector.memset(bias_heads[:], 0.0)
 
         w_rows = Wh.rearrange("h g (p j) e -> p (h g) (j e)", j=PACK)
         w_raw = []
@@ -146,18 +143,16 @@ def tile_basicemotionpredictions_pa_kernel(tc, h2, gamma, beta, Wh, bh, out):
                 )
             w_raw.append(raw)
             if g == 0:
-                for group in range(HEAD_GROUPS):
-                    nc.sync.dma_start(
-                        out=bias_rows[group * SPLIT : (group + 1) * SPLIT, :].rearrange(
-                            "s (n i) -> s n i", i=SUB
-                        ),
-                        in_=bh_tiles[group],
-                    )
+                nc.sync.dma_start(out=bias_heads[0:HEADS, :], in_=bh.rearrange("h g e -> (h g) e"))
 
         ident = keep.tile([P, P], F32)
         make_identity(nc, ident[:])
-        ident_bf = keep.tile([P, P], BF16)
-        nc.vector.tensor_copy(out=ident_bf[:], in_=ident[:])
+        pick = keep.tile([P, HEAD_GROUPS, SUB, GROUP_HEADS, SUB], BF16)
+        nc.vector.memset(pick[:], 0.0)
+        for i in range(SUB):
+            nc.vector.tensor_copy(
+                out=pick[:, :, i, :, i], in_=ident[:, 0:HEADS].rearrange("p (g n) -> p g n", g=HEAD_GROUPS)
+            )
         one_col = keep.tile([P, 1], F32)
         nc.vector.memset(one_col[:], 1.0)
         neg_half = keep.tile([P, PACK], F32)
@@ -222,7 +217,7 @@ def tile_basicemotionpredictions_pa_kernel(tc, h2, gamma, beta, Wh, bh, out):
             spread = w_raw[g][:].rearrange("p n (j s i) -> p s n i j", j=PACK, s=SPLIT)
             for s in range(2):
                 nc.tensor.matmul(
-                    out=passed[:, s, :], lhsT=ident_bf[:], rhs=spread[:, 2 * i + s], start=True, stop=True,
+                    out=passed[:, s, :], lhsT=ident[:], rhs=spread[:, 2 * i + s], start=True, stop=True,
                 )
             fills[g, i] = passed
 
@@ -266,7 +261,6 @@ def tile_basicemotionpredictions_pa_kernel(tc, h2, gamma, beta, Wh, bh, out):
         log_col = keep.tile([P, 1], F32)
         log_alpha = keep.tile([P, 1], F32)
         minus_alpha = keep.tile([P, 1], F32)
-        bias_rows_f = keep.tile([P, P], F32)
         nc.vector.tensor_scalar_mul(log_col[:], one_col[:], math.log(LAMBDA * ALPHA))
         nc.vector.tensor_scalar_mul(log_alpha[:], one_col[:], math.log(ALPHA))
         nc.vector.tensor_scalar_mul(minus_alpha[:], one_col[:], -ALPHA)
@@ -311,7 +305,6 @@ def tile_basicemotionpredictions_pa_kernel(tc, h2, gamma, beta, Wh, bh, out):
             regroup_w(0, by_g=True)
         if W1_BY == "g":
             regroup_w(1, by_g=True)
-        nc.gpsimd.tensor_copy(out=bias_rows_f[:], in_=bias_rows[:])
         if G1_BY == "g":
             regroup_group(1, "g")
         if G1_BY == "gv":
@@ -319,7 +312,14 @@ def tile_basicemotionpredictions_pa_kernel(tc, h2, gamma, beta, Wh, bh, out):
         if G1_BY == "gh":
             regroup_group(1, "g", 0, G1_G)
         bias_ps = psum.tile([P, P], F32, tag="product")
-        nc.tensor.transpose(bias_ps[:], bias_rows_f[:], ident[:])
+        for g in range(HEAD_GROUPS):
+            for i in range(SUB):
+                nc.tensor.matmul(
+                    out=bias_ps[:, g * SPLIT : (g + 1) * SPLIT],
+                    lhsT=pick[:, g, i].rearrange("p n i -> p (n i)"),
+                    rhs=bias_heads[:].rearrange("p (s i) -> p i s", i=SUB)[:, i],
+                    start=(i == 0), stop=(i == SUB - 1),
+                )
         mean_gain = keep.tile([P, len(Z_FACTORS), PACK], F32)
         nc.vector.tensor_tensor(
             out=mean_gain[:],
@@ -441,7 +441,7 @@ def tile_basicemotionpredictions_pa_kernel(tc, h2, gamma, beta, Wh, bh, out):
             for s in range(2):
                 first = HALF + i * 256 + s * P
                 nc.tensor.matmul(
-                    out=passed[:, s, :], lhsT=ident_bf[:],
+                    out=passed[:, s, :], lhsT=ident[:],
                     rhs=e_planes[:, :, first : first + P].rearrange("p j b -> p b j"), start=True, stop=True,
                 )
             fills["e", i] = passed
@@ -864,6 +864,8 @@ def tile_basicemotionpredictions_pa_kernel(tc, h2, gamma, beta, Wh, bh, out):
             at(multiply, j + 1)
             for task in tensor_woven.get(j, []):
                 task()
+            if NORM == 3 and j >= TURN and (j - TURN) % SPLIT == 1 and (j - TURN) // SPLIT < len(rounds) // SPLIT:
+                floor_sums((j - TURN) // SPLIT)
             if j >= FOLDFIRST:
                 at(fold, j - FOLD)
                 at(turn, j - TURN)
@@ -892,11 +894,12 @@ def tile_basicemotionpredictions_pa_kernel(tc, h2, gamma, beta, Wh, bh, out):
                 at(scale_and_store, j - TURN - 1)
                 norm(q)
                 at(combine, j - COMB)
-                floor_sums(q)
+                if NORM != 3:
+                    floor_sums(q)
                 if NORM == 2:
                     invert(q)
             elif place == 1 and 0 <= q < sets:
-                if NORM == 1:
+                if NORM in (1, 3):
                     at(combine, j - COMB)
                     invert(q)
                     at(scale_and_store, j - TURN - 1)

@@ -124,10 +124,10 @@ def tile_basicemotionpredictions_pa_kernel(tc, h2, gamma, beta, Wh, bh, out):
             two = slice(2 * pair, 2 * pair + 2)
             nc.sync.dma_start(out=h2_sb[:, two, :], in_=h2_rows[:, two, :])
 
-        gamma_bf = keep.tile([P, PACK], BF16)
-        nc.sync.dma_start(out=gamma_bf[:], in_=gamma.rearrange("(p j) -> p j", j=PACK))
-        beta_bf = keep.tile([P, PACK], BF16)
-        nc.sync.dma_start(out=beta_bf[:], in_=beta.rearrange("(p j) -> p j", j=PACK))
+        rows = keep.tile([P, 2, HID], BF16)
+        nc.vector.memset(rows[:], 0.0)
+        nc.scalar.dma_start(out=rows[0:1, 0, :], in_=gamma.rearrange("(o f) -> o f", o=1))
+        nc.scalar.dma_start(out=rows[0:1, 1, :], in_=beta.rearrange("(o f) -> o f", o=1))
         bias_heads = keep.tile([P, E], BF16)
         nc.vector.memset(bias_heads[:], 0.0)
 
@@ -142,15 +142,15 @@ def tile_basicemotionpredictions_pa_kernel(tc, h2, gamma, beta, Wh, bh, out):
                     in_=w_rows[:, g * GROUP_HEADS + some.start : g * GROUP_HEADS + some.stop, :],
                 )
             w_raw.append(raw)
-            if g == 0:
+            if g == 1:
                 nc.sync.dma_start(out=bias_heads[0:HEADS, :], in_=bh.rearrange("h g e -> (h g) e"))
 
         ident = keep.tile([P, P], F32)
         make_identity(nc, ident[:])
         pick = keep.tile([P, HEAD_GROUPS, SUB, GROUP_HEADS, SUB], BF16)
-        nc.vector.memset(pick[:], 0.0)
+        nc.gpsimd.memset(pick[:], 0.0)
         for i in range(SUB):
-            nc.vector.tensor_copy(
+            nc.gpsimd.tensor_copy(
                 out=pick[:, :, i, :, i], in_=ident[:, 0:HEADS].rearrange("p (g n) -> p g n", g=HEAD_GROUPS)
             )
         one_col = keep.tile([P, 1], F32)
@@ -256,8 +256,9 @@ def tile_basicemotionpredictions_pa_kernel(tc, h2, gamma, beta, Wh, bh, out):
             for u in range(2)
         ]
         stats = keep.tile([P, 2, 4, 6], F32)
-        gain2 = keep.tile([P, len(Z_FACTORS), PACK], F32)
-        shift2 = keep.tile([P, len(Z_FACTORS), PACK], F32)
+        multiples = keep.tile([P, len(Z_FACTORS), 2, PACK], F32)
+        gain2 = multiples[:, :, 0, :]
+        shift2 = multiples[:, :, 1, :]
         log_col = keep.tile([P, 1], F32)
         log_alpha = keep.tile([P, 1], F32)
         minus_alpha = keep.tile([P, 1], F32)
@@ -276,13 +277,16 @@ def tile_basicemotionpredictions_pa_kernel(tc, h2, gamma, beta, Wh, bh, out):
                         out=stats[:, u, 2 * half + s, :],
                         in_=pairs[:, 2 * s : 2 * s + 2, :].rearrange("p t w -> p (t w)"),
                     )
-            if half == 0:
-                for row, factor in enumerate(Z_FACTORS):
-                    for multiple, small_input in ((gain2, gamma_bf), (shift2, beta_bf)):
-                        nc.gpsimd.tensor_scalar(
-                            out=multiple[:, row, :], in0=small_input[:], scalar1=factor, scalar2=0.0,
-                            op0=ALU.mult, op1=ALU.add,
-                        )
+        affine = psum_acc.tile([P, 2, PACK], F32, name="affine", tag="sums")
+        for w in range(2):
+            for j in range(PACK):
+                nc.tensor.matmul(
+                    out=affine[:, w, j : j + 1],
+                    lhsT=rows[:, w, :].rearrange("p (q j) -> p j q", j=PACK)[:, j],
+                    rhs=pick[:, 0, 0, 0, 0:1], start=True, stop=True,
+                )
+        for row, factor in enumerate(Z_FACTORS):
+            nc.scalar.mul(multiples[:, row], affine[:], factor)
 
         if W0_BY == "s":
             regroup_w(0, by_scalar=True)
@@ -323,7 +327,7 @@ def tile_basicemotionpredictions_pa_kernel(tc, h2, gamma, beta, Wh, bh, out):
         mean_gain = keep.tile([P, len(Z_FACTORS), PACK], F32)
         nc.vector.tensor_tensor(
             out=mean_gain[:],
-            in0=gain2[:],
+            in0=gain2,
             in1=mean_var[:, :, 0].unsqueeze(1).to_broadcast([P, len(Z_FACTORS), PACK]),
             op=ALU.mult,
         )
@@ -341,12 +345,12 @@ def tile_basicemotionpredictions_pa_kernel(tc, h2, gamma, beta, Wh, bh, out):
         scale2 = keep.tile([P, len(Z_FACTORS), PACK], F32)
         nc.vector.tensor_tensor(
             out=scale2[:],
-            in0=gain2[:],
+            in0=gain2,
             in1=rstd[:].unsqueeze(1).to_broadcast([P, len(Z_FACTORS), PACK]),
             op=ALU.mult,
         )
         offset2 = keep.tile([P, len(Z_FACTORS), PACK], F32)
-        nc.vector.tensor_tensor(out=offset2[:], in0=shift2[:], in1=mean_scaled[:], op=ALU.subtract)
+        nc.vector.tensor_tensor(out=offset2[:], in0=shift2, in1=mean_scaled[:], op=ALU.subtract)
         offset_log = keep.tile([P, PACK], F32)
         nc.vector.tensor_scalar_add(offset_log[:], offset2[:, 0, :], math.log(LAMBDA * ALPHA))
 
@@ -534,6 +538,8 @@ def tile_basicemotionpredictions_pa_kernel(tc, h2, gamma, beta, Wh, bh, out):
             clamp_by_vector(0, 1)
             part(0, "exp")
             part(1, "exp")
+            if W0_BY == "v2":
+                regroup_w(0)
             clamp_by_vector(0, 2)
             clamp_by_vector(0, 3)
             quantise_w(0)

import math
from contextlib import ExitStack

import concourse.mybir as mybir
from concourse.masks import make_identity

F32 = mybir.dt.float32
BF16 = mybir.dt.bfloat16
U32 = mybir.dt.uint32
U8 = mybir.dt.uint8
FP8X4 = mybir.dt.float8_e4m3fn_x4
ALU = mybir.AluOpType
ACT = mybir.ActivationFunctionType

P = 128
PACK = 4
BATCH = 1024
HID = P * PACK
HEADS = 96
E = 32
COLS = HEADS * E
BATCH_TILES = BATCH // P
HALF = 512
TILES_PER_HALF = HALF // P
COL_TILES = COLS // P
SPLIT = 8
SUB = E // SPLIT
GROUP_HEADS = P // SUB
HEAD_GROUPS = HEADS // GROUP_HEADS
GROUP_COLS = GROUP_HEADS * E
CHUNK_TILES = 4
CHUNKS = COL_TILES // CHUNK_TILES
CHUNK_COLS = CHUNK_TILES * P
CHUNKS_PER_GROUP = SPLIT // CHUNK_TILES

BN_EPS = 1e-5
ALPHA = 1.6732632423543772
LAMBDA = 1.0507009873554805
L1_FLOOR = 1e-12 / LAMBDA
LIFT_PERIOD = 3
SCALAR_LIFTS = (1,)
Z_FACTORS = (1.0, LAMBDA, -1.0)
GROUPED_STEP = 4
QE_STEP = 6
PAIR = 1
PB = 5
FSTEP = 1
FLAG = 2
FBY = "v"
E_BY = "v"
ELAG = 1
W1_LATE = False
GRATE = 1
WB = 5
GB = 5
HB = 19
G1_G = 8
G_UNITS = ()
TAILX = 35
TAILX2 = 100
FOLDFIRST = 100
QG2_STEP = 11
FLOOR = "v"
NORM = 0
ORDER = 1
FULLRELU = False
RELU2 = False
W0_BY = "v"
CURVE = True
PRE1 = 7
RATE1 = 3
G1_PRE = True
Q1_STEP = 1
QG1_STEP = 0
ARS = False
HEAD = 3
QW = 3
EARLY1 = False
CL1_V = False
E1_FIRST = 1
E1_EVERY = 1
LIFT_FROM = 0
W1_BY = "g"
G1_BY = "v"
G2_BY = "v"
G1_STEP = 1
G2_STEP = 8
CLIP_LIFT = 0
GROUP_LEAD = 7
TURN = 13
FOLD = 5
LIFT = 4
ABS = 4
COMB = 2
RUN = 4

FLOPS = 2 * BATCH * HID * COLS


def tile_basicemotionpredictions_pa_kernel(tc, h2, gamma, beta, Wh, bh, out):
    nc = tc.nc
    with ExitStack() as ctx:
        keep = ctx.enter_context(tc.tile_pool(name="keep", bufs=1))
        w_in = ctx.enter_context(tc.tile_pool(name="w_in", bufs=HEAD_GROUPS))
        w_stage = ctx.enter_context(tc.tile_pool(name="w_stage", bufs=2))
        e_stage = ctx.enter_context(tc.tile_pool(name="e_stage", bufs=4))
        work = ctx.enter_context(tc.tile_pool(name="work", bufs=WB))
        joint_pool = {
            HALF: ctx.enter_context(tc.tile_pool(name="joint_half", bufs=2)),
        }
        grow_pool = ctx.enter_context(tc.tile_pool(name="grow_pool", bufs=GB))
        held = ctx.enter_context(tc.tile_pool(name="held", bufs=HB))
        small = ctx.enter_context(tc.tile_pool(name="small", bufs=2))
        out_stage = ctx.enter_context(tc.tile_pool(name="out_stage", bufs=4))
        psum = ctx.enter_context(tc.psum_pool(name="psum", bufs=PB))
        psum_turn = ctx.enter_context(tc.psum_pool(name="psum_turn", bufs=2))
        psum_acc = ctx.enter_context(tc.psum_pool(name="psum_acc", bufs=6 - PB))

        ctx.enter_context(tc.manual_schedule())

        h2_rows = h2.rearrange("(p t) f -> p t f", t=BATCH_TILES)
        h2_sb = keep.tile([P, BATCH_TILES, HID], BF16)
        for pair in range(BATCH_TILES // 2):
            two = slice(2 * pair, 2 * pair + 2)
            nc.sync.dma_start(out=h2_sb[:, two, :], in_=h2_rows[:, two, :])

        rows = keep.tile([P, 2, HID], BF16)
        nc.vector.memset(rows[:], 0.0)
        nc.scalar.dma_start(out=rows[0:1, 0, :], in_=gamma.rearrange("(o f) -> o f", o=1))
        nc.scalar.dma_start(out=rows[0:1, 1, :], in_=beta.rearrange("(o f) -> o f", o=1))
        bias_heads = keep.tile([P, E], BF16)
        nc.vector.memset(bias_heads[:], 0.0)

        w_rows = Wh.rearrange("h g (p j) e -> p (h g) (j e)", j=PACK)
        w_raw = []
        for g in range(HEAD_GROUPS):
            raw = w_in.tile([P, GROUP_HEADS, PACK * E], BF16, name="w_raw%d" % g, tag="w_raw")
            for part in range(2):
                some = slice(part * GROUP_HEADS // 2, (part + 1) * GROUP_HEADS // 2)
                nc.sync.dma_start(
                    out=raw[:, some, :],
                    in_=w_rows[:, g * GROUP_HEADS + some.start : g * GROUP_HEADS + some.stop, :],
                )
            w_raw.append(raw)
            if g == 1:
                nc.sync.dma_start(out=bias_heads[0:HEADS, :], in_=bh.rearrange("h g e -> (h g) e"))

        ident = keep.tile([P, P], F32)
        make_identity(nc, ident[:])
        pick = keep.tile([P, HEAD_GROUPS, SUB, GROUP_HEADS, SUB], BF16)
        nc.gpsimd.memset(pick[:], 0.0)
        for i in range(SUB):
            nc.gpsimd.tensor_copy(
                out=pick[:, :, i, :, i], in_=ident[:, 0:HEADS].rearrange("p (g n) -> p g n", g=HEAD_GROUPS)
            )
        one_col = keep.tile([P, 1], F32)
        nc.vector.memset(one_col[:], 1.0)
        neg_half = keep.tile([P, PACK], F32)
        nc.vector.memset(neg_half[:], -0.5)
        warm = keep.tile([P, 1], F32)
        nc.scalar.activation(out=warm[:], in_=one_col[:], func=ACT.Abs_reciprocal_sqrt if ARS else ACT.Exp)

        w_codes = keep.tile([P, COLS], U32, align_bytes=64)
        w_scales = keep.tile([P, COLS], U8, align_bytes=64)
        w_grouped = {}
        w_grouped_all = {}

        def regroup_w(k, by_scalar=False, by_g=False):
            g, a = divmod(k, CHUNKS_PER_GROUP)
            grouped = w_stage.tile(
                [P, CHUNK_TILES, GROUP_HEADS, SUB, PACK], BF16, align_bytes=64, tag="w_grouped"
            )
            spread = w_raw[g][:].rearrange(
                "p n (j a s i) -> p a s n j i", j=PACK, a=CHUNKS_PER_GROUP, s=CHUNK_TILES
            )[:, a]
            if by_g:
                for s in range(CHUNK_TILES):
                    nc.gpsimd.tensor_scalar(
                        out=grouped[:, s], in0=spread[:, s].rearrange("p n j i -> p n i j"),
                        scalar1=1.0, scalar2=0.0, op0=ALU.mult, op1=ALU.add,
                    )
            elif by_scalar:
                for s in range(CHUNK_TILES):
                    nc.scalar.copy(
                        out=grouped[:, s].rearrange("p n i j -> p n j i"), in_=spread[:, s]
                    )
            else:
                nc.vector.tensor_copy(out=grouped[:].rearrange("p s n i j -> p s n j i"), in_=spread)
            w_grouped[k] = grouped

        def regroup_group(g, engine, first=0, count=SPLIT):
            if first == 0:
                w_grouped_all[g] = w_stage.tile(
                    [P, SPLIT, GROUP_HEADS, SUB, PACK], BF16, name="grouped_all%d" % g, align_bytes=64, tag="w_grouped_all"
                )
            spread = w_raw[g][:].rearrange("p n (j s i) -> p s n j i", j=PACK, s=SPLIT)
            for s in range(first, first + count if engine != "v" else first):
                if engine == "g":
                    nc.gpsimd.tensor_scalar(
                        out=w_grouped_all[g][:, s], in0=spread[:, s].rearrange("p n j i -> p n i j"),
                        scalar1=1.0, scalar2=0.0, op0=ALU.mult, op1=ALU.add,
                    )
                elif engine == "s":
                    nc.scalar.copy(out=w_grouped_all[g][:, s].rearrange("p n i j -> p n j i"), in_=spread[:, s])
            if engine == "v":
                nc.vector.tensor_copy(
                    out=w_grouped_all[g][:, first : first + count].rearrange("p s n i j -> p s n j i"),
                    in_=spread[:, first : first + count],
                )

        def fill(g, i):
            if i == 0:
                w_grouped_all[g] = w_stage.tile(
                    [P, SPLIT, GROUP_HEADS, SUB, PACK], BF16, name="grouped_all%d" % g, align_bytes=64, tag="w_grouped_all"
                )
            passed = psum_turn.tile([P, 2, HALF], BF16, name="passed", tag="turned")
            spread = w_raw[g][:].rearrange("p n (j s i) -> p s n i j", j=PACK, s=SPLIT)
            for s in range(2):
                nc.tensor.matmul(
                    out=passed[:, s, :], lhsT=ident[:], rhs=spread[:, 2 * i + s], start=True, stop=True,
                )
            fills[g, i] = passed

        def drain_fill(g, i, engine):
            out = w_grouped_all[g][:, 2 * i : 2 * i + 2].rearrange("p s n i j -> p (s n i j)")
            in_ = fills[g, i][:].rearrange("p s c -> p (s c)")
            if engine == "v":
                nc.vector.tensor_copy(out=out, in_=in_)
            else:
                nc.scalar.copy(out=out, in_=in_)

        def quantise_group(g):
            cols = slice(g * GROUP_COLS, (g + 1) * GROUP_COLS)
            nc.vector.quantize_mx(
                out=w_codes[:, cols].bitcast(FP8X4),
                scales=w_scales[:, cols],
                in_=w_grouped_all[g][:].rearrange("p s n i j -> p (s n i j)"),
            )

        def quantise_w(k):
            cols = slice(k * CHUNK_COLS, (k + 1) * CHUNK_COLS)
            nc.vector.quantize_mx(
                out=w_codes[:, cols].bitcast(FP8X4),
                scales=w_scales[:, cols],
                in_=w_grouped[k][:].rearrange("p s n i j -> p (s n i j)"),
            )

        xt = [
            [
                (psum, psum_turn)[half].tile(
                    [P, TILES_PER_HALF, P], F32, name="xt%d%d" % (u, half),
                    tag=("product", "turned")[half],
                )
                for half in range(2)
            ]
            for u in range(2)
        ]
        stats = keep.tile([P, 2, 4, 6], F32)
        multiples = keep.tile([P, len(Z_FACTORS), 2, PACK], F32)
        gain2 = multiples[:, :, 0, :]
        shift2 = multiples[:, :, 1, :]
        log_col = keep.tile([P, 1], F32)
        log_alpha = keep.tile([P, 1], F32)
        minus_alpha = keep.tile([P, 1], F32)
        nc.vector.tensor_scalar_mul(log_col[:], one_col[:], math.log(LAMBDA * ALPHA))
        nc.vector.tensor_scalar_mul(log_alpha[:], one_col[:], math.log(ALPHA))
        nc.vector.tensor_scalar_mul(minus_alpha[:], one_col[:], -ALPHA)
        for half in range(2):
            for t in range(half * TILES_PER_HALF, (half + 1) * TILES_PER_HALF):
                words = h2_sb[:, t, :].bitcast(F32).rearrange("p (q u) -> p u q", u=2)
                for u in range(2):
                    nc.tensor.transpose(xt[u][half][:, t % TILES_PER_HALF, :], words[:, u, :], ident[:])
            for u in range(2):
                pairs = xt[u][half][:].bitcast(BF16)
                for s in range(2):
                    nc.vector.bn_stats(
                        out=stats[:, u, 2 * half + s, :],
                        in_=pairs[:, 2 * s : 2 * s + 2, :].rearrange("p t w -> p (t w)"),
                    )
        affine = psum_acc.tile([P, 2, PACK], F32, name="affine", tag="sums")
        for w in range(2):
            for j in range(PACK):
                nc.tensor.matmul(
                    out=affine[:, w, j : j + 1],
                    lhsT=rows[:, w, :].rearrange("p (q j) -> p j q", j=PACK)[:, j],
                    rhs=pick[:, 0, 0, 0, 0:1], start=True, stop=True,
                )
        for row, factor in enumerate(Z_FACTORS):
            nc.scalar.mul(multiples[:, row], affine[:], factor)

        if W0_BY == "s":
            regroup_w(0, by_scalar=True)

        mean_var = keep.tile([P, PACK, 2], F32)
        for u in range(2):
            for odd in range(2):
                nc.vector.bn_aggr(
                    out=mean_var[:, 2 * u + odd, :], in_=stats[:, u, :, 3 * odd : 3 * odd + 3]
                )
        var_eps = keep.tile([P, PACK], F32)
        nc.vector.tensor_scalar_add(var_eps[:], mean_var[:, :, 1], BN_EPS)
        rstd = keep.tile([P, PACK], F32)
        if ARS:
            nc.scalar.activation(out=rstd[:], in_=var_eps[:], func=ACT.Abs_reciprocal_sqrt)
            nc.scalar.activation(out=warm[:], in_=one_col[:], func=ACT.Exp)
        else:
            nc.gpsimd.tensor_tensor(out=rstd[:], in0=var_eps[:], in1=neg_half[:], op=ALU.pow)
        if W0_BY == "g":
            regroup_w(0, by_g=True)
        if W1_BY == "g":
            regroup_w(1, by_g=True)
        if G1_BY == "g":
            regroup_group(1, "g")
        if G1_BY == "gv":
            regroup_group(1, "g", 0, 4)
        if G1_BY == "gh":
            regroup_group(1, "g", 0, G1_G)
        bias_ps = psum.tile([P, P], F32, tag="product")
        for g in range(HEAD_GROUPS):
            for i in range(SUB):
                nc.tensor.matmul(
                    out=bias_ps[:, g * SPLIT : (g + 1) * SPLIT],
                    lhsT=pick[:, g, i].rearrange("p n i -> p (n i)"),
                    rhs=bias_heads[:].rearrange("p (s i) -> p i s", i=SUB)[:, i],
                    start=(i == 0), stop=(i == SUB - 1),
                )
        mean_gain = keep.tile([P, len(Z_FACTORS), PACK], F32)
        nc.vector.tensor_tensor(
            out=mean_gain[:],
            in0=gain2,
            in1=mean_var[:, :, 0].unsqueeze(1).to_broadcast([P, len(Z_FACTORS), PACK]),
            op=ALU.mult,
        )
        if W0_BY == "v":
            regroup_w(0)
            if QW == -1:
                quantise_w(0)
        mean_scaled = keep.tile([P, len(Z_FACTORS), PACK], F32)
        nc.vector.tensor_tensor(
            out=mean_scaled[:],
            in0=mean_gain[:],
            in1=rstd[:].unsqueeze(1).to_broadcast([P, len(Z_FACTORS), PACK]),
            op=ALU.mult,
        )
        scale2 = keep.tile([P, len(Z_FACTORS), PACK], F32)
        nc.vector.tensor_tensor(
            out=scale2[:],
            in0=gain2,
            in1=rstd[:].unsqueeze(1).to_broadcast([P, len(Z_FACTORS), PACK]),
            op=ALU.mult,
        )
        offset2 = keep.tile([P, len(Z_FACTORS), PACK], F32)
        nc.vector.tensor_tensor(out=offset2[:], in0=shift2, in1=mean_scaled[:], op=ALU.subtract)
        offset_log = keep.tile([P, PACK], F32)
        nc.vector.tensor_scalar_add(offset_log[:], offset2[:, 0, :], math.log(LAMBDA * ALPHA))

        e_planes = keep.tile([P, PACK, BATCH], BF16)
        e_grouped = keep.tile([P, BATCH, PACK], BF16, align_bytes=64)
        e_codes = keep.tile([P, BATCH], U32, align_bytes=64)
        e_scales = keep.tile([P, BATCH], U8, align_bytes=64)

        e_parts = {}
        joint_parts = {}

        e_clamped = {}
        fills = {}

        def feature(half, j):
            u, odd = divmod(j, 2)
            return xt[u][half][:].bitcast(BF16).rearrange("p t (b o) -> p (t b) o", o=2)[:, :, odd]

        def clamp_by_vector(half, j):
            clamped = e_stage.tile([P, HALF], F32, tag="e_clamped")
            nc.vector.tensor_scalar(
                out=clamped[:], in0=feature(half, j), scalar1=scale2[:, 0, j : j + 1],
                scalar2=offset2[:, 2, j : j + 1], op0=ALU.mult, op1=ALU.min,
            )
            e_clamped[half, j] = (clamped, 1.0, offset_log[:, j : j + 1])

        def clamp_by_scalar(half, j):
            clamped = e_stage.tile([P, HALF], F32, tag="e_clamped")
            nc.scalar.activation(
                out=clamped[:], in_=feature(half, j), func=ACT.Relu,
                scale=scale2[:, 2, j : j + 1], bias=offset2[:, 2, j : j + 1],
            )
            e_clamped[half, j] = (clamped, -1.0, log_col[:])

        CL1 = clamp_by_vector if CL1_V else clamp_by_scalar

        def selu_parts(half, j, first=0, count=HALF, joint=False, what="both"):
            if what != "relu":
                clamped, sign, bias = e_clamped[half, j]
            if joint:
                if (half, first) not in joint_parts:
                    joint_parts[half, first] = (
                        joint_pool[count].tile([P, PACK, count], F32, name="decayed_all", tag="decayed"),
                        joint_pool[count].tile([P, PACK, count], F32, name="linear_all", tag="linear"),
                    )
                decayed = joint_parts[half, first][0][:, j, :]
                linear = joint_parts[half, first][1][:, j, :]
            else:
                decayed_tile = e_stage.tile([P, count], F32, tag="e_decayed")
                linear_tile = e_stage.tile([P, count], F32, tag="e_linear")
                decayed = decayed_tile[:]
                linear = linear_tile[:]
            if what != "relu":
                nc.scalar.activation(
                    out=decayed, in_=clamped[:, first : first + count], func=ACT.Exp, scale=sign,
                    bias=bias,
                )
            if what != "exp":
                nc.scalar.activation(
                    out=linear, in_=feature(half, j)[:, first : first + count], func=ACT.Relu,
                    scale=scale2[:, 1, j : j + 1], bias=offset2[:, 1, j : j + 1],
                )
            e_parts[half, j, first] = (decayed, linear)

        def selu_plane(half, j, first=0, count=HALF):
            rows = slice(half * HALF + first, half * HALF + first + count)
            decayed, linear = e_parts[half, j, first]
            nc.vector.scalar_tensor_tensor(
                out=e_planes[:, j, rows], in0=decayed, scalar=LAMBDA * ALPHA, in1=linear,
                op0=ALU.subtract, op1=ALU.add,
            )

        def selu_planes(half=1, first=0, count=HALF):
            rows = slice(half * HALF + first, half * HALF + first + count)
            nc.vector.scalar_tensor_tensor(
                out=e_planes[:, :, rows],
                in0=joint_parts[half, first][0][:],
                scalar=LAMBDA * ALPHA,
                in1=joint_parts[half, first][1][:],
                op0=ALU.subtract, op1=ALU.add,
            )

        def regroup_e_by_gpsimd(i):
            rows = slice(HALF + i * P, HALF + (i + 1) * P)
            nc.gpsimd.tensor_scalar(
                out=e_grouped[:, rows, :], in0=e_planes[:, :, rows].rearrange("p j b -> p b j"),
                scalar1=1.0, scalar2=0.0, op0=ALU.mult, op1=ALU.add,
            )

        def fill_e(i):
            passed = psum_turn.tile([P, 2, HALF], BF16, name="passed_e", tag="turned")
            for s in range(2):
                first = HALF + i * 256 + s * P
                nc.tensor.matmul(
                    out=passed[:, s, :], lhsT=ident[:],
                    rhs=e_planes[:, :, first : first + P].rearrange("p j b -> p b j"), start=True, stop=True,
                )
            fills["e", i] = passed

        def drain_e(i, engine):
            out = e_grouped[:, HALF + i * 256 : HALF + (i + 1) * 256, :].rearrange("p b j -> p (b j)")
            in_ = fills["e", i][:].rearrange("p s c -> p (s c)")
            if engine == "v":
                nc.vector.tensor_copy(out=out, in_=in_)
            else:
                nc.scalar.copy(out=out, in_=in_)

        def regroup_e(half, first=0, count=HALF):
            rows = slice(half * HALF + first, half * HALF + first + count)
            nc.vector.tensor_copy(
                out=e_grouped[:, rows, :].rearrange("p (c i) j -> p c j i", i=RUN),
                in_=e_planes[:, :, rows].rearrange("p j (c i) -> p c j i", i=RUN),
            )

        def quantise_e(half, first=0, count=HALF):
            rows = slice(half * HALF + first, half * HALF + first + count)
            nc.vector.quantize_mx(
                out=e_codes[:, rows].bitcast(FP8X4),
                scales=e_scales[:, rows],
                in_=e_grouped[:, rows, :].rearrange("p b j -> p (b j)"),
            )

        half1 = []
        for j in range(PACK):
            if not CL1_V:
                half1.append(lambda j=j: clamp_by_scalar(1, j))
            else:
                half1.append(lambda j=j: clamp_by_vector(1, j))
            half1.append(lambda j=j: selu_parts(1, j, 0, HALF, True, "exp"))
            half1.append(lambda j=j: selu_parts(1, j, 0, HALF, True, "relu"))
        if HEAD == 0:
            clamp_by_vector(0, 0)
            clamp_by_vector(0, 1)
            selu_parts(0, 0)
            quantise_w(0)
            clamp_by_vector(0, 2)
            selu_parts(0, 1)
            selu_plane(0, 0)
            clamp_by_vector(0, 3)
            selu_parts(0, 2)
            selu_plane(0, 1)
            selu_parts(0, 3, 0, HALF // 2)
            selu_plane(0, 2)
            selu_parts(0, 3, HALF // 2, HALF // 2)
            selu_plane(0, 3, 0, HALF // 2)
            regroup_e(0, 0, HALF // 2)
            CL1(1, 0)
            selu_plane(0, 3, HALF // 2, HALF // 2)
            quantise_e(0, 0, HALF // 2)
            regroup_e(0, HALF // 2, HALF // 2)
            selu_parts(1, 0, 0, HALF, True)
            CL1(1, 1)
            quantise_e(0, HALF // 2, HALF // 2)
        elif HEAD == 3:
            def part(j, what, first=0, count=HALF):
                if (0, 0) not in joint_parts:
                    joint_parts[0, 0] = (
                        joint_pool[HALF].tile([P, PACK, HALF], F32, name="decayed_all", tag="decayed"),
                        joint_pool[HALF].tile([P, PACK, HALF], F32, name="linear_all", tag="linear"),
                    )
                if what == "exp":
                    clamped, sign, bias = e_clamped[0, j]
                    nc.scalar.activation(
                        out=joint_parts[0, 0][0][:, j, first : first + count], in_=clamped[:, first : first + count],
                        func=ACT.Exp, scale=sign, bias=bias,
                    )
                else:
                    nc.scalar.activation(
                        out=joint_parts[0, 0][1][:, j, first : first + count], in_=feature(0, j)[:, first : first + count],
                        func=ACT.Relu, scale=scale2[:, 1, j : j + 1], bias=offset2[:, 1, j : j + 1],
                    )

            def planes(j, many, first=0, count=HALF):
                nc.vector.scalar_tensor_tensor(
                    out=e_planes[:, j : j + many, first : first + count],
                    in0=joint_parts[0, 0][0][:, j : j + many, first : first + count],
                    scalar=LAMBDA * ALPHA, in1=joint_parts[0, 0][1][:, j : j + many, first : first + count],
                    op0=ALU.subtract, op1=ALU.add,
                )

            R = HALF // 2
            part(2, "relu")
            clamp_by_vector(0, 0)
            part(3, "relu")
            clamp_by_vector(0, 1)
            part(0, "exp")
            part(1, "exp")
            if W0_BY == "v2":
                regroup_w(0)
            clamp_by_vector(0, 2)
            clamp_by_vector(0, 3)
            quantise_w(0)
            part(0, "relu")
            planes(0, 1)
            part(1, "relu")
            planes(1, 1)
            part(2, "exp")
            part(3, "exp", 0, R)
            planes(2, 1)
            planes(3, 1, 0, R)
            part(3, "exp", R, R)
            regroup_e(0, 0, R)
            planes(3, 1, R, R)
            quantise_e(0, 0, R)
            regroup_e(0, R, R)
            if W1_LATE:
                regroup_w(1)
            quantise_e(0, R, R)
            for task in half1[:PRE1]:
                task()
            if G1_PRE and G1_BY == "v":
                regroup_group(1, "v")
            if G1_BY == "gh" and G1_G < SPLIT:
                regroup_group(1, "v", G1_G, SPLIT - G1_G)
        else:
            nq = HEAD
            w = HALF // nq
            if ORDER == 1:
                for r in range(nq):
                    joint_parts[0, r * w] = (
                        joint_pool[w].tile([P, PACK, w], F32, name="decayed_all", tag="decayed"),
                        joint_pool[w].tile([P, PACK, w], F32, name="linear_all", tag="linear"),
                    )
                if FULLRELU:
                    assert False
                for (sj, vj) in ((2, 0), (3, 1)):
                    for r in range(nq if RELU2 else 1):
                        selu_parts(0, sj, r * w, w, True, "relu")
                    clamp_by_vector(0, vj)
                if QW == 1:
                    quantise_w(0)
                for j in (0, 1):
                    selu_parts(0, j, 0, w, True, "exp")
                clamp_by_vector(0, 2)
                clamp_by_vector(0, 3)
                for j in (0, 1):
                    selu_parts(0, j, 0, w, True, "relu")
                for j in (2, 3):
                    selu_parts(0, j, 0, w, True, "exp")
                if QW == 3:
                    quantise_w(0)
                selu_planes(0, 0, w)
                regroup_e(0, 0, w)
                quantise_e(0, 0, w)
                for r in range(1, nq):
                    for j in range(PACK):
                        if not (RELU2 and j >= 2):
                            selu_parts(0, j, r * w, w, True, "relu")
                        selu_parts(0, j, r * w, w, True, "exp")
                    selu_planes(0, r * w, w)
                    regroup_e(0, r * w, w)
                    quantise_e(0, r * w, w)
            for j in range(PACK if ORDER == 0 else 0):
                clamp_by_vector(0, j)
                if j == QW:
                    quantise_w(0)
            for r in range(nq if ORDER == 0 else 0):
                for j in range(PACK):
                    selu_parts(0, j, r * w, w, True)
                selu_planes(0, r * w, w)
                regroup_e(0, r * w, w)
                quantise_e(0, r * w, w)
            for task in half1[:PRE1]:
                task()
            if G1_PRE and G1_BY == "v":
                regroup_group(1, "v")
            if G1_BY == "gh" and G1_G < SPLIT:
                regroup_group(1, "v", G1_G, SPLIT - G1_G)
        if W1_BY == "v" and not W1_LATE:
            regroup_w(1)
        bias_less = keep.tile([P, COL_TILES], F32)
        if CURVE:
            nc.scalar.copy(out=bias_less[:], in_=bias_ps[:, 0:COL_TILES])
            bias_drop = keep.tile([P, COL_TILES], F32)
            nc.scalar.activation(
                out=bias_drop[:], in_=bias_ps[:, 0:COL_TILES], func=ACT.Identity, bias=minus_alpha[:], scale=-1.0
            )
        else:
            nc.scalar.activation(
                out=bias_less[:], in_=bias_ps[:, 0:COL_TILES], func=ACT.Identity, bias=minus_alpha[:], scale=1.0
            )
        bias_log = keep.tile([P, COL_TILES], F32)
        nc.scalar.activation(
            out=bias_log[:], in_=bias_ps[:, 0:COL_TILES], func=ACT.Identity, bias=log_alpha[:], scale=1.0
        )
        bias_minus = keep.tile([P, COL_TILES], F32)
        nc.scalar.mul(bias_minus[:], bias_ps[:, 0:COL_TILES], -1.0)

        out_rows = out.rearrange("(p t) h g e -> p t (h g e)", t=BATCH_TILES)
        rounds = [(half, c) for half in range(2) for c in range(COL_TILES)]
        p_tiles = {}
        growths = {}
        curves = {}
        lows = {}
        d_tiles = {}
        sizes = {}
        sums = {}
        inverses = {}
        totals = {}
        divisors = {}
        d_banks = {}
        results = {}

        def multiply(n):
            half, c = rounds[n]
            rows = slice(half * HALF, (half + 1) * HALF)
            cols = slice(c * P, (c + 1) * P)
            p_t = psum.tile([P, HALF], F32, tag="product")
            nc.tensor.matmul_mx(
                out=p_t[:],
                lhsT=w_codes[:, cols].bitcast(FP8X4), lhsT_scale=w_scales[:, cols],
                rhs=e_codes[:, rows].bitcast(FP8X4), rhs_scale=e_scales[:, rows],
                start=True, stop=True,
            )
            p_tiles[n] = p_t

        def grow(n):
            c = rounds[n][1]
            if n % PAIR == 0:
                growths[n // PAIR] = grow_pool.tile([P, PAIR, HALF], F32, name="grown", tag="grown")
            nc.scalar.activation(
                out=growths[n // PAIR][:, n % PAIR, :], in_=p_tiles[n][:], func=ACT.Exp, bias=bias_log[:, c : c + 1], scale=1.0
            )

        def clip(m):
            clipped = grow_pool.tile([P, PAIR, HALF], F32, tag="clipped")
            if CURVE:
                c = rounds[m][1]
                nc.gpsimd.tensor_scalar(
                    out=clipped[:].rearrange("p r b -> p (r b)"),
                    in0=growths[m][:].rearrange("p r b -> p (r b)"), scalar1=1.0, scalar2=bias_drop[:, c : c + 1],
                    op0=ALU.mult, op1=ALU.add,
                )
            else:
                nc.gpsimd.tensor_scalar(
                    out=clipped[:].rearrange("p r b -> p (r b)"),
                    in0=growths[m][:].rearrange("p r b -> p (r b)"), scalar1=ALPHA, scalar2=0.0,
                    op0=ALU.min, op1=ALU.max,
                )
            curves[m] = clipped

        def combine(n):
            c = rounds[n][1]
            low = work.tile([P, HALF], F32, tag="low")
            nc.vector.scalar_tensor_tensor(
                out=low[:], in0=p_tiles[n][:], scalar=bias_minus[:, c : c + 1], in1=curves[n // PAIR][:, n % PAIR, :],
                op0=ALU.max, op1=ALU.min if CURVE else ALU.add,
            )
            lows[n] = low

        def magnitude(n):
            c = rounds[n][1]
            size = work.tile([P, HALF], F32, tag="size")
            nc.scalar.activation(
                out=size[:], in_=lows[n][:], func=ACT.Abs, bias=bias_less[:, c : c + 1], scale=1.0
            )
            sizes[n] = size

        def lift(n):
            c = rounds[n][1]
            d_t = held.tile([P, HALF], F32, tag="d_t")
            if n >= LIFT_FROM and n % LIFT_PERIOD in SCALAR_LIFTS:
                nc.scalar.activation(
                    out=d_t[:], in_=lows[n][:], func=ACT.Identity, bias=bias_less[:, c : c + 1],
                    scale=1.0,
                )
            else:
                nc.gpsimd.tensor_scalar(
                    out=d_t[:], in0=lows[n][:], scalar1=1.0,
                    scalar2=bias_less[:, c : c + 1], op0=ALU.mult, op1=ALU.add,
                )
            d_tiles[n] = d_t

        def fold(n):
            q, s = divmod(n, SPLIT)
            if s == 0:
                sums[q] = psum_acc.tile([P, TILES_PER_HALF, P], F32, name="sums%d" % q, tag="sums")
            for t in range(TILES_PER_HALF):
                nc.tensor.matmul(
                    out=sums[q][:, t, :], lhsT=sizes[n][:, t * P : (t + 1) * P], rhs=ident[:],
                    is_transpose=True,
                    start=(s == 0 and t == 0), stop=(s == SPLIT - 1 and t == TILES_PER_HALF - 1),
                )

        def norm(q):
            total = small.tile([P, TILES_PER_HALF * GROUP_HEADS], F32, tag="total")
            nc.vector.tensor_reduce(
                out=total[:], in_=sums[q][:].rearrange("p t (n i) -> p (t n) i", i=SUB),
                axis=mybir.AxisListType.X, op=ALU.add,
            )
            totals[q] = total

        def floor_sums(q):
            total = totals[q]
            divisor = small.tile([P, TILES_PER_HALF * GROUP_HEADS], F32, tag="divisor")
            if FLOOR == "g":
                nc.gpsimd.tensor_scalar(
                    out=divisor[:], in0=total[:], scalar1=3.0e38, scalar2=L1_FLOOR, op0=ALU.min, op1=ALU.max
                )
                divisors[q] = divisor
                return
            unused = small.tile([P, 1], F32, tag="unused")
            nc.vector.tensor_scalar(
                out=divisor[:], in0=total[:], scalar1=L1_FLOOR, scalar2=None, op0=ALU.max, op1=ALU.add,
                accum_out=unused[:],
            )
            divisors[q] = divisor

        def invert(q):
            divisor = divisors[q]
            inverse = small.tile([P, TILES_PER_HALF, GROUP_HEADS], F32, tag="inverse")
            nc.vector.reciprocal(out=inverse[:].rearrange("p t n -> p (t n)"), in_=divisor[:])
            inverses[q] = inverse

        def turn(x):
            q, u = divmod(x, SPLIT)
            t, a = divmod(u, CHUNKS_PER_GROUP)
            if x >= TAILX and (x % 2 == 1 or x >= TAILX2):
                d_ps = psum.tile([P, CHUNK_TILES, P], F32, tag="product")
            else:
                d_ps = psum_turn.tile([P, CHUNK_TILES, P], F32, tag="turned")
            for i in range(CHUNK_TILES):
                n = q * SPLIT + a * CHUNK_TILES + i
                nc.tensor.transpose(d_ps[:, i, :], d_tiles[n][:, t * P : (t + 1) * P], ident[:])
            d_banks[x] = d_ps

        def scale_and_store(x):
            q, u = divmod(x, SPLIT)
            t, a = divmod(u, CHUNKS_PER_GROUP)
            half, g = divmod(q, HEAD_GROUPS)
            if a == 0:
                results[q, t] = out_stage.tile([P, GROUP_COLS], F32, name="result", tag="result")
            result = results[q, t]
            turned = d_banks[x]
            engine = nc.vector
            if x in G_UNITS:
                turned = out_stage.tile([P, CHUNK_TILES, P], F32, name="lifted", tag="lifted")
                nc.scalar.copy(out=turned[:], in_=d_banks[x][:])
                engine = nc.gpsimd
            engine.tensor_tensor(
                out=result[:].rearrange("p (n s i) -> p s n i", s=SPLIT, i=SUB)[
                    :, a * CHUNK_TILES : (a + 1) * CHUNK_TILES
                ],
                in0=turned[:].rearrange("p s (n i) -> p s n i", i=SUB),
                in1=inverses[q][:, t, :]
                .unsqueeze(1)
                .unsqueeze(3)
                .to_broadcast([P, CHUNK_TILES, GROUP_HEADS, SUB]),
                op=ALU.mult,
            )
            if a == CHUNKS_PER_GROUP - 1:
                nc.sync.dma_start(
                    out=out_rows[
                        :, half * TILES_PER_HALF + t, g * GROUP_COLS : (g + 1) * GROUP_COLS
                    ],
                    in_=result[:],
                )

        def at(stage, n):
            if 0 <= n < len(rounds):
                stage(n)

        def later(stage, *what):
            return lambda: stage(*what)

        early = {}
        woven = {}

        def weave(step, engine, stage, *what):
            woven.setdefault(step, ([], []))[engine].append(later(stage, *what))

        for i, task in enumerate(half1[PRE1:]):
            woven.setdefault(E1_FIRST + i // RATE1, ([], []))[0 if i % 3 or not CL1_V else 1].append(task)
        weave(GROUPED_STEP, 1, selu_planes)
        if E_BY == "v":
            weave(GROUPED_STEP + 1, 1, regroup_e, 1)
        elif E_BY == "pe":
            for i in range(2):
                early.setdefault(GROUPED_STEP + 2 + i, []).append(later(fill_e, i))
                weave(GROUPED_STEP + 2 + i + ELAG, 0 if FBY == "s" else 1, drain_e, i, FBY)
        weave(QE_STEP, 1, quantise_e, 1)
        weave(Q1_STEP, 1, quantise_w, 1)
        if G1_BY == "v" and not G1_PRE:
            weave(G1_STEP, 1, regroup_group, 1, "v")
        if G1_BY == "gv":
            weave(G1_STEP, 1, regroup_group, 1, "v", 4, 4)
        weave(QG1_STEP, 1, quantise_group, 1)
        tensor_woven = early
        g_woven = {}
        if G1_BY == "gl":
            for s in range(SPLIT):
                g_woven.setdefault(G1_STEP + s // GRATE, []).append(later(regroup_group, 1, "g", s, 1))
        if G2_BY == "gl":
            for s in range(SPLIT):
                g_woven.setdefault(G2_STEP + s // GRATE, []).append(later(regroup_group, 2, "g", s, 1))
        if G2_BY == "sl":
            for s in range(SPLIT):
                weave(G2_STEP + s // GRATE, 0, regroup_group, 2, "s", s, 1)
        if G1_BY == "sl":
            for s in range(SPLIT):
                weave(G1_STEP + s // GRATE, 0, regroup_group, 1, "s", s, 1)
        if E_BY == "g":
            for i in range(4):
                g_woven.setdefault(GROUPED_STEP + 1 + i // 2, []).append(later(regroup_e_by_gpsimd, i))
        if G2_BY == "v":
            weave(G2_STEP, 1, regroup_group, 2, "v")
        elif G2_BY == "pe":
            for i in range(4):
                tensor_woven.setdefault(G2_STEP - 5 + FSTEP * i, []).append(later(fill, 2, i))
                weave(G2_STEP - 5 + FSTEP * i + FLAG, 0 if FBY == "s" else 1, drain_fill, 2, i, FBY)
        else:
            for s in range(SPLIT):
                weave(G2_STEP + s // 2 - 4, 0, regroup_group, 2, "s", s, 1)
        weave(QG2_STEP if G2_BY != "pe" else G2_STEP - 4 + 3 * FSTEP + FLAG, 1, quantise_group, 2)

        for j in range(-1, len(rounds) + TURN + 2):
            at(multiply, j + 1)
            for task in tensor_woven.get(j, []):
                task()
            if NORM == 3 and j >= TURN and (j - TURN) % SPLIT == 1 and (j - TURN) // SPLIT < len(rounds) // SPLIT:
                floor_sums((j - TURN) // SPLIT)
            if j >= FOLDFIRST:
                at(fold, j - FOLD)
                at(turn, j - TURN)
            else:
                at(turn, j - TURN)
                at(fold, j - FOLD)
            at(grow, j)
            at(lift, j - LIFT)
            if j % PAIR == PAIR - 1 and 0 <= j < len(rounds):
                clip(j // PAIR)
            for task in g_woven.get(j, []):
                task()
            at(magnitude, j - ABS)
            for task in woven.get(j, ([], []))[0]:
                task()
            q, place = divmod(j - TURN, SPLIT)
            sets = len(rounds) // SPLIT
            if NORM == 0:
                at(scale_and_store, j - TURN - 1)
                if place == 0 and 0 <= q < sets:
                    norm(q)
                    floor_sums(q)
                    invert(q)
                at(combine, j - COMB)
            elif place == 0 and 0 <= q < sets:
                at(scale_and_store, j - TURN - 1)
                norm(q)
                at(combine, j - COMB)
                if NORM != 3:
                    floor_sums(q)
                if NORM == 2:
                    invert(q)
            elif place == 1 and 0 <= q < sets:
                if NORM in (1, 3):
                    at(combine, j - COMB)
                    invert(q)
                    at(scale_and_store, j - TURN - 1)
                else:
                    at(combine, j - COMB)
                    at(scale_and_store, j - TURN - 1)
            else:
                at(scale_and_store, j - TURN - 1)
                at(combine, j - COMB)
            for task in woven.get(j, ([], []))[1]:
                task()
